import numpy as np
import ml_dtypes


def mxq(x, axis, fmt="e4m3"):
    dtype, down = {"e4m3": (ml_dtypes.float8_e4m3fn, 7), "e5m2": (ml_dtypes.float8_e5m2, 14)}[fmt]
    v = np.moveaxis(np.asarray(x, np.float32).astype(ml_dtypes.bfloat16).astype(np.float64), axis, -1)
    blocks = v.reshape(v.shape[:-1] + (-1, 32))
    amax = np.abs(blocks).max(-1, keepdims=True)
    byte = np.maximum(np.where(amax > 0, np.frexp(amax)[1] - 1 + 127, 0) - down, 1)
    scale = np.exp2(byte - 127.0)
    codes = (blocks / scale).astype(np.float32).astype(dtype).astype(np.float64)
    return np.moveaxis((codes * scale).reshape(v.shape), -1, axis)


WIDE = False


def mx_kscale(k):
    if not WIDE:
        return np.ones(k)
    levels = np.array([10, -10, 5, -5, 0])
    a = np.random.permutation(np.resize(levels, k // 512 * 4)).reshape(k // 512, 4)
    idx = np.arange(k)
    return np.exp2(a[idx // 512, idx % 128 // 32])


BF16 = ml_dtypes.bfloat16


def bf(x):
    return np.asarray(x, np.float32).astype(BF16)


def f64(x):
    return np.asarray(x).astype(np.float64)


B, C, T, H = 4, 256, 2048, 1024
EPS_LN = 1e-5
EPS_STD = 1e-5


def ln_dim1(z, g, b):
    mu = z.mean(axis=1, keepdims=True)
    var = ((z - mu) ** 2).mean(axis=1, keepdims=True)
    return (z - mu) / np.sqrt(var + EPS_LN) * g[None, :, None] + b[None, :, None]


def stats(x, m):
    mean = (m * x).sum(axis=2)
    std = np.sqrt(np.maximum((m * x * x).sum(axis=2) - mean ** 2, EPS_STD))
    return mean, std


def setup_inputs():
    s = mx_kscale(H)
    drop = np.random.randint(B, size=T)
    mask = (np.arange(B)[:, None, None] != drop[None, None, :]) * 1.0
    off = 0.5 * np.random.standard_normal((B, C, 1))
    gain = 0.5 + np.random.random((B, C, 1))
    pad = np.random.standard_normal((B, C, 1)) * (1.0 - mask)
    x = off + gain * np.random.standard_normal((B, C, T)) + pad
    return {"h": bf(np.tanh(np.random.standard_normal((B, H, T))) * s[None, :, None]),
            "x": bf(x),
            "mask": bf(mask),
            "w2": bf(np.random.standard_normal((C, H)) * 3.0 / np.sqrt(H) / s[None, :]),
            "b2": bf(0.1 * np.random.standard_normal(C)),
            "g2": bf(1.0 + 0.1 * np.random.standard_normal(2 * C)),
            "be2": bf(0.1 * np.random.standard_normal(2 * C))}


def reference(h, x, mask, w2, b2, g2, be2):
    x, mask = f64(x), f64(mask)
    alpha = (mxq(f64(w2), 1, "e4m3") @ mxq(f64(h), 1, "e4m3")) + f64(b2)[None, :, None]
    alpha = np.where(mask == 0, -np.inf, alpha)
    e = np.exp(alpha - alpha.max(axis=2, keepdims=True))
    alpha = e / e.sum(axis=2, keepdims=True)
    mean, std = stats(x, alpha)
    out = np.concatenate([mean, std], axis=1)[:, :, None]
    return ln_dim1(out, f64(g2), f64(be2))

@@ -1,0 +1,309 @@
+import concourse.mybir as mybir
+from concourse.masks import make_identity
+
+F32 = mybir.dt.float32
+BF16 = mybir.dt.bfloat16
+U32 = mybir.dt.uint32
+U8 = mybir.dt.uint8
+FP8X4 = mybir.dt.float8_e4m3fn_x4
+ALU = mybir.AluOpType
+ACT = mybir.ActivationFunctionType
+AXIS = mybir.AxisListType
+
+B, C, T, H = 4, 256, 2048, 1024
+EPS_LN = 1e-5
+EPS_STD = 1e-5
+FLOPS = 2 * B * C * H * T
+
+P = 128
+PACK = 4
+K_PASS = P * PACK
+PASSES = H // K_PASS
+T_TILE = 512
+T_TILES = T // T_TILE
+C_TILES = C // P
+TILES = B * T_TILES
+RUN = 4
+MASKED = -1e30
+
+LOAD_LEAD = 2
+REGROUP_LEAD = 2
+
+
+def tile_attentivestatspool_pb_t_kernel(tc, h, x, mask, w2, b2, g2, be2, out):
+    nc = tc.nc
+    with tc.tile_pool(name="const", bufs=1) as const, tc.tile_pool(
+        name="raw", bufs=PASSES * (LOAD_LEAD + 2)
+    ) as raw_pool, tc.tile_pool(
+        name="grouped", bufs=PASSES * (REGROUP_LEAD + 2)
+    ) as grouped_pool, tc.tile_pool(name="codes", bufs=3 * PASSES) as codes_pool, tc.tile_pool(
+        name="scores", bufs=2
+    ) as score_pool, tc.tile_pool(name="prod", bufs=2) as prod_pool, tc.psum_pool(
+        name="banks", bufs=6
+    ) as bank_pool, tc.psum_pool(name="misc", bufs=2) as misc_pool, tc.manual_schedule():
+        ident_bf = const.tile([P, P], BF16)
+        make_identity(nc, ident_bf[:])
+        ident_f32 = const.tile([P, P], F32)
+        make_identity(nc, ident_f32[:])
+        averager = const.tile([P, P], F32)
+        nc.vector.memset(averager[:], 1.0 / (2 * C))
+        y_pad = const.tile([P, P], F32)
+        nc.vector.memset(y_pad[:], 0.0)
+        gb_rows = const.tile([P, P], BF16)
+        nc.vector.memset(gb_rows[:], 0.0)
+        warm = const.tile([P, 1], F32)
+        nc.vector.memset(warm[:], 0.0)
+        nc.scalar.activation(out=warm[:], in_=warm[:], func=ACT.Exp)
+
+        w2_rows = const.tile([P, C_TILES, H], BF16)
+        nc.sync.dma_start(out=w2_rows[:], in_=w2.rearrange("(ct c) k -> c ct k", c=P))
+        nc.gpsimd.dma_start(out=gb_rows[0:4, :], in_=g2.rearrange("(r c) -> r c", c=P))
+        nc.gpsimd.dma_start(out=gb_rows[4:8, :], in_=be2.rearrange("(r c) -> r c", c=P))
+        w2_sorted = const.tile([P, C_TILES * PASSES, PACK, P], BF16)
+        nc.vector.tensor_copy(
+            out=w2_sorted[:],
+            in_=w2_rows[:].rearrange("c ct (g p j) -> c (ct g) j p", p=P, j=PACK),
+        )
+        w2_grouped = const.tile([P, PASSES, C_TILES, P, PACK], BF16, align_bytes=64)
+        for g in range(PASSES):
+            w2_t = misc_pool.tile([P, C_TILES, PACK, P], BF16, tag="misc")
+            for ct in range(C_TILES):
+                for j in range(PACK):
+                    nc.tensor.transpose(
+                        w2_t[:, ct, j, :], w2_sorted[:, ct * PASSES + g, j, :], ident_bf[:]
+                    )
+            nc.vector.tensor_copy(
+                out=w2_grouped[:, g], in_=w2_t[:].rearrange("p ct j c -> p ct c j")
+            )
+        w2_codes = const.tile([P, PASSES * C], U32, align_bytes=64)
+        w2_scales = const.tile([P, PASSES * C], U8, align_bytes=64)
+        nc.vector.quantize_mx(
+            out=w2_codes[:].bitcast(FP8X4),
+            scales=w2_scales[:],
+            in_=w2_grouped[:].rearrange("p g ct c j -> p (g ct c j)"),
+        )
+
+        gb_t = misc_pool.tile([P, P], BF16, tag="misc")
+        nc.tensor.transpose(gb_t[:], gb_rows[:], ident_bf[:])
+        gb = const.tile([P, 8], F32)
+        nc.vector.tensor_copy(out=gb[:], in_=gb_t[:, 0:8])
+
+        neg_max = const.tile([P, B * C_TILES], F32)
+        sum_e = const.tile([P, B * C_TILES], F32)
+        sum_ex = const.tile([P, B * C_TILES], F32)
+        sum_exx = const.tile([P, B * C_TILES], F32)
+
+        penalty = const.tile([P, B, T], BF16)
+        x_rows = const.tile([P, B, C_TILES, T], BF16)
+        raw = {}
+        grouped = {}
+        codes = {}
+        scales = {}
+        banks = {}
+        scores = {}
+
+        def load_tile(i):
+            if i < 0 or i >= TILES:
+                return
+            b, tt = divmod(i, T_TILES)
+            frames = slice(tt * T_TILE, (tt + 1) * T_TILE)
+            for g in range(PASSES):
+                raw[i, g] = raw_pool.tile([P, PACK, T_TILE], BF16, name="raw", tag="raw")
+                nc.sync.dma_start(
+                    out=raw[i, g][:],
+                    in_=h[b, g * K_PASS : (g + 1) * K_PASS, frames].rearrange(
+                        "(p j) t -> p j t", j=PACK
+                    ),
+                )
+            if tt == 0:
+                nc.sync.dma_start(out=penalty[:, b, :], in_=mask[b, 0, :].partition_broadcast(P))
+            if tt == T_TILES - 1:
+                nc.sync.dma_start(
+                    out=x_rows[:, b], in_=x[b].rearrange("(ct c) t -> c ct t", c=P)
+                )
+
+        def regroup_tile(i):
+            if i < 0 or i >= TILES:
+                return
+            for g in range(PASSES):
+                grouped[i, g] = grouped_pool.tile(
+                    [P, T_TILE, PACK], BF16, name="grouped", tag="grouped", align_bytes=64
+                )
+                nc.scalar.copy(
+                    out=grouped[i, g][:].rearrange("p (c r) j -> p c j r", r=RUN),
+                    in_=raw[i, g][:].rearrange("p j (c r) -> p c j r", r=RUN),
+                )
+
+        def quantise_and_multiply(i):
+            if i < 0 or i >= TILES:
+                return
+            b, tt = divmod(i, T_TILES)
+            if tt == 0:
+                nc.vector.tensor_scalar(
+                    out=penalty[:, b, :],
+                    in0=penalty[:, b, :],
+                    scalar1=0.0,
+                    scalar2=MASKED,
+                    op0=ALU.is_equal,
+                    op1=ALU.mult,
+                )
+            for g in range(PASSES):
+                codes[i, g] = codes_pool.tile(
+                    [P, T_TILE], U32, name="codes", tag="codes", align_bytes=64
+                )
+                scales[i, g] = codes_pool.tile(
+                    [P, T_TILE], U8, name="scales", tag="scales", align_bytes=64
+                )
+                nc.vector.quantize_mx(
+                    out=codes[i, g][:].bitcast(FP8X4),
+                    scales=scales[i, g][:],
+                    in_=grouped[i, g][:].rearrange("p t j -> p (t j)"),
+                )
+            for ct in range(C_TILES):
+                banks[i, ct] = bank_pool.tile([P, T_TILE], F32, name="bank", tag="bank")
+                for g in range(PASSES):
+                    channels = slice(g * C + ct * P, g * C + (ct + 1) * P)
+                    nc.tensor.matmul_mx(
+                        out=banks[i, ct][:],
+                        lhsT=w2_codes[:, channels].bitcast(FP8X4),
+                        lhsT_scale=w2_scales[:, channels],
+                        rhs=codes[i, g][:].bitcast(FP8X4),
+                        rhs_scale=scales[i, g][:],
+                        start=(g == 0),
+                        stop=(g == PASSES - 1),
+                    )
+
+        def mask_scores(i):
+            if i < 0 or i >= TILES:
+                return
+            b, tt = divmod(i, T_TILES)
+            frames = slice(tt * T_TILE, (tt + 1) * T_TILE)
+            if tt == 0:
+                scores[b] = score_pool.tile([P, C_TILES, T], F32, name="scores", tag="scores")
+            for ct in range(C_TILES):
+                nc.vector.tensor_tensor(
+                    out=scores[b][:, ct, frames],
+                    in0=banks[i, ct][:],
+                    in1=penalty[:, b, frames],
+                    op=ALU.add,
+                )
+
+        def pool_step(k):
+            if k < 0 or k >= B * 2 * C_TILES:
+                return
+            b, step = divmod(k, 2 * C_TILES)
+            ct = step % C_TILES
+            col = slice(b * C_TILES + ct, b * C_TILES + ct + 1)
+            row = scores[b][:, ct, :]
+            if step < C_TILES:
+                nc.vector.tensor_reduce(
+                    out=neg_max[:, col], in_=row, axis=AXIS.X, op=ALU.max, negate=True
+                )
+                nc.scalar.activation(
+                    out=row, in_=row, func=ACT.Exp, bias=neg_max[:, col], accum_out=sum_e[:, col]
+                )
+            else:
+                prod = prod_pool.tile([P, T], F32, name="prod", tag="prod")
+                nc.vector.scalar_tensor_tensor(
+                    out=prod[:],
+                    in0=row,
+                    scalar=1.0,
+                    in1=x_rows[:, b, ct, :],
+                    op0=ALU.mult,
+                    op1=ALU.mult,
+                    accum_out=sum_ex[:, col],
+                )
+                nc.vector.scalar_tensor_tensor(
+                    out=prod[:],
+                    in0=prod[:],
+                    scalar=1.0,
+                    in1=x_rows[:, b, ct, :],
+                    op0=ALU.mult,
+                    op1=ALU.mult,
+                    accum_out=sum_exx[:, col],
+                )
+
+        assert 2 * C_TILES == T_TILES
+        for n in range(-REGROUP_LEAD - LOAD_LEAD, TILES + T_TILES):
+            load_tile(n + REGROUP_LEAD + LOAD_LEAD)
+            regroup_tile(n + REGROUP_LEAD)
+            quantise_and_multiply(n)
+            mask_scores(n - 1)
+            pool_step(n - T_TILES)
+
+        nc.scalar.activation(out=warm[:], in_=sum_e[:, B * C_TILES - 1 :], func=ACT.Sqrt)
+
+        def by_utterance(stat):
+            return stat[:].rearrange("p (b ct) -> p b ct", ct=C_TILES)
+
+        v = const.tile([P, 2, B, C_TILES], F32)
+        full = [P, 2, B, C_TILES]
+        recip = const.tile([P, B * C_TILES], F32)
+        nc.vector.reciprocal(out=recip[:], in_=sum_e[:])
+        nc.vector.tensor_tensor(
+            out=v[:, 0], in0=by_utterance(sum_ex), in1=by_utterance(recip), op=ALU.mult
+        )
+        second = const.tile([P, B, C_TILES], F32)
+        nc.vector.tensor_tensor(
+            out=second[:], in0=by_utterance(sum_exx), in1=by_utterance(recip), op=ALU.mult
+        )
+        mean_sq = const.tile([P, B, C_TILES], F32)
+        nc.vector.tensor_tensor(out=mean_sq[:], in0=v[:, 0], in1=v[:, 0], op=ALU.mult)
+        variance = const.tile([P, B, C_TILES], F32)
+        nc.vector.tensor_tensor(out=variance[:], in0=second[:], in1=mean_sq[:], op=ALU.subtract)
+        nc.vector.tensor_scalar_max(out=variance[:], in0=variance[:], scalar1=EPS_STD)
+        nc.scalar.activation(out=v[:, 1], in_=variance[:], func=ACT.Sqrt)
+
+        def mean_over_entries(values, name):
+            share = misc_pool.tile(full, F32, name=name + "_share", tag="misc")
+            nc.tensor.matmul(
+                out=share[:].rearrange("p s b ct -> p (s b ct)"),
+                lhsT=averager[:],
+                rhs=values[:].rearrange("p s b ct -> p (s b ct)"),
+                start=True,
+                stop=True,
+            )
+            result = const.tile([P, B], F32, name=name)
+            nc.vector.tensor_reduce(
+                out=result[:],
+                in_=share[:].rearrange("p s b ct -> p b s ct"),
+                axis=AXIS.XY,
+                op=ALU.add,
+            )
+            return result
+
+        def per_utterance(stat):
+            return stat[:].unsqueeze(1).unsqueeze(3).to_broadcast(full)
+
+        def per_entry(columns):
+            return columns.rearrange("p (s ct) -> p s ct", s=2).unsqueeze(2).to_broadcast(full)
+
+        mu = mean_over_entries(v, "mu")
+        centred = const.tile(full, F32)
+        nc.vector.tensor_tensor(out=centred[:], in0=v[:], in1=per_utterance(mu), op=ALU.subtract)
+        squared = const.tile(full, F32)
+        nc.vector.tensor_tensor(out=squared[:], in0=centred[:], in1=centred[:], op=ALU.mult)
+        var_ln = mean_over_entries(squared, "var_ln")
+        nc.vector.tensor_scalar_add(out=var_ln[:], in0=var_ln[:], scalar1=EPS_LN)
+        std_ln = const.tile([P, B], F32)
+        nc.scalar.activation(out=std_ln[:], in_=var_ln[:], func=ACT.Sqrt)
+        rstd_ln = const.tile([P, B], F32)
+        nc.vector.reciprocal(out=rstd_ln[:], in_=std_ln[:])
+        nc.vector.tensor_tensor(
+            out=centred[:], in0=centred[:], in1=per_utterance(rstd_ln), op=ALU.mult
+        )
+        nc.vector.tensor_tensor(
+            out=centred[:], in0=centred[:], in1=per_entry(gb[:, 0:4]), op=ALU.mult
+        )
+        rows = 2 * B * C_TILES
+        nc.vector.tensor_tensor(
+            out=y_pad[:, 0:rows].rearrange("p (b s ct) -> p s b ct", s=2, ct=C_TILES),
+            in0=centred[:],
+            in1=per_entry(gb[:, 4:8]),
+            op=ALU.add,
+        )
+        y_t = misc_pool.tile([P, P], F32, tag="misc")
+        nc.tensor.transpose(y_t[:], y_pad[:], ident_f32[:])
+        y_rows = const.tile([rows, P], F32)
+        nc.scalar.copy(out=y_rows[:], in_=y_t[0:rows, :])
+        nc.sync.dma_start(out=out.rearrange("b (e c) o -> (b e) (c o)", c=P), in_=y_rows[:])

@@ -28,19 +28,20 @@ MASKED = -1e30
 
 LOAD_LEAD = 2
 REGROUP_LEAD = 2
+HELPED_TILES = 4
 
 
 def tile_attentivestatspool_pb_t_kernel(tc, h, x, mask, w2, b2, g2, be2, out):
     nc = tc.nc
     with tc.tile_pool(name="const", bufs=1) as const, tc.tile_pool(
-        name="raw", bufs=PASSES * (LOAD_LEAD + 2)
-    ) as raw_pool, tc.tile_pool(
-        name="grouped", bufs=PASSES * (REGROUP_LEAD + 2)
-    ) as grouped_pool, tc.tile_pool(name="codes", bufs=3 * PASSES) as codes_pool, tc.tile_pool(
-        name="scores", bufs=2
-    ) as score_pool, tc.tile_pool(name="prod", bufs=2) as prod_pool, tc.psum_pool(
-        name="banks", bufs=6
-    ) as bank_pool, tc.psum_pool(name="misc", bufs=2) as misc_pool, tc.manual_schedule():
+        name="raw", bufs=LOAD_LEAD + 2
+    ) as raw_pool, tc.tile_pool(name="grouped", bufs=REGROUP_LEAD + 2) as grouped_pool, tc.tile_pool(
+        name="codes", bufs=3
+    ) as codes_pool, tc.tile_pool(name="scores", bufs=2) as score_pool, tc.tile_pool(
+        name="prod", bufs=2
+    ) as prod_pool, tc.psum_pool(name="banks", bufs=6) as bank_pool, tc.psum_pool(
+        name="misc", bufs=2
+    ) as misc_pool, tc.manual_schedule():
         ident_bf = const.tile([P, P], BF16)
         make_identity(nc, ident_bf[:])
         ident_f32 = const.tile([P, P], F32)
@@ -53,12 +54,12 @@ def tile_attentivestatspool_pb_t_kernel(tc, h, x, mask, w2, b2, g2, be2, out):
         nc.vector.memset(gb_rows[:], 0.0)
         warm = const.tile([P, 1], F32)
         nc.vector.memset(warm[:], 0.0)
-        nc.scalar.activation(out=warm[:], in_=warm[:], func=ACT.Exp)
 
         w2_rows = const.tile([P, C_TILES, H], BF16)
-        nc.sync.dma_start(out=w2_rows[:], in_=w2.rearrange("(ct c) k -> c ct k", c=P))
-        nc.gpsimd.dma_start(out=gb_rows[0:4, :], in_=g2.rearrange("(r c) -> r c", c=P))
-        nc.gpsimd.dma_start(out=gb_rows[4:8, :], in_=be2.rearrange("(r c) -> r c", c=P))
+        nc.scalar.dma_start(out=w2_rows[:], in_=w2.rearrange("(ct c) k -> c ct k", c=P))
+        nc.scalar.dma_start(out=gb_rows[0:4, :], in_=g2.rearrange("(r c) -> r c", c=P))
+        nc.scalar.dma_start(out=gb_rows[4:8, :], in_=be2.rearrange("(r c) -> r c", c=P))
+        nc.scalar.activation(out=warm[:], in_=warm[:], func=ACT.Exp)
         w2_sorted = const.tile([P, C_TILES * PASSES, PACK, P], BF16)
         nc.vector.tensor_copy(
             out=w2_sorted[:],
@@ -75,11 +76,11 @@ def tile_attentivestatspool_pb_t_kernel(tc, h, x, mask, w2, b2, g2, be2, out):
             nc.vector.tensor_copy(
                 out=w2_grouped[:, g], in_=w2_t[:].rearrange("p ct j c -> p ct c j")
             )
-        w2_codes = const.tile([P, PASSES * C], U32, align_bytes=64)
-        w2_scales = const.tile([P, PASSES * C], U8, align_bytes=64)
+        w2_codes = const.tile([P, PASSES, C], U32, align_bytes=64)
+        w2_scales = const.tile([P, PASSES, C], U8, align_bytes=64)
         nc.vector.quantize_mx(
-            out=w2_codes[:].bitcast(FP8X4),
-            scales=w2_scales[:],
+            out=w2_codes[:].rearrange("p g c -> p (g c)").bitcast(FP8X4),
+            scales=w2_scales[:].rearrange("p g c -> p (g c)"),
             in_=w2_grouped[:].rearrange("p g ct c j -> p (g ct c j)"),
         )
 
@@ -88,10 +89,9 @@ def tile_attentivestatspool_pb_t_kernel(tc, h, x, mask, w2, b2, g2, be2, out):
         gb = const.tile([P, 8], F32)
         nc.vector.tensor_copy(out=gb[:], in_=gb_t[:, 0:8])
 
-        neg_max = const.tile([P, B * C_TILES], F32)
-        sum_e = const.tile([P, B * C_TILES], F32)
-        sum_ex = const.tile([P, B * C_TILES], F32)
-        sum_exx = const.tile([P, B * C_TILES], F32)
+        neg_max = const.tile([P, B, C_TILES], F32)
+        sum_e = const.tile([P, B, C_TILES], F32)
+        sums = const.tile([P, 2, B, C_TILES], F32)
 
         penalty = const.tile([P, B, T], BF16)
         x_rows = const.tile([P, B, C_TILES, T], BF16)
@@ -101,38 +101,49 @@ def tile_attentivestatspool_pb_t_kernel(tc, h, x, mask, w2, b2, g2, be2, out):
         scales = {}
         banks = {}
         scores = {}
+        prod = {}
 
         def load_tile(i):
-            if i < 0 or i >= TILES:
+            if i < 0:
                 return
             b, tt = divmod(i, T_TILES)
-            frames = slice(tt * T_TILE, (tt + 1) * T_TILE)
-            for g in range(PASSES):
-                raw[i, g] = raw_pool.tile([P, PACK, T_TILE], BF16, name="raw", tag="raw")
-                nc.sync.dma_start(
-                    out=raw[i, g][:],
-                    in_=h[b, g * K_PASS : (g + 1) * K_PASS, frames].rearrange(
-                        "(p j) t -> p j t", j=PACK
-                    ),
-                )
-            if tt == 0:
+            if b < B:
+                frames = slice(tt * T_TILE, (tt + 1) * T_TILE)
+                raw[i] = raw_pool.tile([P, PASSES, PACK, T_TILE], BF16, name="raw", tag="raw")
+                for g in range(PASSES):
+                    nc.sync.dma_start(
+                        out=raw[i][:, g],
+                        in_=h[b, g * K_PASS : (g + 1) * K_PASS, frames].rearrange(
+                            "(p j) t -> p j t", j=PACK
+                        ),
+                    )
+            if tt == 1 and b < B:
                 nc.sync.dma_start(out=penalty[:, b, :], in_=mask[b, 0, :].partition_broadcast(P))
-            if tt == T_TILES - 1:
+            if tt == 1 and 1 <= b <= B:
                 nc.sync.dma_start(
-                    out=x_rows[:, b], in_=x[b].rearrange("(ct c) t -> c ct t", c=P)
+                    out=x_rows[:, b - 1], in_=x[b - 1].rearrange("(ct c) t -> c ct t", c=P)
                 )
 
-        def regroup_tile(i):
+        def regroup_views(i, g):
+            dst = grouped[i][:, g].rearrange("p (c r) j -> p c j r", r=RUN)
+            src = raw[i][:, g].rearrange("p j (c r) -> p c j r", r=RUN)
+            return dst, src
+
+        def regroup_on_scalar(i):
             if i < 0 or i >= TILES:
                 return
-            for g in range(PASSES):
-                grouped[i, g] = grouped_pool.tile(
-                    [P, T_TILE, PACK], BF16, name="grouped", tag="grouped", align_bytes=64
-                )
-                nc.scalar.copy(
-                    out=grouped[i, g][:].rearrange("p (c r) j -> p c j r", r=RUN),
-                    in_=raw[i, g][:].rearrange("p j (c r) -> p c j r", r=RUN),
-                )
+            grouped[i] = grouped_pool.tile(
+                [P, PASSES, T_TILE, PACK], BF16, name="grouped", tag="grouped", align_bytes=64
+            )
+            for g in range(PASSES - 1 if i < HELPED_TILES else PASSES):
+                dst, src = regroup_views(i, g)
+                nc.scalar.copy(out=dst, in_=src)
+
+        def regroup_on_vector(i):
+            if i < 0 or i >= HELPED_TILES:
+                return
+            dst, src = regroup_views(i, PASSES - 1)
+            nc.vector.tensor_copy(out=dst, in_=src)
 
         def quantise_and_multiply(i):
             if i < 0 or i >= TILES:
@@ -147,28 +158,27 @@ def tile_attentivestatspool_pb_t_kernel(tc, h, x, mask, w2, b2, g2, be2, out):
                     op0=ALU.is_equal,
                     op1=ALU.mult,
                 )
-            for g in range(PASSES):
-                codes[i, g] = codes_pool.tile(
-                    [P, T_TILE], U32, name="codes", tag="codes", align_bytes=64
-                )
-                scales[i, g] = codes_pool.tile(
-                    [P, T_TILE], U8, name="scales", tag="scales", align_bytes=64
-                )
-                nc.vector.quantize_mx(
-                    out=codes[i, g][:].bitcast(FP8X4),
-                    scales=scales[i, g][:],
-                    in_=grouped[i, g][:].rearrange("p t j -> p (t j)"),
-                )
+            codes[i] = codes_pool.tile(
+                [P, PASSES, T_TILE], U32, name="codes", tag="codes", align_bytes=64
+            )
+            scales[i] = codes_pool.tile(
+                [P, PASSES, T_TILE], U8, name="scales", tag="scales", align_bytes=64
+            )
+            nc.vector.quantize_mx(
+                out=codes[i][:].rearrange("p g t -> p (g t)").bitcast(FP8X4),
+                scales=scales[i][:].rearrange("p g t -> p (g t)"),
+                in_=grouped[i][:].rearrange("p g t j -> p (g t j)"),
+            )
             for ct in range(C_TILES):
+                channels = slice(ct * P, (ct + 1) * P)
                 banks[i, ct] = bank_pool.tile([P, T_TILE], F32, name="bank", tag="bank")
                 for g in range(PASSES):
-                    channels = slice(g * C + ct * P, g * C + (ct + 1) * P)
                     nc.tensor.matmul_mx(
                         out=banks[i, ct][:],
-                        lhsT=w2_codes[:, channels].bitcast(FP8X4),
-                        lhsT_scale=w2_scales[:, channels],
-                        rhs=codes[i, g][:].bitcast(FP8X4),
-                        rhs_scale=scales[i, g][:],
+                        lhsT=w2_codes[:, g, channels].bitcast(FP8X4),
+                        lhsT_scale=w2_scales[:, g, channels],
+                        rhs=codes[i][:, g, :].bitcast(FP8X4),
+                        rhs_scale=scales[i][:, g, :],
                         start=(g == 0),
                         stop=(g == PASSES - 1),
                     )
@@ -192,65 +202,63 @@ def tile_attentivestatspool_pb_t_kernel(tc, h, x, mask, w2, b2, g2, be2, out):
             if k < 0 or k >= B * 2 * C_TILES:
                 return
             b, step = divmod(k, 2 * C_TILES)
-            ct = step % C_TILES
-            col = slice(b * C_TILES + ct, b * C_TILES + ct + 1)
-            row = scores[b][:, ct, :]
             if step < C_TILES:
+                ct = step
+                row = scores[b][:, ct, :]
                 nc.vector.tensor_reduce(
-                    out=neg_max[:, col], in_=row, axis=AXIS.X, op=ALU.max, negate=True
+                    out=neg_max[:, b, ct : ct + 1], in_=row, axis=AXIS.X, op=ALU.max, negate=True
                 )
                 nc.scalar.activation(
-                    out=row, in_=row, func=ACT.Exp, bias=neg_max[:, col], accum_out=sum_e[:, col]
+                    out=row,
+                    in_=row,
+                    func=ACT.Exp,
+                    bias=neg_max[:, b, ct : ct + 1],
+                    accum_out=sum_e[:, b, ct : ct + 1],
                 )
-            else:
-                prod = prod_pool.tile([P, T], F32, name="prod", tag="prod")
+                return
+            power = step - C_TILES
+            for ct in range(C_TILES):
+                if power == 0:
+                    prod[b, ct] = prod_pool.tile([P, T], F32, name="prod", tag="prod")
                 nc.vector.scalar_tensor_tensor(
-                    out=prod[:],
-                    in0=row,
+                    out=prod[b, ct][:],
+                    in0=scores[b][:, ct, :] if power == 0 else prod[b, ct][:],
                     scalar=1.0,
                     in1=x_rows[:, b, ct, :],
                     op0=ALU.mult,
                     op1=ALU.mult,
-                    accum_out=sum_ex[:, col],
-                )
-                nc.vector.scalar_tensor_tensor(
-                    out=prod[:],
-                    in0=prod[:],
-                    scalar=1.0,
-                    in1=x_rows[:, b, ct, :],
-                    op0=ALU.mult,
-                    op1=ALU.mult,
-                    accum_out=sum_exx[:, col],
+                    accum_out=sums[:, power, b, ct : ct + 1],
                 )
 
         assert 2 * C_TILES == T_TILES
         for n in range(-REGROUP_LEAD - LOAD_LEAD, TILES + T_TILES):
             load_tile(n + REGROUP_LEAD + LOAD_LEAD)
-            regroup_tile(n + REGROUP_LEAD)
+            regroup_on_scalar(n + REGROUP_LEAD)
             quantise_and_multiply(n)
             mask_scores(n - 1)
+            regroup_on_vector(n + 1)
             pool_step(n - T_TILES)
 
-        nc.scalar.activation(out=warm[:], in_=sum_e[:, B * C_TILES - 1 :], func=ACT.Sqrt)
+        nc.scalar.activation(out=warm[:], in_=sum_e[:, B - 1, C_TILES - 1 :], func=ACT.Sqrt)
 
-        def by_utterance(stat):
-            return stat[:].rearrange("p (b ct) -> p b ct", ct=C_TILES)
-
-        v = const.tile([P, 2, B, C_TILES], F32)
         full = [P, 2, B, C_TILES]
-        recip = const.tile([P, B * C_TILES], F32)
+
+        def per_utterance(stat):
+            return stat[:].unsqueeze(1).unsqueeze(3).to_broadcast(full)
+
+        def per_entry(columns):
+            return columns.rearrange("p (s ct) -> p s ct", s=2).unsqueeze(2).to_broadcast(full)
+
+        v = const.tile(full, F32)
+        recip = const.tile([P, B, C_TILES], F32)
         nc.vector.reciprocal(out=recip[:], in_=sum_e[:])
         nc.vector.tensor_tensor(
-            out=v[:, 0], in0=by_utterance(sum_ex), in1=by_utterance(recip), op=ALU.mult
-        )
-        second = const.tile([P, B, C_TILES], F32)
-        nc.vector.tensor_tensor(
-            out=second[:], in0=by_utterance(sum_exx), in1=by_utterance(recip), op=ALU.mult
+            out=v[:], in0=sums[:], in1=recip[:].unsqueeze(1).to_broadcast(full), op=ALU.mult
         )
         mean_sq = const.tile([P, B, C_TILES], F32)
         nc.vector.tensor_tensor(out=mean_sq[:], in0=v[:, 0], in1=v[:, 0], op=ALU.mult)
         variance = const.tile([P, B, C_TILES], F32)
-        nc.vector.tensor_tensor(out=variance[:], in0=second[:], in1=mean_sq[:], op=ALU.subtract)
+        nc.vector.tensor_tensor(out=variance[:], in0=v[:, 1], in1=mean_sq[:], op=ALU.subtract)
         nc.vector.tensor_scalar_max(out=variance[:], in0=variance[:], scalar1=EPS_STD)
         nc.scalar.activation(out=v[:, 1], in_=variance[:], func=ACT.Sqrt)
 
@@ -272,17 +280,15 @@ def tile_attentivestatspool_pb_t_kernel(tc, h, x, mask, w2, b2, g2, be2, out):
             )
             return result
 
-        def per_utterance(stat):
-            return stat[:].unsqueeze(1).unsqueeze(3).to_broadcast(full)
-
-        def per_entry(columns):
-            return columns.rearrange("p (s ct) -> p s ct", s=2).unsqueeze(2).to_broadcast(full)
-
         mu = mean_over_entries(v, "mu")
         centred = const.tile(full, F32)
         nc.vector.tensor_tensor(out=centred[:], in0=v[:], in1=per_utterance(mu), op=ALU.subtract)
         squared = const.tile(full, F32)
         nc.vector.tensor_tensor(out=squared[:], in0=centred[:], in1=centred[:], op=ALU.mult)
+        gained = const.tile(full, F32)
+        nc.vector.tensor_tensor(
+            out=gained[:], in0=centred[:], in1=per_entry(gb[:, 0:4]), op=ALU.mult
+        )
         var_ln = mean_over_entries(squared, "var_ln")
         nc.vector.tensor_scalar_add(out=var_ln[:], in0=var_ln[:], scalar1=EPS_LN)
         std_ln = const.tile([P, B], F32)
@@ -290,15 +296,12 @@ def tile_attentivestatspool_pb_t_kernel(tc, h, x, mask, w2, b2, g2, be2, out):
         rstd_ln = const.tile([P, B], F32)
         nc.vector.reciprocal(out=rstd_ln[:], in_=std_ln[:])
         nc.vector.tensor_tensor(
-            out=centred[:], in0=centred[:], in1=per_utterance(rstd_ln), op=ALU.mult
-        )
-        nc.vector.tensor_tensor(
-            out=centred[:], in0=centred[:], in1=per_entry(gb[:, 0:4]), op=ALU.mult
+            out=gained[:], in0=gained[:], in1=per_utterance(rstd_ln), op=ALU.mult
         )
         rows = 2 * B * C_TILES
         nc.vector.tensor_tensor(
             out=y_pad[:, 0:rows].rearrange("p (b s ct) -> p s b ct", s=2, ct=C_TILES),
-            in0=centred[:],
+            in0=gained[:],
             in1=per_entry(gb[:, 4:8]),
             op=ALU.add,
         )

@@ -56,22 +56,18 @@ def tile_attentivestatspool_pb_t_kernel(tc, h, x, mask, w2, b2, g2, be2, out):
         nc.vector.memset(warm[:], 0.0)
 
         w2_rows = const.tile([P, C_TILES, H], BF16)
-        nc.scalar.dma_start(out=w2_rows[:], in_=w2.rearrange("(ct c) k -> c ct k", c=P))
+        nc.sync.dma_start(out=w2_rows[:], in_=w2.rearrange("(ct c) k -> c ct k", c=P))
         nc.scalar.dma_start(out=gb_rows[0:4, :], in_=g2.rearrange("(r c) -> r c", c=P))
         nc.scalar.dma_start(out=gb_rows[4:8, :], in_=be2.rearrange("(r c) -> r c", c=P))
         nc.scalar.activation(out=warm[:], in_=warm[:], func=ACT.Exp)
-        w2_sorted = const.tile([P, C_TILES * PASSES, PACK, P], BF16)
-        nc.vector.tensor_copy(
-            out=w2_sorted[:],
-            in_=w2_rows[:].rearrange("c ct (g p j) -> c (ct g) j p", p=P, j=PACK),
-        )
+        w2_by_word = w2_rows[:].rearrange("c ct (g p j) -> c ct g j p", p=P, j=PACK)
         w2_grouped = const.tile([P, PASSES, C_TILES, P, PACK], BF16, align_bytes=64)
         for g in range(PASSES):
             w2_t = misc_pool.tile([P, C_TILES, PACK, P], BF16, tag="misc")
             for ct in range(C_TILES):
                 for j in range(PACK):
                     nc.tensor.transpose(
-                        w2_t[:, ct, j, :], w2_sorted[:, ct * PASSES + g, j, :], ident_bf[:]
+                        w2_t[:, ct, j, :], w2_by_word[:, ct, g, j, :], ident_bf[:]
                     )
             nc.vector.tensor_copy(
                 out=w2_grouped[:, g], in_=w2_t[:].rearrange("p ct j c -> p ct c j")
@@ -244,59 +240,58 @@ def tile_attentivestatspool_pb_t_kernel(tc, h, x, mask, w2, b2, g2, be2, out):
         full = [P, 2, B, C_TILES]
 
         def per_utterance(stat):
-            return stat[:].unsqueeze(1).unsqueeze(3).to_broadcast(full)
+            return stat.unsqueeze(1).unsqueeze(3).to_broadcast(full)
 
         def per_entry(columns):
             return columns.rearrange("p (s ct) -> p s ct", s=2).unsqueeze(2).to_broadcast(full)
 
-        v = const.tile(full, F32)
+        moments = const.tile([P, 2, 2 * B, C_TILES], F32)
+        v = moments[:, :, 0:B, :]
+        v_sq = moments[:, :, B : 2 * B, :]
         recip = const.tile([P, B, C_TILES], F32)
         nc.vector.reciprocal(out=recip[:], in_=sum_e[:])
         nc.vector.tensor_tensor(
-            out=v[:], in0=sums[:], in1=recip[:].unsqueeze(1).to_broadcast(full), op=ALU.mult
+            out=v, in0=sums[:], in1=recip[:].unsqueeze(1).to_broadcast(full), op=ALU.mult
         )
-        mean_sq = const.tile([P, B, C_TILES], F32)
-        nc.vector.tensor_tensor(out=mean_sq[:], in0=v[:, 0], in1=v[:, 0], op=ALU.mult)
+        nc.vector.tensor_tensor(out=v_sq[:, 0], in0=v[:, 0], in1=v[:, 0], op=ALU.mult)
         variance = const.tile([P, B, C_TILES], F32)
-        nc.vector.tensor_tensor(out=variance[:], in0=v[:, 1], in1=mean_sq[:], op=ALU.subtract)
-        nc.vector.tensor_scalar_max(out=variance[:], in0=variance[:], scalar1=EPS_STD)
-        nc.scalar.activation(out=v[:, 1], in_=variance[:], func=ACT.Sqrt)
+        nc.vector.tensor_tensor(out=variance[:], in0=v[:, 1], in1=v_sq[:, 0], op=ALU.subtract)
+        nc.vector.tensor_scalar_max(out=v_sq[:, 1], in0=variance[:], scalar1=EPS_STD)
+        nc.scalar.activation(out=v[:, 1], in_=v_sq[:, 1], func=ACT.Sqrt)
 
-        def mean_over_entries(values, name):
-            share = misc_pool.tile(full, F32, name=name + "_share", tag="misc")
-            nc.tensor.matmul(
-                out=share[:].rearrange("p s b ct -> p (s b ct)"),
-                lhsT=averager[:],
-                rhs=values[:].rearrange("p s b ct -> p (s b ct)"),
-                start=True,
-                stop=True,
-            )
-            result = const.tile([P, B], F32, name=name)
-            nc.vector.tensor_reduce(
-                out=result[:],
-                in_=share[:].rearrange("p s b ct -> p b s ct"),
-                axis=AXIS.XY,
-                op=ALU.add,
-            )
-            return result
-
-        mu = mean_over_entries(v, "mu")
-        centred = const.tile(full, F32)
-        nc.vector.tensor_tensor(out=centred[:], in0=v[:], in1=per_utterance(mu), op=ALU.subtract)
-        squared = const.tile(full, F32)
-        nc.vector.tensor_tensor(out=squared[:], in0=centred[:], in1=centred[:], op=ALU.mult)
-        gained = const.tile(full, F32)
-        nc.vector.tensor_tensor(
-            out=gained[:], in0=centred[:], in1=per_entry(gb[:, 0:4]), op=ALU.mult
+        share = misc_pool.tile([P, 2, 2 * B, C_TILES], F32, tag="misc")
+        nc.tensor.matmul(
+            out=share[:].rearrange("p s m ct -> p (s m ct)"),
+            lhsT=averager[:],
+            rhs=moments[:].rearrange("p s m ct -> p (s m ct)"),
+            start=True,
+            stop=True,
         )
-        var_ln = mean_over_entries(squared, "var_ln")
-        nc.vector.tensor_scalar_add(out=var_ln[:], in0=var_ln[:], scalar1=EPS_LN)
+        averages = const.tile([P, 2 * B], F32)
+        nc.vector.tensor_reduce(
+            out=averages[:], in_=share[:].rearrange("p s m ct -> p m s ct"), axis=AXIS.XY, op=ALU.add
+        )
+        mu = averages[:, 0:B]
+        mu_sq = const.tile([P, B], F32)
+        nc.vector.tensor_tensor(out=mu_sq[:], in0=mu, in1=mu, op=ALU.mult)
+        var_ln = const.tile([P, B], F32)
+        nc.vector.tensor_tensor(
+            out=var_ln[:], in0=averages[:, B : 2 * B], in1=mu_sq[:], op=ALU.subtract
+        )
+        nc.vector.tensor_scalar(
+            out=var_ln[:], in0=var_ln[:], scalar1=0.0, scalar2=EPS_LN, op0=ALU.max, op1=ALU.add
+        )
         std_ln = const.tile([P, B], F32)
         nc.scalar.activation(out=std_ln[:], in_=var_ln[:], func=ACT.Sqrt)
+        gained = const.tile(full, F32)
+        nc.vector.tensor_tensor(out=gained[:], in0=v, in1=per_utterance(mu), op=ALU.subtract)
+        nc.vector.tensor_tensor(
+            out=gained[:], in0=gained[:], in1=per_entry(gb[:, 0:4]), op=ALU.mult
+        )
         rstd_ln = const.tile([P, B], F32)
         nc.vector.reciprocal(out=rstd_ln[:], in_=std_ln[:])
         nc.vector.tensor_tensor(
-            out=gained[:], in0=gained[:], in1=per_utterance(rstd_ln), op=ALU.mult
+            out=gained[:], in0=gained[:], in1=per_utterance(rstd_ln[:]), op=ALU.mult
         )
         rows = 2 * B * C_TILES
         nc.vector.tensor_tensor(

@@ -125,15 +125,33 @@ def tile_attentivestatspool_pb_t_kernel(tc, h, x, mask, w2, b2, g2, be2, out):
             src = raw[i][:, g].rearrange("p j (c r) -> p c j r", r=RUN)
             return dst, src
 
+        def on_gpsimd(i):
+            return i >= HELPED_TILES + REGROUP_LEAD and (i - REGROUP_LEAD) % T_TILES < C_TILES
+
         def regroup_on_scalar(i):
             if i < 0 or i >= TILES:
                 return
             grouped[i] = grouped_pool.tile(
                 [P, PASSES, T_TILE, PACK], BF16, name="grouped", tag="grouped", align_bytes=64
             )
-            for g in range(PASSES - 1 if i < HELPED_TILES else PASSES):
+            for g in range(PASSES - 1 if i < HELPED_TILES or on_gpsimd(i) else PASSES):
                 dst, src = regroup_views(i, g)
                 nc.scalar.copy(out=dst, in_=src)
+
+        token = const.tile([P, 1], U32)
+
+        def regroup_on_gpsimd(i):
+            if i >= TILES or not on_gpsimd(i):
+                return
+            nc.gpsimd.tensor_copy(out=token[:], in_=codes[i - REGROUP_LEAD][:, 0, 0:1])
+            nc.gpsimd.tensor_scalar(
+                out=grouped[i][:, PASSES - 1],
+                in0=raw[i][:, PASSES - 1].rearrange("p j t -> p t j"),
+                scalar1=1.0,
+                scalar2=0.0,
+                op0=ALU.mult,
+                op1=ALU.add,
+            )
 
         def regroup_on_vector(i):
             if i < 0 or i >= HELPED_TILES:
@@ -231,6 +249,7 @@ def tile_attentivestatspool_pb_t_kernel(tc, h, x, mask, w2, b2, g2, be2, out):
             load_tile(n + REGROUP_LEAD + LOAD_LEAD)
             regroup_on_scalar(n + REGROUP_LEAD)
             quantise_and_multiply(n)
+            regroup_on_gpsimd(n + REGROUP_LEAD)
             mask_scores(n - 1)
             regroup_on_vector(n + 1)
             pool_step(n - T_TILES)

@@ -28,6 +28,9 @@ MASKED = -1e30
 
 LOAD_LEAD = 2
 REGROUP_LEAD = 2
+GPSIMD_STEPS = (1,)
+FIRST_PART = 512
+VECTOR_STEPS = (3,)
 HELPED_TILES = 4
 
 
@@ -38,7 +41,7 @@ def tile_attentivestatspool_pb_t_kernel(tc, h, x, mask, w2, b2, g2, be2, out):
     ) as raw_pool, tc.tile_pool(name="grouped", bufs=REGROUP_LEAD + 2) as grouped_pool, tc.tile_pool(
         name="codes", bufs=3
     ) as codes_pool, tc.tile_pool(name="scores", bufs=2) as score_pool, tc.tile_pool(
-        name="prod", bufs=2
+        name="prod", bufs=4
     ) as prod_pool, tc.psum_pool(name="banks", bufs=6) as bank_pool, tc.psum_pool(
         name="misc", bufs=2
     ) as misc_pool, tc.manual_schedule():
@@ -126,7 +129,10 @@ def tile_attentivestatspool_pb_t_kernel(tc, h, x, mask, w2, b2, g2, be2, out):
             return dst, src
 
         def on_gpsimd(i):
-            return i >= HELPED_TILES + REGROUP_LEAD and (i - REGROUP_LEAD) % T_TILES < C_TILES
+            return i >= HELPED_TILES + REGROUP_LEAD and (i - REGROUP_LEAD) % T_TILES in GPSIMD_STEPS
+
+        def on_vector(i):
+            return i < HELPED_TILES or (i - REGROUP_LEAD) % T_TILES in VECTOR_STEPS
 
         def regroup_on_scalar(i):
             if i < 0 or i >= TILES:
@@ -134,16 +140,52 @@ def tile_attentivestatspool_pb_t_kernel(tc, h, x, mask, w2, b2, g2, be2, out):
             grouped[i] = grouped_pool.tile(
                 [P, PASSES, T_TILE, PACK], BF16, name="grouped", tag="grouped", align_bytes=64
             )
-            for g in range(PASSES - 1 if i < HELPED_TILES or on_gpsimd(i) else PASSES):
+            for g in range(PASSES - 1 if on_vector(i) or on_gpsimd(i) else PASSES):
                 dst, src = regroup_views(i, g)
                 nc.scalar.copy(out=dst, in_=src)
 
-        token = const.tile([P, 1], U32)
+        token = const.tile([P, 1], F32)
+        token_bf = const.tile([P, 1], BF16)
+        junk = const.tile([P, T], BF16)
+
+        def wait_for_vector(n):
+            b, step = divmod(n - 1 - T_TILES, 2 * C_TILES)
+            if n + 1 < TILES and on_vector(n + 1):
+                nc.gpsimd.tensor_copy(out=token_bf[:], in_=grouped[n + 1][:, PASSES - 1, T_TILE - 1, PACK - 1 :])
+                return
+            if step < C_TILES:
+                written = neg_max[:, b, step : step + 1]
+            elif step == C_TILES:
+                written = sums[:, 0, b, C_TILES - 1 :]
+            else:
+                written = sums[:, 1, b, 0:1]
+            nc.gpsimd.tensor_copy(out=token[:], in_=written)
+
+        def second_moment_elsewhere(n):
+            b, step = divmod(n - T_TILES, T_TILES)
+            ct = C_TILES - 1
+            if step == 3 and 0 <= b < B - 1:
+                part = slice(0, FIRST_PART)
+            elif step == 0 and 1 <= b < B:
+                b -= 1
+                part = slice(FIRST_PART, T)
+            elif step == 2 and 1 <= b < B:
+                b -= 1
+                nc.scalar.activation(
+                    out=junk[:], in_=prod[b, ct][:], func=ACT.Copy, accum_out=sums[:, 1, b, ct : ct + 1]
+                )
+                return
+            else:
+                return
+            wait_for_vector(n)
+            nc.gpsimd.tensor_tensor(
+                out=prod[b, ct][:, part], in0=prod[b, ct][:, part], in1=x_rows[:, b, ct, part], op=ALU.mult
+            )
 
         def regroup_on_gpsimd(i):
             if i >= TILES or not on_gpsimd(i):
                 return
-            nc.gpsimd.tensor_copy(out=token[:], in_=codes[i - REGROUP_LEAD][:, 0, 0:1])
+            wait_for_vector(i - REGROUP_LEAD)
             nc.gpsimd.tensor_scalar(
                 out=grouped[i][:, PASSES - 1],
                 in0=raw[i][:, PASSES - 1].rearrange("p j t -> p t j"),
@@ -154,7 +196,7 @@ def tile_attentivestatspool_pb_t_kernel(tc, h, x, mask, w2, b2, g2, be2, out):
             )
 
         def regroup_on_vector(i):
-            if i < 0 or i >= HELPED_TILES:
+            if i < 0 or i >= TILES or not on_vector(i):
                 return
             dst, src = regroup_views(i, PASSES - 1)
             nc.vector.tensor_copy(out=dst, in_=src)
@@ -231,7 +273,7 @@ def tile_attentivestatspool_pb_t_kernel(tc, h, x, mask, w2, b2, g2, be2, out):
                 )
                 return
             power = step - C_TILES
-            for ct in range(C_TILES):
+            for ct in range(C_TILES - 1 if power == 1 and b < B - 1 else C_TILES):
                 if power == 0:
                     prod[b, ct] = prod_pool.tile([P, T], F32, name="prod", tag="prod")
                 nc.vector.scalar_tensor_tensor(
@@ -248,10 +290,11 @@ def tile_attentivestatspool_pb_t_kernel(tc, h, x, mask, w2, b2, g2, be2, out):
         for n in range(-REGROUP_LEAD - LOAD_LEAD, TILES + T_TILES):
             load_tile(n + REGROUP_LEAD + LOAD_LEAD)
             regroup_on_scalar(n + REGROUP_LEAD)
+            regroup_on_vector(n + 1)
             quantise_and_multiply(n)
             regroup_on_gpsimd(n + REGROUP_LEAD)
+            second_moment_elsewhere(n)
             mask_scores(n - 1)
-            regroup_on_vector(n + 1)
             pool_step(n - T_TILES)
 
         nc.scalar.activation(out=warm[:], in_=sum_e[:, B - 1, C_TILES - 1 :], func=ACT.Sqrt)

@@ -31,6 +31,8 @@ REGROUP_LEAD = 2
 GPSIMD_STEPS = (1,)
 FIRST_PART = 512
 VECTOR_STEPS = (3,)
+W2_AFTER = 0
+FIRST_PIECES = 1
 HELPED_TILES = 4
 
 
@@ -58,6 +60,21 @@ def tile_attentivestatspool_pb_t_kernel(tc, h, x, mask, w2, b2, g2, be2, out):
         warm = const.tile([P, 1], F32)
         nc.vector.memset(warm[:], 0.0)
 
+        raw = {}
+
+        def load_piece(i, g):
+            b, tt = divmod(i, T_TILES)
+            nc.sync.dma_start(
+                out=raw[i][:, g],
+                in_=h[b, g * K_PASS : (g + 1) * K_PASS, tt * T_TILE : (tt + 1) * T_TILE].rearrange(
+                    "(p j) t -> p j t", j=PACK
+                ),
+            )
+
+        raw[0] = raw_pool.tile([P, PASSES, PACK, T_TILE], BF16, name="raw", tag="raw")
+        for g in range(FIRST_PIECES):
+            load_piece(0, g)
+
         w2_rows = const.tile([P, C_TILES, H], BF16)
         nc.sync.dma_start(out=w2_rows[:], in_=w2.rearrange("(ct c) k -> c ct k", c=P))
         nc.scalar.dma_start(out=gb_rows[0:4, :], in_=g2.rearrange("(r c) -> r c", c=P))
@@ -65,28 +82,29 @@ def tile_attentivestatspool_pb_t_kernel(tc, h, x, mask, w2, b2, g2, be2, out):
         nc.scalar.activation(out=warm[:], in_=warm[:], func=ACT.Exp)
         w2_by_word = w2_rows[:].rearrange("c ct (g p j) -> c ct g j p", p=P, j=PACK)
         w2_grouped = const.tile([P, PASSES, C_TILES, P, PACK], BF16, align_bytes=64)
-        for g in range(PASSES):
-            w2_t = misc_pool.tile([P, C_TILES, PACK, P], BF16, tag="misc")
-            for ct in range(C_TILES):
-                for j in range(PACK):
-                    nc.tensor.transpose(
-                        w2_t[:, ct, j, :], w2_by_word[:, ct, g, j, :], ident_bf[:]
-                    )
-            nc.vector.tensor_copy(
-                out=w2_grouped[:, g], in_=w2_t[:].rearrange("p ct j c -> p ct c j")
-            )
         w2_codes = const.tile([P, PASSES, C], U32, align_bytes=64)
         w2_scales = const.tile([P, PASSES, C], U8, align_bytes=64)
-        nc.vector.quantize_mx(
-            out=w2_codes[:].rearrange("p g c -> p (g c)").bitcast(FP8X4),
-            scales=w2_scales[:].rearrange("p g c -> p (g c)"),
-            in_=w2_grouped[:].rearrange("p g ct c j -> p (g ct c j)"),
-        )
-
-        gb_t = misc_pool.tile([P, P], BF16, tag="misc")
-        nc.tensor.transpose(gb_t[:], gb_rows[:], ident_bf[:])
         gb = const.tile([P, 8], F32)
-        nc.vector.tensor_copy(out=gb[:], in_=gb_t[:, 0:8])
+
+        def turn_w2():
+            for g in range(PASSES):
+                w2_t = misc_pool.tile([P, C_TILES, PACK, P], BF16, name="w2_t", tag="misc")
+                for ct in range(C_TILES):
+                    for j in range(PACK):
+                        nc.tensor.transpose(
+                            w2_t[:, ct, j, :], w2_by_word[:, ct, g, j, :], ident_bf[:]
+                        )
+                nc.scalar.copy(out=w2_grouped[:, g], in_=w2_t[:].rearrange("p ct j c -> p ct c j"))
+            gb_t = misc_pool.tile([P, P], BF16, name="gb_t", tag="misc")
+            nc.tensor.transpose(gb_t[:], gb_rows[:], ident_bf[:])
+            nc.scalar.copy(out=gb[:], in_=gb_t[:, 0:8])
+
+        def quantise_w2():
+            nc.vector.quantize_mx(
+                out=w2_codes[:].rearrange("p g c -> p (g c)").bitcast(FP8X4),
+                scales=w2_scales[:].rearrange("p g c -> p (g c)"),
+                in_=w2_grouped[:].rearrange("p g ct c j -> p (g ct c j)"),
+            )
 
         neg_max = const.tile([P, B, C_TILES], F32)
         sum_e = const.tile([P, B, C_TILES], F32)
@@ -94,7 +112,6 @@ def tile_attentivestatspool_pb_t_kernel(tc, h, x, mask, w2, b2, g2, be2, out):
 
         penalty = const.tile([P, B, T], BF16)
         x_rows = const.tile([P, B, C_TILES, T], BF16)
-        raw = {}
         grouped = {}
         codes = {}
         scales = {}
@@ -107,15 +124,10 @@ def tile_attentivestatspool_pb_t_kernel(tc, h, x, mask, w2, b2, g2, be2, out):
                 return
             b, tt = divmod(i, T_TILES)
             if b < B:
-                frames = slice(tt * T_TILE, (tt + 1) * T_TILE)
-                raw[i] = raw_pool.tile([P, PASSES, PACK, T_TILE], BF16, name="raw", tag="raw")
-                for g in range(PASSES):
-                    nc.sync.dma_start(
-                        out=raw[i][:, g],
-                        in_=h[b, g * K_PASS : (g + 1) * K_PASS, frames].rearrange(
-                            "(p j) t -> p j t", j=PACK
-                        ),
-                    )
+                if i > 0:
+                    raw[i] = raw_pool.tile([P, PASSES, PACK, T_TILE], BF16, name="raw", tag="raw")
+                for g in range(FIRST_PIECES if i == 0 else 0, PASSES):
+                    load_piece(i, g)
             if tt == 1 and b < B:
                 nc.sync.dma_start(out=penalty[:, b, :], in_=mask[b, 0, :].partition_broadcast(P))
             if tt == 1 and 1 <= b <= B:
@@ -144,22 +156,15 @@ def tile_attentivestatspool_pb_t_kernel(tc, h, x, mask, w2, b2, g2, be2, out):
                 dst, src = regroup_views(i, g)
                 nc.scalar.copy(out=dst, in_=src)
 
+        newest = [None]
+        before_quantise = {}
         token = const.tile([P, 1], F32)
         token_bf = const.tile([P, 1], BF16)
         junk = const.tile([P, T], BF16)
 
         def wait_for_vector(n):
-            b, step = divmod(n - 1 - T_TILES, 2 * C_TILES)
-            if n + 1 < TILES and on_vector(n + 1):
-                nc.gpsimd.tensor_copy(out=token_bf[:], in_=grouped[n + 1][:, PASSES - 1, T_TILE - 1, PACK - 1 :])
-                return
-            if step < C_TILES:
-                written = neg_max[:, b, step : step + 1]
-            elif step == C_TILES:
-                written = sums[:, 0, b, C_TILES - 1 :]
-            else:
-                written = sums[:, 1, b, 0:1]
-            nc.gpsimd.tensor_copy(out=token[:], in_=written)
+            written = before_quantise.get(n, newest[0])
+            nc.gpsimd.tensor_copy(out=token_bf[:] if written.dtype == BF16 else token[:], in_=written)
 
         def second_moment_elsewhere(n):
             b, step = divmod(n - T_TILES, T_TILES)
@@ -200,20 +205,27 @@ def tile_attentivestatspool_pb_t_kernel(tc, h, x, mask, w2, b2, g2, be2, out):
                 return
             dst, src = regroup_views(i, PASSES - 1)
             nc.vector.tensor_copy(out=dst, in_=src)
+            newest[0] = grouped[i][:, PASSES - 1, T_TILE - 1, PACK - 1 :]
+
+        def make_penalty(i):
+            b, tt = divmod(i, T_TILES)
+            if tt != 1 or b < 0 or b >= B:
+                return
+            nc.vector.tensor_scalar(
+                out=penalty[:, b, :],
+                in0=penalty[:, b, :],
+                scalar1=0.0,
+                scalar2=MASKED,
+                op0=ALU.is_equal,
+                op1=ALU.mult,
+            )
+            newest[0] = penalty[:, b, T - 1 :]
 
         def quantise_and_multiply(i):
             if i < 0 or i >= TILES:
                 return
             b, tt = divmod(i, T_TILES)
-            if tt == 0:
-                nc.vector.tensor_scalar(
-                    out=penalty[:, b, :],
-                    in0=penalty[:, b, :],
-                    scalar1=0.0,
-                    scalar2=MASKED,
-                    op0=ALU.is_equal,
-                    op1=ALU.mult,
-                )
+            before_quantise[i] = newest[0]
             codes[i] = codes_pool.tile(
                 [P, PASSES, T_TILE], U32, name="codes", tag="codes", align_bytes=64
             )
@@ -225,6 +237,8 @@ def tile_attentivestatspool_pb_t_kernel(tc, h, x, mask, w2, b2, g2, be2, out):
                 scales=scales[i][:].rearrange("p g t -> p (g t)"),
                 in_=grouped[i][:].rearrange("p g t j -> p (g t j)"),
             )
+            if i == 0:
+                quantise_w2()
             for ct in range(C_TILES):
                 channels = slice(ct * P, (ct + 1) * P)
                 banks[i, ct] = bank_pool.tile([P, T_TILE], F32, name="bank", tag="bank")
@@ -253,6 +267,7 @@ def tile_attentivestatspool_pb_t_kernel(tc, h, x, mask, w2, b2, g2, be2, out):
                     in1=penalty[:, b, frames],
                     op=ALU.add,
                 )
+            newest[0] = scores[b][:, C_TILES - 1, (tt + 1) * T_TILE - 1 : (tt + 1) * T_TILE]
 
         def pool_step(k):
             if k < 0 or k >= B * 2 * C_TILES:
@@ -264,6 +279,7 @@ def tile_attentivestatspool_pb_t_kernel(tc, h, x, mask, w2, b2, g2, be2, out):
                 nc.vector.tensor_reduce(
                     out=neg_max[:, b, ct : ct + 1], in_=row, axis=AXIS.X, op=ALU.max, negate=True
                 )
+                newest[0] = neg_max[:, b, ct : ct + 1]
                 nc.scalar.activation(
                     out=row,
                     in_=row,
@@ -273,7 +289,12 @@ def tile_attentivestatspool_pb_t_kernel(tc, h, x, mask, w2, b2, g2, be2, out):
                 )
                 return
             power = step - C_TILES
+            last_step = power == 1 and b == B - 1
+            if last_step:
+                nc.vector.reciprocal(out=recip[:], in_=sum_e[:])
             for ct in range(C_TILES - 1 if power == 1 and b < B - 1 else C_TILES):
+                if last_step and ct == C_TILES - 1:
+                    nc.vector.tensor_tensor(out=v[:, 0], in0=sums[:, 0], in1=recip[:], op=ALU.mult)
                 if power == 0:
                     prod[b, ct] = prod_pool.tile([P, T], F32, name="prod", tag="prod")
                 nc.vector.scalar_tensor_tensor(
@@ -285,15 +306,27 @@ def tile_attentivestatspool_pb_t_kernel(tc, h, x, mask, w2, b2, g2, be2, out):
                     op1=ALU.mult,
                     accum_out=sums[:, power, b, ct : ct + 1],
                 )
+                newest[0] = sums[:, power, b, ct : ct + 1]
+
+        moments = const.tile([P, 2, 2 * B, C_TILES], F32)
+        v = moments[:, :, 0:B, :]
+        v_sq = moments[:, :, B : 2 * B, :]
+        recip = const.tile([P, B, C_TILES], F32)
 
         assert 2 * C_TILES == T_TILES
         for n in range(-REGROUP_LEAD - LOAD_LEAD, TILES + T_TILES):
             load_tile(n + REGROUP_LEAD + LOAD_LEAD)
             regroup_on_scalar(n + REGROUP_LEAD)
-            regroup_on_vector(n + 1)
+            if n + REGROUP_LEAD == W2_AFTER:
+                turn_w2()
+            make_penalty(n)
+            if n + 1 >= HELPED_TILES:
+                regroup_on_vector(n + 1)
             quantise_and_multiply(n)
             regroup_on_gpsimd(n + REGROUP_LEAD)
             second_moment_elsewhere(n)
+            if n + 1 < HELPED_TILES:
+                regroup_on_vector(n + 1)
             mask_scores(n - 1)
             pool_step(n - T_TILES)
 
@@ -307,19 +340,13 @@ def tile_attentivestatspool_pb_t_kernel(tc, h, x, mask, w2, b2, g2, be2, out):
         def per_entry(columns):
             return columns.rearrange("p (s ct) -> p s ct", s=2).unsqueeze(2).to_broadcast(full)
 
-        moments = const.tile([P, 2, 2 * B, C_TILES], F32)
-        v = moments[:, :, 0:B, :]
-        v_sq = moments[:, :, B : 2 * B, :]
-        recip = const.tile([P, B, C_TILES], F32)
-        nc.vector.reciprocal(out=recip[:], in_=sum_e[:])
-        nc.vector.tensor_tensor(
-            out=v, in0=sums[:], in1=recip[:].unsqueeze(1).to_broadcast(full), op=ALU.mult
-        )
         nc.vector.tensor_tensor(out=v_sq[:, 0], in0=v[:, 0], in1=v[:, 0], op=ALU.mult)
         variance = const.tile([P, B, C_TILES], F32)
-        nc.vector.tensor_tensor(out=variance[:], in0=v[:, 1], in1=v_sq[:, 0], op=ALU.subtract)
+        nc.vector.tensor_tensor(out=variance[:], in0=sums[:, 1], in1=recip[:], op=ALU.mult)
+        nc.vector.tensor_tensor(out=variance[:], in0=variance[:], in1=v_sq[:, 0], op=ALU.subtract)
         nc.vector.tensor_scalar_max(out=v_sq[:, 1], in0=variance[:], scalar1=EPS_STD)
         nc.scalar.activation(out=v[:, 1], in_=v_sq[:, 1], func=ACT.Sqrt)
+        nc.scalar.activation(out=warm[:], in_=warm[:], func=ACT.Abs_reciprocal_sqrt)
 
         share = misc_pool.tile([P, 2, 2 * B, C_TILES], F32, tag="misc")
         nc.tensor.matmul(
@@ -337,21 +364,21 @@ def tile_attentivestatspool_pb_t_kernel(tc, h, x, mask, w2, b2, g2, be2, out):
         mu_sq = const.tile([P, B], F32)
         nc.vector.tensor_tensor(out=mu_sq[:], in0=mu, in1=mu, op=ALU.mult)
         var_ln = const.tile([P, B], F32)
-        nc.vector.tensor_tensor(
-            out=var_ln[:], in0=averages[:, B : 2 * B], in1=mu_sq[:], op=ALU.subtract
+        nc.vector.scalar_tensor_tensor(
+            out=var_ln[:],
+            in0=averages[:, B : 2 * B],
+            scalar=EPS_LN,
+            in1=mu_sq[:],
+            op0=ALU.add,
+            op1=ALU.subtract,
         )
-        nc.vector.tensor_scalar(
-            out=var_ln[:], in0=var_ln[:], scalar1=0.0, scalar2=EPS_LN, op0=ALU.max, op1=ALU.add
-        )
-        std_ln = const.tile([P, B], F32)
-        nc.scalar.activation(out=std_ln[:], in_=var_ln[:], func=ACT.Sqrt)
+        rstd_ln = const.tile([P, B], F32)
+        nc.scalar.activation(out=rstd_ln[:], in_=var_ln[:], func=ACT.Abs_reciprocal_sqrt)
         gained = const.tile(full, F32)
         nc.vector.tensor_tensor(out=gained[:], in0=v, in1=per_utterance(mu), op=ALU.subtract)
         nc.vector.tensor_tensor(
             out=gained[:], in0=gained[:], in1=per_entry(gb[:, 0:4]), op=ALU.mult
         )
-        rstd_ln = const.tile([P, B], F32)
-        nc.vector.reciprocal(out=rstd_ln[:], in_=std_ln[:])
         nc.vector.tensor_tensor(
             out=gained[:], in0=gained[:], in1=per_utterance(rstd_ln[:]), op=ALU.mult
         )

@@ -23,7 +23,7 @@ T_TILE = 512
 T_TILES = T // T_TILE
 C_TILES = C // P
 TILES = B * T_TILES
-RUN = 4
+RUN = 8
 MASKED = -1e30
 
 LOAD_LEAD = 2

@@ -30,9 +30,16 @@ LOAD_LEAD = 2
 REGROUP_LEAD = 2
 GPSIMD_STEPS = (1,)
 FIRST_PART = 512
-VECTOR_STEPS = (3,)
+VECTOR_STEPS = ()
 W2_AFTER = 0
 FIRST_PIECES = 1
+FOLD_STEP = 2
+VECTOR_SHARE = 256
+HEAD_SHARE = 512
+GPSIMD_SHARE = 512
+GPSIMD_SHORT_STEPS = ()
+GPSIMD_SHORT = 192
+SECOND_PART = 1536
 HELPED_TILES = 4
 
 
@@ -44,7 +51,7 @@ def tile_attentivestatspool_pb_t_kernel(tc, h, x, mask, w2, b2, g2, be2, out):
         name="codes", bufs=3
     ) as codes_pool, tc.tile_pool(name="scores", bufs=2) as score_pool, tc.tile_pool(
         name="prod", bufs=4
-    ) as prod_pool, tc.psum_pool(name="banks", bufs=6) as bank_pool, tc.psum_pool(
+    ) as prod_pool, tc.tile_pool(name="fold", bufs=2) as fold_pool, tc.psum_pool(name="banks", bufs=6) as bank_pool, tc.psum_pool(
         name="misc", bufs=2
     ) as misc_pool, tc.manual_schedule():
         ident_bf = const.tile([P, P], BF16)
@@ -135,13 +142,19 @@ def tile_attentivestatspool_pb_t_kernel(tc, h, x, mask, w2, b2, g2, be2, out):
                     out=x_rows[:, b - 1], in_=x[b - 1].rearrange("(ct c) t -> c ct t", c=P)
                 )
 
-        def regroup_views(i, g):
-            dst = grouped[i][:, g].rearrange("p (c r) j -> p c j r", r=RUN)
-            src = raw[i][:, g].rearrange("p j (c r) -> p c j r", r=RUN)
+        def regroup_views(i, g, start=0, end=T_TILE):
+            dst = grouped[i][:, g, start:end].rearrange("p (c r) j -> p c j r", r=RUN)
+            src = raw[i][:, g, :, start:end].rearrange("p j (c r) -> p c j r", r=RUN)
             return dst, src
 
+        def vector_frames(i):
+            return HEAD_SHARE if i < HELPED_TILES else VECTOR_SHARE
+
         def on_gpsimd(i):
-            return i >= HELPED_TILES + REGROUP_LEAD and (i - REGROUP_LEAD) % T_TILES in GPSIMD_STEPS
+            return i >= HELPED_TILES + REGROUP_LEAD and (i - REGROUP_LEAD) % T_TILES in GPSIMD_STEPS + GPSIMD_SHORT_STEPS
+
+        def gpsimd_frames(i):
+            return GPSIMD_SHARE if (i - REGROUP_LEAD) % T_TILES in GPSIMD_STEPS else GPSIMD_SHORT
 
         def on_vector(i):
             return i < HELPED_TILES or (i - REGROUP_LEAD) % T_TILES in VECTOR_STEPS
@@ -152,48 +165,70 @@ def tile_attentivestatspool_pb_t_kernel(tc, h, x, mask, w2, b2, g2, be2, out):
             grouped[i] = grouped_pool.tile(
                 [P, PASSES, T_TILE, PACK], BF16, name="grouped", tag="grouped", align_bytes=64
             )
-            for g in range(PASSES - 1 if on_vector(i) or on_gpsimd(i) else PASSES):
-                dst, src = regroup_views(i, g)
-                nc.scalar.copy(out=dst, in_=src)
+            for g in range(PASSES):
+                end = T_TILE
+                if g == PASSES - 1 and on_vector(i):
+                    end = T_TILE - vector_frames(i)
+                if g == PASSES - 1 and on_gpsimd(i):
+                    end = T_TILE - gpsimd_frames(i)
+                if end > 0:
+                    dst, src = regroup_views(i, g, 0, end)
+                    nc.scalar.copy(out=dst, in_=src)
 
         newest = [None]
         before_quantise = {}
         token = const.tile([P, 1], F32)
         token_bf = const.tile([P, 1], BF16)
-        junk = const.tile([P, T], BF16)
+        ones = const.tile([P, 1], F32)
+        nc.vector.memset(ones[:], 1.0)
+        folded_sb = {}
 
         def wait_for_vector(n):
             written = before_quantise.get(n, newest[0])
             nc.gpsimd.tensor_copy(out=token_bf[:] if written.dtype == BF16 else token[:], in_=written)
 
         def second_moment_elsewhere(n):
-            b, step = divmod(n - T_TILES, T_TILES)
+            later, step = divmod(n - T_TILES, T_TILES)
+            earlier = later - 1
             ct = C_TILES - 1
-            if step == 3 and 0 <= b < B - 1:
-                part = slice(0, FIRST_PART)
-            elif step == 0 and 1 <= b < B:
-                b -= 1
-                part = slice(FIRST_PART, T)
-            elif step == 2 and 1 <= b < B:
-                b -= 1
-                nc.scalar.activation(
-                    out=junk[:], in_=prod[b, ct][:], func=ACT.Copy, accum_out=sums[:, 1, b, ct : ct + 1]
+
+            def multiply(b, part):
+                wait_for_vector(n)
+                nc.gpsimd.tensor_tensor(
+                    out=prod[b, ct][:, part], in0=prod[b, ct][:, part], in1=x_rows[:, b, ct, part], op=ALU.mult
                 )
-                return
-            else:
-                return
-            wait_for_vector(n)
-            nc.gpsimd.tensor_tensor(
-                out=prod[b, ct][:, part], in0=prod[b, ct][:, part], in1=x_rows[:, b, ct, part], op=ALU.mult
-            )
+
+            if step == 3 and 0 <= later < B - 1:
+                multiply(later, slice(0, FIRST_PART))
+            if step == 0 and 0 <= earlier < B - 1:
+                multiply(earlier, slice(FIRST_PART, T))
+            if step == FOLD_STEP and 0 <= earlier < B - 1:
+                folded = misc_pool.tile([P, P], F32, name="folded", tag="misc")
+                for q in range(T // P):
+                    nc.tensor.matmul(
+                        out=folded[:],
+                        lhsT=prod[earlier, ct][:, q * P : (q + 1) * P],
+                        rhs=ident_f32[:],
+                        is_transpose=True,
+                        start=(q == 0),
+                        stop=(q == T // P - 1),
+                    )
+                folded_sb[earlier] = fold_pool.tile([P, P], F32, name="folded_sb", tag="folded_sb")
+                nc.scalar.copy(out=folded_sb[earlier][:], in_=folded[:])
+            if step == FOLD_STEP + 1 and 0 <= earlier < B - 1:
+                total = misc_pool.tile([P, 1], F32, name="total", tag="misc")
+                nc.tensor.matmul(
+                    out=total[:], lhsT=folded_sb[earlier][:], rhs=ones[:, 0:1], start=True, stop=True
+                )
+                nc.scalar.copy(out=sums[:, 1, earlier, ct : ct + 1], in_=total[:])
 
         def regroup_on_gpsimd(i):
             if i >= TILES or not on_gpsimd(i):
                 return
             wait_for_vector(i - REGROUP_LEAD)
             nc.gpsimd.tensor_scalar(
-                out=grouped[i][:, PASSES - 1],
-                in0=raw[i][:, PASSES - 1].rearrange("p j t -> p t j"),
+                out=grouped[i][:, PASSES - 1, T_TILE - gpsimd_frames(i) :],
+                in0=raw[i][:, PASSES - 1, :, T_TILE - gpsimd_frames(i) :].rearrange("p j t -> p t j"),
                 scalar1=1.0,
                 scalar2=0.0,
                 op0=ALU.mult,
@@ -203,7 +238,7 @@ def tile_attentivestatspool_pb_t_kernel(tc, h, x, mask, w2, b2, g2, be2, out):
         def regroup_on_vector(i):
             if i < 0 or i >= TILES or not on_vector(i):
                 return
-            dst, src = regroup_views(i, PASSES - 1)
+            dst, src = regroup_views(i, PASSES - 1, T_TILE - vector_frames(i), T_TILE)
             nc.vector.tensor_copy(out=dst, in_=src)
             newest[0] = grouped[i][:, PASSES - 1, T_TILE - 1, PACK - 1 :]
 

@@ -192,22 +192,21 @@ def tile_attentivestatspool_pb_t_kernel(tc, h, x, mask, w2, b2, g2, be2, out):
             earlier = later - 1
             ct = C_TILES - 1
 
-            def multiply(b, part):
-                wait_for_vector(n)
+            def multiply(b, part, home):
                 nc.gpsimd.tensor_tensor(
-                    out=prod[b, ct][:, part], in0=prod[b, ct][:, part], in1=x_rows[:, b, ct, part], op=ALU.mult
+                    out=prod[b, home][:, part], in0=prod[b, ct][:, part], in1=x_rows[:, b, ct, part], op=ALU.mult
                 )
 
             if step == 3 and 0 <= later < B - 1:
-                multiply(later, slice(0, FIRST_PART))
+                multiply(later, slice(0, FIRST_PART), ct)
             if step == 0 and 0 <= earlier < B - 1:
-                multiply(earlier, slice(FIRST_PART, T))
+                multiply(earlier, slice(FIRST_PART, T), 0)
             if step == FOLD_STEP and 0 <= earlier < B - 1:
                 folded = misc_pool.tile([P, P], F32, name="folded", tag="misc")
                 for q in range(T // P):
                     nc.tensor.matmul(
                         out=folded[:],
-                        lhsT=prod[earlier, ct][:, q * P : (q + 1) * P],
+                        lhsT=prod[earlier, ct if q * P < FIRST_PART else 0][:, q * P : (q + 1) * P],
                         rhs=ident_f32[:],
                         is_transpose=True,
                         start=(q == 0),

@@ -24,16 +24,18 @@ T_TILES = T // T_TILE
 C_TILES = C // P
 TILES = B * T_TILES
 RUN = 8
+PAD = 16
 MASKED = -1e30
 
 LOAD_LEAD = 2
 REGROUP_LEAD = 2
 GPSIMD_STEPS = (1,)
-FIRST_PART = 512
+FIRST_PART = 0
 VECTOR_STEPS = ()
 W2_AFTER = 0
 FIRST_PIECES = 1
 FOLD_STEP = 2
+SHIFT_FROM = 7
 VECTOR_SHARE = 256
 HEAD_SHARE = 512
 GPSIMD_SHARE = 512
@@ -117,7 +119,8 @@ def tile_attentivestatspool_pb_t_kernel(tc, h, x, mask, w2, b2, g2, be2, out):
         sum_e = const.tile([P, B, C_TILES], F32)
         sums = const.tile([P, 2, B, C_TILES], F32)
 
-        penalty = const.tile([P, B, T], BF16)
+        penalty = const.tile([P, B, T + PAD], BF16)
+        nc.vector.memset(penalty[:, :, T:], 1.0)
         x_rows = const.tile([P, B, C_TILES, T], BF16)
         grouped = {}
         codes = {}
@@ -136,7 +139,7 @@ def tile_attentivestatspool_pb_t_kernel(tc, h, x, mask, w2, b2, g2, be2, out):
                 for g in range(FIRST_PIECES if i == 0 else 0, PASSES):
                     load_piece(i, g)
             if tt == 1 and b < B:
-                nc.sync.dma_start(out=penalty[:, b, :], in_=mask[b, 0, :].partition_broadcast(P))
+                nc.sync.dma_start(out=penalty[:, b, 0:T], in_=mask[b, 0, :].partition_broadcast(P))
             if tt == 1 and 1 <= b <= B:
                 nc.sync.dma_start(
                     out=x_rows[:, b - 1], in_=x[b - 1].rearrange("(ct c) t -> c ct t", c=P)
@@ -197,7 +200,7 @@ def tile_attentivestatspool_pb_t_kernel(tc, h, x, mask, w2, b2, g2, be2, out):
                     out=prod[b, home][:, part], in0=prod[b, ct][:, part], in1=x_rows[:, b, ct, part], op=ALU.mult
                 )
 
-            if step == 3 and 0 <= later < B - 1:
+            if step == 3 and 0 <= later < B - 1 and FIRST_PART > 0:
                 multiply(later, slice(0, FIRST_PART), ct)
             if step == 0 and 0 <= earlier < B - 1:
                 multiply(earlier, slice(FIRST_PART, T), 0)
@@ -224,12 +227,11 @@ def tile_attentivestatspool_pb_t_kernel(tc, h, x, mask, w2, b2, g2, be2, out):
         def regroup_on_gpsimd(i):
             if i >= TILES or not on_gpsimd(i):
                 return
-            wait_for_vector(i - REGROUP_LEAD)
             nc.gpsimd.tensor_scalar(
                 out=grouped[i][:, PASSES - 1, T_TILE - gpsimd_frames(i) :],
                 in0=raw[i][:, PASSES - 1, :, T_TILE - gpsimd_frames(i) :].rearrange("p j t -> p t j"),
                 scalar1=1.0,
-                scalar2=0.0,
+                scalar2=penalty[:, (i - REGROUP_LEAD) // T_TILES, T : T + 1],
                 op0=ALU.mult,
                 op1=ALU.add,
             )
@@ -253,7 +255,7 @@ def tile_attentivestatspool_pb_t_kernel(tc, h, x, mask, w2, b2, g2, be2, out):
                 op0=ALU.is_equal,
                 op1=ALU.mult,
             )
-            newest[0] = penalty[:, b, T - 1 :]
+            newest[0] = penalty[:, b, T : T + 1]
 
         def quantise_and_multiply(i):
             if i < 0 or i >= TILES:
@@ -287,21 +289,30 @@ def tile_attentivestatspool_pb_t_kernel(tc, h, x, mask, w2, b2, g2, be2, out):
                         stop=(g == PASSES - 1),
                     )
 
-        def mask_scores(i):
-            if i < 0 or i >= TILES:
-                return
+        def mask_bank(i, ct):
             b, tt = divmod(i, T_TILES)
             frames = slice(tt * T_TILE, (tt + 1) * T_TILE)
-            if tt == 0:
+            if tt == 0 and ct == 0:
                 scores[b] = score_pool.tile([P, C_TILES, T], F32, name="scores", tag="scores")
-            for ct in range(C_TILES):
-                nc.vector.tensor_tensor(
-                    out=scores[b][:, ct, frames],
-                    in0=banks[i, ct][:],
-                    in1=penalty[:, b, frames],
-                    op=ALU.add,
-                )
-            newest[0] = scores[b][:, C_TILES - 1, (tt + 1) * T_TILE - 1 : (tt + 1) * T_TILE]
+            nc.vector.tensor_tensor(
+                out=scores[b][:, ct, frames],
+                in0=banks[i, ct][:],
+                in1=penalty[:, b, frames],
+                op=ALU.add,
+            )
+            newest[0] = scores[b][:, ct, (tt + 1) * T_TILE - 1 : (tt + 1) * T_TILE]
+
+        def mask_scores(n):
+            turn = n % T_TILES
+            if n < SHIFT_FROM or turn in (1, 2):
+                todo = [(n - 1, 0), (n - 1, 1)]
+            elif turn == 3:
+                todo = []
+            else:
+                todo = [(n - 2, 0), (n - 2, 1), (n - 1, 0), (n - 1, 1)]
+            for i, ct in todo:
+                if 0 <= i < TILES:
+                    mask_bank(i, ct)
 
         def pool_step(k):
             if k < 0 or k >= B * 2 * C_TILES:
@@ -361,7 +372,7 @@ def tile_attentivestatspool_pb_t_kernel(tc, h, x, mask, w2, b2, g2, be2, out):
             second_moment_elsewhere(n)
             if n + 1 < HELPED_TILES:
                 regroup_on_vector(n + 1)
-            mask_scores(n - 1)
+            mask_scores(n)
             pool_step(n - T_TILES)
 
         nc.scalar.activation(out=warm[:], in_=sum_e[:, B - 1, C_TILES - 1 :], func=ACT.Sqrt)

@@ -27,21 +27,19 @@ RUN = 8
 PAD = 16
 MASKED = -1e30
 
-LOAD_LEAD = 2
+LOAD_LEAD = 4
 REGROUP_LEAD = 2
-GPSIMD_STEPS = (1,)
-FIRST_PART = 0
-VECTOR_STEPS = ()
-W2_AFTER = 0
+GPSIMD_EXTRA = ()
+GPSIMD_PEN = (4,)
+GPSIMD_STEP = 2
+VECTOR_AT = (6, 10, 14)
+VECTOR_SHARE = 512
+HEAD_SHARES = {0: (0, 512), 1: (0, 512), 2: (0, 512), 3: (0, 512)}
 FIRST_PIECES = 1
+X_COLS = 1024
+X_PARTS = T // X_COLS
+EXX_CUTS = (0, 900, 2750, 4096)
 FOLD_STEP = 2
-SHIFT_FROM = 7
-VECTOR_SHARE = 256
-HEAD_SHARE = 512
-GPSIMD_SHARE = 512
-GPSIMD_SHORT_STEPS = ()
-GPSIMD_SHORT = 192
-SECOND_PART = 1536
 HELPED_TILES = 4
 
 
@@ -52,10 +50,10 @@ def tile_attentivestatspool_pb_t_kernel(tc, h, x, mask, w2, b2, g2, be2, out):
     ) as raw_pool, tc.tile_pool(name="grouped", bufs=REGROUP_LEAD + 2) as grouped_pool, tc.tile_pool(
         name="codes", bufs=3
     ) as codes_pool, tc.tile_pool(name="scores", bufs=2) as score_pool, tc.tile_pool(
-        name="prod", bufs=4
-    ) as prod_pool, tc.tile_pool(name="fold", bufs=2) as fold_pool, tc.psum_pool(name="banks", bufs=6) as bank_pool, tc.psum_pool(
-        name="misc", bufs=2
-    ) as misc_pool, tc.manual_schedule():
+        name="prod", bufs=2
+    ) as prod_pool, tc.tile_pool(name="fold", bufs=2) as fold_pool, tc.psum_pool(name="banks", bufs=4) as bank_pool, tc.psum_pool(
+        name="xbanks", bufs=2
+    ) as x_pool, tc.psum_pool(name="misc", bufs=2) as misc_pool, tc.manual_schedule():
         ident_bf = const.tile([P, P], BF16)
         make_identity(nc, ident_bf[:])
         ident_f32 = const.tile([P, P], F32)
@@ -118,6 +116,7 @@ def tile_attentivestatspool_pb_t_kernel(tc, h, x, mask, w2, b2, g2, be2, out):
         neg_max = const.tile([P, B, C_TILES], F32)
         sum_e = const.tile([P, B, C_TILES], F32)
         sums = const.tile([P, 2, B, C_TILES], F32)
+        half_sums = const.tile([P, X_PARTS, B - 1, C_TILES], F32)
 
         penalty = const.tile([P, B, T + PAD], BF16)
         nc.vector.memset(penalty[:, :, T:], 1.0)
@@ -127,7 +126,9 @@ def tile_attentivestatspool_pb_t_kernel(tc, h, x, mask, w2, b2, g2, be2, out):
         scales = {}
         banks = {}
         scores = {}
-        prod = {}
+
+        def load_mask(b):
+            nc.sync.dma_start(out=penalty[:, b, 0:T], in_=mask[b, 0, :].partition_broadcast(P))
 
         def load_tile(i):
             if i < 0:
@@ -138,9 +139,11 @@ def tile_attentivestatspool_pb_t_kernel(tc, h, x, mask, w2, b2, g2, be2, out):
                     raw[i] = raw_pool.tile([P, PASSES, PACK, T_TILE], BF16, name="raw", tag="raw")
                 for g in range(FIRST_PIECES if i == 0 else 0, PASSES):
                     load_piece(i, g)
-            if tt == 1 and b < B:
-                nc.sync.dma_start(out=penalty[:, b, 0:T], in_=mask[b, 0, :].partition_broadcast(P))
-            if tt == 1 and 1 <= b <= B:
+            if tt == 1 and b == 0:
+                load_mask(0)
+            if tt == 3 and b + 1 < B:
+                load_mask(b + 1)
+            if tt == 3 and 1 <= b <= B:
                 nc.sync.dma_start(
                     out=x_rows[:, b - 1], in_=x[b - 1].rearrange("(ct c) t -> c ct t", c=P)
                 )
@@ -150,17 +153,17 @@ def tile_attentivestatspool_pb_t_kernel(tc, h, x, mask, w2, b2, g2, be2, out):
             src = raw[i][:, g, :, start:end].rearrange("p j (c r) -> p c j r", r=RUN)
             return dst, src
 
-        def vector_frames(i):
-            return HEAD_SHARE if i < HELPED_TILES else VECTOR_SHARE
+        def vector_frames(i, g):
+            if i in HEAD_SHARES:
+                return HEAD_SHARES[i][g]
+            return VECTOR_SHARE if g == PASSES - 1 else 0
 
         def on_gpsimd(i):
-            return i >= HELPED_TILES + REGROUP_LEAD and (i - REGROUP_LEAD) % T_TILES in GPSIMD_STEPS + GPSIMD_SHORT_STEPS
-
-        def gpsimd_frames(i):
-            return GPSIMD_SHARE if (i - REGROUP_LEAD) % T_TILES in GPSIMD_STEPS else GPSIMD_SHORT
+            n = i - REGROUP_LEAD
+            return i < TILES and (n in GPSIMD_EXTRA + GPSIMD_PEN or n >= HELPED_TILES and n % T_TILES == GPSIMD_STEP)
 
         def on_vector(i):
-            return i < HELPED_TILES or (i - REGROUP_LEAD) % T_TILES in VECTOR_STEPS
+            return i < HELPED_TILES or (VECTOR_SHARE > 0 and i - 1 in VECTOR_AT)
 
         def regroup_on_scalar(i):
             if i < 0 or i >= TILES:
@@ -170,68 +173,100 @@ def tile_attentivestatspool_pb_t_kernel(tc, h, x, mask, w2, b2, g2, be2, out):
             )
             for g in range(PASSES):
                 end = T_TILE
-                if g == PASSES - 1 and on_vector(i):
-                    end = T_TILE - vector_frames(i)
+                if on_vector(i):
+                    end = T_TILE - vector_frames(i, g)
                 if g == PASSES - 1 and on_gpsimd(i):
-                    end = T_TILE - gpsimd_frames(i)
+                    end = 0
                 if end > 0:
                     dst, src = regroup_views(i, g, 0, end)
                     nc.scalar.copy(out=dst, in_=src)
 
-        newest = [None]
-        before_quantise = {}
-        token = const.tile([P, 1], F32)
-        token_bf = const.tile([P, 1], BF16)
         ones = const.tile([P, 1], F32)
         nc.vector.memset(ones[:], 1.0)
         folded_sb = {}
-
-        def wait_for_vector(n):
-            written = before_quantise.get(n, newest[0])
-            nc.gpsimd.tensor_copy(out=token_bf[:] if written.dtype == BF16 else token[:], in_=written)
+        prod = {}
 
         def second_moment_elsewhere(n):
             later, step = divmod(n - T_TILES, T_TILES)
             earlier = later - 1
-            ct = C_TILES - 1
-
-            def multiply(b, part, home):
+            part = {3: 0, 0: 1, 1: 2}.get(step)
+            b = later if step == 3 else earlier
+            if part is not None and 0 <= b < B - 1:
+                cut = slice(EXX_CUTS[part], EXX_CUTS[part + 1])
+                row = prod[b][:].rearrange("p ct t -> p (ct t)")
                 nc.gpsimd.tensor_tensor(
-                    out=prod[b, home][:, part], in0=prod[b, ct][:, part], in1=x_rows[:, b, ct, part], op=ALU.mult
+                    out=row[:, cut],
+                    in0=row[:, cut],
+                    in1=x_rows[:, b].rearrange("p ct t -> p (ct t)")[:, cut],
+                    op=ALU.mult,
                 )
-
-            if step == 3 and 0 <= later < B - 1 and FIRST_PART > 0:
-                multiply(later, slice(0, FIRST_PART), ct)
-            if step == 0 and 0 <= earlier < B - 1:
-                multiply(earlier, slice(FIRST_PART, T), 0)
             if step == FOLD_STEP and 0 <= earlier < B - 1:
-                folded = misc_pool.tile([P, P], F32, name="folded", tag="misc")
-                for q in range(T // P):
-                    nc.tensor.matmul(
-                        out=folded[:],
-                        lhsT=prod[earlier, ct if q * P < FIRST_PART else 0][:, q * P : (q + 1) * P],
-                        rhs=ident_f32[:],
-                        is_transpose=True,
-                        start=(q == 0),
-                        stop=(q == T // P - 1),
-                    )
-                folded_sb[earlier] = fold_pool.tile([P, P], F32, name="folded_sb", tag="folded_sb")
+                folded = misc_pool.tile([P, C_TILES, P], F32, name="folded", tag="misc")
+                for ct in range(C_TILES):
+                    for q in range(T // P):
+                        nc.tensor.matmul(
+                            out=folded[:, ct],
+                            lhsT=prod[earlier][:, ct, q * P : (q + 1) * P],
+                            rhs=ident_f32[:],
+                            is_transpose=True,
+                            start=(q == 0),
+                            stop=(q == T // P - 1),
+                        )
+                folded_sb[earlier] = fold_pool.tile([P, C_TILES, P], F32, name="folded_sb", tag="folded_sb")
                 nc.scalar.copy(out=folded_sb[earlier][:], in_=folded[:])
             if step == FOLD_STEP + 1 and 0 <= earlier < B - 1:
-                total = misc_pool.tile([P, 1], F32, name="total", tag="misc")
+                total = misc_pool.tile([P, C_TILES], F32, name="total", tag="misc")
+                for ct in range(C_TILES):
+                    nc.tensor.matmul(
+                        out=total[:, ct : ct + 1], lhsT=folded_sb[earlier][:, ct], rhs=ones[:, 0:1], start=True, stop=True
+                    )
+                nc.scalar.copy(out=sums[:, 1, earlier], in_=total[:])
+
+        x_banks = {}
+
+        def x_to_psum(b, ct, part):
+            bank = x_pool.tile([P, X_COLS], BF16, name="x_bank", tag="x_bank")
+            for start in range(0, X_COLS, T_TILE):
                 nc.tensor.matmul(
-                    out=total[:], lhsT=folded_sb[earlier][:], rhs=ones[:, 0:1], start=True, stop=True
+                    out=bank[:, start : start + T_TILE],
+                    lhsT=ident_bf[:],
+                    rhs=x_rows[:, b, ct, part * X_COLS + start : part * X_COLS + start + T_TILE],
+                    start=True,
+                    stop=True,
                 )
-                nc.scalar.copy(out=sums[:, 1, earlier, ct : ct + 1], in_=total[:])
+            x_banks[b, ct, part] = bank
+
+        def copy_x(n):
+            b, step = divmod(n - T_TILES, T_TILES)
+            if step == 1 and 0 <= b < B - 1:
+                for part in reversed(range(X_PARTS)):
+                    x_to_psum(b, 0, part)
+            if step == 2 and 0 <= b < B - 1:
+                for part in range(X_PARTS):
+                    x_to_psum(b, 1, part)
+
+        def weigh_half(b, ct, part):
+            if b not in prod:
+                prod[b] = prod_pool.tile([P, C_TILES, T], F32, name="prod", tag="prod")
+            cols = slice(part * X_COLS, (part + 1) * X_COLS)
+            nc.vector.scalar_tensor_tensor(
+                out=prod[b][:, ct, cols],
+                in0=scores[b][:, ct, cols],
+                scalar=1.0,
+                in1=x_banks[b, ct, part][:],
+                op0=ALU.mult,
+                op1=ALU.mult,
+                accum_out=half_sums[:, part, b, ct : ct + 1],
+            )
 
         def regroup_on_gpsimd(i):
             if i >= TILES or not on_gpsimd(i):
                 return
             nc.gpsimd.tensor_scalar(
-                out=grouped[i][:, PASSES - 1, T_TILE - gpsimd_frames(i) :],
-                in0=raw[i][:, PASSES - 1, :, T_TILE - gpsimd_frames(i) :].rearrange("p j t -> p t j"),
+                out=grouped[i][:, PASSES - 1],
+                in0=raw[i][:, PASSES - 1].rearrange("p j t -> p t j"),
                 scalar1=1.0,
-                scalar2=penalty[:, (i - REGROUP_LEAD) // T_TILES, T : T + 1],
+                scalar2=penalty[:, newest_penalty[0], T : T + 1] if i - REGROUP_LEAD not in GPSIMD_EXTRA else zero[i - REGROUP_LEAD][:],
                 op0=ALU.mult,
                 op1=ALU.add,
             )
@@ -239,14 +274,25 @@ def tile_attentivestatspool_pb_t_kernel(tc, h, x, mask, w2, b2, g2, be2, out):
         def regroup_on_vector(i):
             if i < 0 or i >= TILES or not on_vector(i):
                 return
-            dst, src = regroup_views(i, PASSES - 1, T_TILE - vector_frames(i), T_TILE)
-            nc.vector.tensor_copy(out=dst, in_=src)
-            newest[0] = grouped[i][:, PASSES - 1, T_TILE - 1, PACK - 1 :]
+            for g in range(PASSES):
+                if vector_frames(i, g) > 0:
+                    dst, src = regroup_views(i, g, T_TILE - vector_frames(i, g), T_TILE)
+                    nc.vector.tensor_copy(out=dst, in_=src)
+
+        newest_penalty = [0]
+        zero = {n: const.tile([P, 1], BF16, name="zero%d" % n) for n in GPSIMD_EXTRA}
 
         def make_penalty(i):
             b, tt = divmod(i, T_TILES)
-            if tt != 1 or b < 0 or b >= B:
+            if i == 1:
+                b = 0
+            elif i == T_TILES:
+                b = 1
+            elif tt == 2 and 1 <= b < B - 1:
+                b = b + 1
+            else:
                 return
+            newest_penalty[0] = b
             nc.vector.tensor_scalar(
                 out=penalty[:, b, :],
                 in0=penalty[:, b, :],
@@ -255,13 +301,11 @@ def tile_attentivestatspool_pb_t_kernel(tc, h, x, mask, w2, b2, g2, be2, out):
                 op0=ALU.is_equal,
                 op1=ALU.mult,
             )
-            newest[0] = penalty[:, b, T : T + 1]
 
         def quantise_and_multiply(i):
             if i < 0 or i >= TILES:
                 return
             b, tt = divmod(i, T_TILES)
-            before_quantise[i] = newest[0]
             codes[i] = codes_pool.tile(
                 [P, PASSES, T_TILE], U32, name="codes", tag="codes", align_bytes=64
             )
@@ -274,6 +318,7 @@ def tile_attentivestatspool_pb_t_kernel(tc, h, x, mask, w2, b2, g2, be2, out):
                 in_=grouped[i][:].rearrange("p g t j -> p (g t j)"),
             )
             if i == 0:
+                regroup_on_vector(1)
                 quantise_w2()
             for ct in range(C_TILES):
                 channels = slice(ct * P, (ct + 1) * P)
@@ -300,58 +345,62 @@ def tile_attentivestatspool_pb_t_kernel(tc, h, x, mask, w2, b2, g2, be2, out):
                 in1=penalty[:, b, frames],
                 op=ALU.add,
             )
-            newest[0] = scores[b][:, ct, (tt + 1) * T_TILE - 1 : (tt + 1) * T_TILE]
 
         def mask_scores(n):
-            turn = n % T_TILES
-            if n < SHIFT_FROM or turn in (1, 2):
-                todo = [(n - 1, 0), (n - 1, 1)]
-            elif turn == 3:
-                todo = []
-            else:
-                todo = [(n - 2, 0), (n - 2, 1), (n - 1, 0), (n - 1, 1)]
-            for i, ct in todo:
-                if 0 <= i < TILES:
-                    mask_bank(i, ct)
+            if 0 <= n - 1 < TILES:
+                for ct in range(C_TILES):
+                    mask_bank(n - 1, ct)
+
+        def maximum_and_exp(b, ct):
+            row = scores[b][:, ct, :]
+            nc.vector.tensor_reduce(
+                out=neg_max[:, b, ct : ct + 1], in_=row, axis=AXIS.X, op=ALU.max, negate=True
+            )
+            nc.scalar.activation(
+                out=row,
+                in_=row,
+                func=ACT.Exp,
+                bias=neg_max[:, b, ct : ct + 1],
+                accum_out=sum_e[:, b, ct : ct + 1],
+            )
+
+        def weigh_row(b, ct, power):
+            if b not in prod:
+                prod[b] = prod_pool.tile([P, C_TILES, T], F32, name="prod", tag="prod")
+            nc.vector.scalar_tensor_tensor(
+                out=prod[b][:, ct],
+                in0=scores[b][:, ct, :] if power == 0 else prod[b][:, ct],
+                scalar=1.0,
+                in1=x_rows[:, b, ct, :],
+                op0=ALU.mult,
+                op1=ALU.mult,
+                accum_out=sums[:, power, b, ct : ct + 1],
+            )
 
         def pool_step(k):
-            if k < 0 or k >= B * 2 * C_TILES:
-                return
-            b, step = divmod(k, 2 * C_TILES)
-            if step < C_TILES:
-                ct = step
-                row = scores[b][:, ct, :]
-                nc.vector.tensor_reduce(
-                    out=neg_max[:, b, ct : ct + 1], in_=row, axis=AXIS.X, op=ALU.max, negate=True
+            b, step = divmod(k, T_TILES)
+            if step == 0 and 0 <= b < B:
+                maximum_and_exp(b, 0)
+            if step == 0 and 0 <= b - 1 < B - 1:
+                weigh_half(b - 1, 1, 1)
+            if step == 1 and 0 <= b < B:
+                maximum_and_exp(b, 1)
+            if step == 2 and 0 <= b < B - 1:
+                weigh_half(b, 0, 1)
+                weigh_half(b, 0, 0)
+            if step == 3 and 0 <= b < B - 1:
+                weigh_half(b, 1, 0)
+            if step == 2 and b == B - 1:
+                nc.vector.tensor_tensor(
+                    out=sums[:, 0, 0 : B - 1], in0=half_sums[:, 0], in1=half_sums[:, 1], op=ALU.add
                 )
-                newest[0] = neg_max[:, b, ct : ct + 1]
-                nc.scalar.activation(
-                    out=row,
-                    in_=row,
-                    func=ACT.Exp,
-                    bias=neg_max[:, b, ct : ct + 1],
-                    accum_out=sum_e[:, b, ct : ct + 1],
-                )
-                return
-            power = step - C_TILES
-            last_step = power == 1 and b == B - 1
-            if last_step:
+                weigh_row(b, 0, 0)
+                weigh_row(b, 1, 0)
+            if step == 3 and b == B - 1:
                 nc.vector.reciprocal(out=recip[:], in_=sum_e[:])
-            for ct in range(C_TILES - 1 if power == 1 and b < B - 1 else C_TILES):
-                if last_step and ct == C_TILES - 1:
-                    nc.vector.tensor_tensor(out=v[:, 0], in0=sums[:, 0], in1=recip[:], op=ALU.mult)
-                if power == 0:
-                    prod[b, ct] = prod_pool.tile([P, T], F32, name="prod", tag="prod")
-                nc.vector.scalar_tensor_tensor(
-                    out=prod[b, ct][:],
-                    in0=scores[b][:, ct, :] if power == 0 else prod[b, ct][:],
-                    scalar=1.0,
-                    in1=x_rows[:, b, ct, :],
-                    op0=ALU.mult,
-                    op1=ALU.mult,
-                    accum_out=sums[:, power, b, ct : ct + 1],
-                )
-                newest[0] = sums[:, power, b, ct : ct + 1]
+                weigh_row(b, 0, 1)
+                nc.vector.tensor_tensor(out=v[:, 0], in0=sums[:, 0], in1=recip[:], op=ALU.mult)
+                weigh_row(b, 1, 1)
 
         moments = const.tile([P, 2, 2 * B, C_TILES], F32)
         v = moments[:, :, 0:B, :]
@@ -362,18 +411,21 @@ def tile_attentivestatspool_pb_t_kernel(tc, h, x, mask, w2, b2, g2, be2, out):
         for n in range(-REGROUP_LEAD - LOAD_LEAD, TILES + T_TILES):
             load_tile(n + REGROUP_LEAD + LOAD_LEAD)
             regroup_on_scalar(n + REGROUP_LEAD)
-            if n + REGROUP_LEAD == W2_AFTER:
+            if n + REGROUP_LEAD == 0:
                 turn_w2()
-            make_penalty(n)
             if n + 1 >= HELPED_TILES:
                 regroup_on_vector(n + 1)
+            make_penalty(n)
+            if n in GPSIMD_EXTRA:
+                nc.vector.memset(zero[n][:], 0.0)
             quantise_and_multiply(n)
             regroup_on_gpsimd(n + REGROUP_LEAD)
             second_moment_elsewhere(n)
-            if n + 1 < HELPED_TILES:
+            if n + 1 < HELPED_TILES and n != 0:
                 regroup_on_vector(n + 1)
             mask_scores(n)
             pool_step(n - T_TILES)
+            copy_x(n)
 
         nc.scalar.activation(out=warm[:], in_=sum_e[:, B - 1, C_TILES - 1 :], func=ACT.Sqrt)
 

@@ -18,6 +18,7 @@ FLOPS = 2 * B * C * H * T
 P = 128
 PACK = 4
 K_PASS = P * PACK
+PAIRS = PACK // 2
 PASSES = H // K_PASS
 T_TILE = 512
 T_TILES = T // T_TILE
@@ -29,17 +30,32 @@ MASKED = -1e30
 
 LOAD_LEAD = 4
 REGROUP_LEAD = 2
-GPSIMD_EXTRA = ()
-GPSIMD_PEN = (4,)
+GP = {5: 4, 6: 5, 8: 6, 12: 10}
+ZERO_AT = (4,)
+LATE = (4,)
+PEN_AT = {1: 0, 5: 1, 6: 2, 10: 3}
 GPSIMD_STEP = 2
 VECTOR_AT = (6, 10, 14)
 VECTOR_SHARE = 512
-HEAD_SHARES = {0: (0, 512), 1: (0, 512), 2: (0, 512), 3: (0, 512)}
-FIRST_PIECES = 1
+HEAD_SHARES = {0: (256, 256), 1: (0, 512), 2: (0, 512), 3: (0, 512), 11: (0, 512), 15: (0, 512)}
+FIRST_PIECES = 2
 X_COLS = 1024
 X_PARTS = T // X_COLS
-EXX_CUTS = (0, 900, 2750, 4096)
-FOLD_STEP = 2
+EXX_PARTS = {3: (0, 900), 0: (900, 2750), 1: (2750, 4096)}
+LAST_PARTS = {3: (0, 2048), 1: (2048, 4096)}
+FOLD_STEPS = (1, 2)
+MASK_AFTER = {1: 0, 5: 1, 7: 2, 11: 3}
+X_AFTER = {6: 0, 11: 1, 15: 2, 19: 3}
+X_COPIES = {
+    5: ((0, 0, 1), (0, 0, 0), (0, 1, 0)),
+    6: ((0, 1, 1),),
+    8: ((1, 0, 1), (1, 0, 0)),
+    9: ((1, 1, 0),),
+    10: ((1, 1, 1),),
+    12: ((2, 0, 1), (2, 0, 0)),
+    13: ((2, 1, 0),),
+    14: ((2, 1, 1),),
+}
 HELPED_TILES = 4
 
 
@@ -52,8 +68,8 @@ def tile_attentivestatspool_pb_t_kernel(tc, h, x, mask, w2, b2, g2, be2, out):
     ) as codes_pool, tc.tile_pool(name="scores", bufs=2) as score_pool, tc.tile_pool(
         name="prod", bufs=2
     ) as prod_pool, tc.tile_pool(name="fold", bufs=2) as fold_pool, tc.psum_pool(name="banks", bufs=4) as bank_pool, tc.psum_pool(
-        name="xbanks", bufs=2
-    ) as x_pool, tc.psum_pool(name="misc", bufs=2) as misc_pool, tc.manual_schedule():
+        name="xbanks", bufs=3
+    ) as x_pool, tc.psum_pool(name="misc", bufs=1) as misc_pool, tc.manual_schedule():
         ident_bf = const.tile([P, P], BF16)
         make_identity(nc, ident_bf[:])
         ident_f32 = const.tile([P, P], F32)
@@ -87,7 +103,7 @@ def tile_attentivestatspool_pb_t_kernel(tc, h, x, mask, w2, b2, g2, be2, out):
         nc.scalar.dma_start(out=gb_rows[0:4, :], in_=g2.rearrange("(r c) -> r c", c=P))
         nc.scalar.dma_start(out=gb_rows[4:8, :], in_=be2.rearrange("(r c) -> r c", c=P))
         nc.scalar.activation(out=warm[:], in_=warm[:], func=ACT.Exp)
-        w2_by_word = w2_rows[:].rearrange("c ct (g p j) -> c ct g j p", p=P, j=PACK)
+        w2_pairs = w2_rows[:].bitcast(F32).rearrange("c ct (g p u) -> c ct g u p", p=P, u=PAIRS)
         w2_grouped = const.tile([P, PASSES, C_TILES, P, PACK], BF16, align_bytes=64)
         w2_codes = const.tile([P, PASSES, C], U32, align_bytes=64)
         w2_scales = const.tile([P, PASSES, C], U8, align_bytes=64)
@@ -95,13 +111,13 @@ def tile_attentivestatspool_pb_t_kernel(tc, h, x, mask, w2, b2, g2, be2, out):
 
         def turn_w2():
             for g in range(PASSES):
-                w2_t = misc_pool.tile([P, C_TILES, PACK, P], BF16, name="w2_t", tag="misc")
+                w2_t = x_pool.tile([P, C_TILES, PAIRS, P], F32, name="w2_t", tag="x_bank")
                 for ct in range(C_TILES):
-                    for j in range(PACK):
-                        nc.tensor.transpose(
-                            w2_t[:, ct, j, :], w2_by_word[:, ct, g, j, :], ident_bf[:]
-                        )
-                nc.scalar.copy(out=w2_grouped[:, g], in_=w2_t[:].rearrange("p ct j c -> p ct c j"))
+                    for u in range(PAIRS):
+                        nc.tensor.transpose(w2_t[:, ct, u, :], w2_pairs[:, ct, g, u, :], ident_f32[:])
+                nc.scalar.copy(
+                    out=w2_grouped[:, g].bitcast(F32), in_=w2_t[:].rearrange("p ct u c -> p ct c u")
+                )
             gb_t = misc_pool.tile([P, P], BF16, name="gb_t", tag="misc")
             nc.tensor.transpose(gb_t[:], gb_rows[:], ident_bf[:])
             nc.scalar.copy(out=gb[:], in_=gb_t[:, 0:8])
@@ -139,13 +155,11 @@ def tile_attentivestatspool_pb_t_kernel(tc, h, x, mask, w2, b2, g2, be2, out):
                     raw[i] = raw_pool.tile([P, PASSES, PACK, T_TILE], BF16, name="raw", tag="raw")
                 for g in range(FIRST_PIECES if i == 0 else 0, PASSES):
                     load_piece(i, g)
-            if tt == 1 and b == 0:
-                load_mask(0)
-            if tt == 3 and b + 1 < B:
-                load_mask(b + 1)
-            if tt == 3 and 1 <= b <= B:
+            if i in MASK_AFTER:
+                load_mask(MASK_AFTER[i])
+            if i in X_AFTER:
                 nc.sync.dma_start(
-                    out=x_rows[:, b - 1], in_=x[b - 1].rearrange("(ct c) t -> c ct t", c=P)
+                    out=x_rows[:, X_AFTER[i]], in_=x[X_AFTER[i]].rearrange("(ct c) t -> c ct t", c=P)
                 )
 
         def regroup_views(i, g, start=0, end=T_TILE):
@@ -154,16 +168,13 @@ def tile_attentivestatspool_pb_t_kernel(tc, h, x, mask, w2, b2, g2, be2, out):
             return dst, src
 
         def vector_frames(i, g):
-            if i in HEAD_SHARES:
-                return HEAD_SHARES[i][g]
-            return VECTOR_SHARE if g == PASSES - 1 else 0
+            return HEAD_SHARES[i][g]
 
         def on_gpsimd(i):
-            n = i - REGROUP_LEAD
-            return i < TILES and (n in GPSIMD_EXTRA + GPSIMD_PEN or n >= HELPED_TILES and n % T_TILES == GPSIMD_STEP)
+            return i in GP
 
         def on_vector(i):
-            return i < HELPED_TILES or (VECTOR_SHARE > 0 and i - 1 in VECTOR_AT)
+            return i in HEAD_SHARES
 
         def regroup_on_scalar(i):
             if i < 0 or i >= TILES:
@@ -183,16 +194,17 @@ def tile_attentivestatspool_pb_t_kernel(tc, h, x, mask, w2, b2, g2, be2, out):
 
         ones = const.tile([P, 1], F32)
         nc.vector.memset(ones[:], 1.0)
+        folded = {}
         folded_sb = {}
         prod = {}
 
         def second_moment_elsewhere(n):
             later, step = divmod(n - T_TILES, T_TILES)
             earlier = later - 1
-            part = {3: 0, 0: 1, 1: 2}.get(step)
             b = later if step == 3 else earlier
-            if part is not None and 0 <= b < B - 1:
-                cut = slice(EXX_CUTS[part], EXX_CUTS[part + 1])
+            parts = LAST_PARTS if b == B - 2 else EXX_PARTS
+            if step in parts and 0 <= b < B - 1:
+                cut = slice(*parts[step])
                 row = prod[b][:].rearrange("p ct t -> p (ct t)")
                 nc.gpsimd.tensor_tensor(
                     out=row[:, cut],
@@ -200,21 +212,29 @@ def tile_attentivestatspool_pb_t_kernel(tc, h, x, mask, w2, b2, g2, be2, out):
                     in1=x_rows[:, b].rearrange("p ct t -> p (ct t)")[:, cut],
                     op=ALU.mult,
                 )
-            if step == FOLD_STEP and 0 <= earlier < B - 1:
-                folded = misc_pool.tile([P, C_TILES, P], F32, name="folded", tag="misc")
-                for ct in range(C_TILES):
-                    for q in range(T // P):
-                        nc.tensor.matmul(
-                            out=folded[:, ct],
-                            lhsT=prod[earlier][:, ct, q * P : (q + 1) * P],
-                            rhs=ident_f32[:],
-                            is_transpose=True,
-                            start=(q == 0),
-                            stop=(q == T // P - 1),
-                        )
-                folded_sb[earlier] = fold_pool.tile([P, C_TILES, P], F32, name="folded_sb", tag="folded_sb")
-                nc.scalar.copy(out=folded_sb[earlier][:], in_=folded[:])
-            if step == FOLD_STEP + 1 and 0 <= earlier < B - 1:
+        def fold(n):
+            later, step = divmod(n - T_TILES, T_TILES)
+            earlier = later - 1
+            if step in FOLD_STEPS and 0 <= earlier < B - 1:
+                ct = FOLD_STEPS.index(step)
+                if ct == 0:
+                    folded[earlier] = misc_pool.tile([P, C_TILES, P], F32, name="folded", tag="misc")
+                for q in range(T // P):
+                    nc.tensor.matmul(
+                        out=folded[earlier][:, ct],
+                        lhsT=prod[earlier][:, ct, q * P : (q + 1) * P],
+                        rhs=ident_f32[:],
+                        is_transpose=True,
+                        start=(q == 0),
+                        stop=(q == T // P - 1),
+                    )
+                if ct == C_TILES - 1:
+                    folded_sb[earlier] = fold_pool.tile([P, C_TILES, P], F32, name="folded_sb", tag="folded_sb")
+                    nc.scalar.copy(out=folded_sb[earlier][:], in_=folded[earlier][:])
+        def total_of_fold(n):
+            later, step = divmod(n - T_TILES, T_TILES)
+            earlier = later - 1
+            if step == FOLD_STEPS[-1] + 1 and 0 <= earlier < B - 1:
                 total = misc_pool.tile([P, C_TILES], F32, name="total", tag="misc")
                 for ct in range(C_TILES):
                     nc.tensor.matmul(
@@ -237,13 +257,8 @@ def tile_attentivestatspool_pb_t_kernel(tc, h, x, mask, w2, b2, g2, be2, out):
             x_banks[b, ct, part] = bank
 
         def copy_x(n):
-            b, step = divmod(n - T_TILES, T_TILES)
-            if step == 1 and 0 <= b < B - 1:
-                for part in reversed(range(X_PARTS)):
-                    x_to_psum(b, 0, part)
-            if step == 2 and 0 <= b < B - 1:
-                for part in range(X_PARTS):
-                    x_to_psum(b, 1, part)
+            for b, ct, part in X_COPIES.get(n, ()):
+                x_to_psum(b, ct, part)
 
         def weigh_half(b, ct, part):
             if b not in prod:
@@ -260,13 +275,11 @@ def tile_attentivestatspool_pb_t_kernel(tc, h, x, mask, w2, b2, g2, be2, out):
             )
 
         def regroup_on_gpsimd(i):
-            if i >= TILES or not on_gpsimd(i):
-                return
             nc.gpsimd.tensor_scalar(
                 out=grouped[i][:, PASSES - 1],
                 in0=raw[i][:, PASSES - 1].rearrange("p j t -> p t j"),
                 scalar1=1.0,
-                scalar2=penalty[:, newest_penalty[0], T : T + 1] if i - REGROUP_LEAD not in GPSIMD_EXTRA else zero[i - REGROUP_LEAD][:],
+                scalar2=zero[GP[i]][:] if GP[i] in ZERO_AT else penalty[:, newest_penalty[0], T : T + 1],
                 op0=ALU.mult,
                 op1=ALU.add,
             )
@@ -280,18 +293,12 @@ def tile_attentivestatspool_pb_t_kernel(tc, h, x, mask, w2, b2, g2, be2, out):
                     nc.vector.tensor_copy(out=dst, in_=src)
 
         newest_penalty = [0]
-        zero = {n: const.tile([P, 1], BF16, name="zero%d" % n) for n in GPSIMD_EXTRA}
+        zero = {n: const.tile([P, 1], BF16, name="zero%d" % n) for n in ZERO_AT}
 
         def make_penalty(i):
-            b, tt = divmod(i, T_TILES)
-            if i == 1:
-                b = 0
-            elif i == T_TILES:
-                b = 1
-            elif tt == 2 and 1 <= b < B - 1:
-                b = b + 1
-            else:
+            if i not in PEN_AT:
                 return
+            b = PEN_AT[i]
             newest_penalty[0] = b
             nc.vector.tensor_scalar(
                 out=penalty[:, b, :],
@@ -370,7 +377,7 @@ def tile_attentivestatspool_pb_t_kernel(tc, h, x, mask, w2, b2, g2, be2, out):
             nc.vector.scalar_tensor_tensor(
                 out=prod[b][:, ct],
                 in0=scores[b][:, ct, :] if power == 0 else prod[b][:, ct],
-                scalar=1.0,
+                scalar=1.0 if power == 0 else recip[:, b, ct : ct + 1],
                 in1=x_rows[:, b, ct, :],
                 op0=ALU.mult,
                 op1=ALU.mult,
@@ -381,7 +388,7 @@ def tile_attentivestatspool_pb_t_kernel(tc, h, x, mask, w2, b2, g2, be2, out):
             b, step = divmod(k, T_TILES)
             if step == 0 and 0 <= b < B:
                 maximum_and_exp(b, 0)
-            if step == 0 and 0 <= b - 1 < B - 1:
+            if step == 0 and 0 <= b - 1 < B - 2:
                 weigh_half(b - 1, 1, 1)
             if step == 1 and 0 <= b < B:
                 maximum_and_exp(b, 1)
@@ -390,16 +397,21 @@ def tile_attentivestatspool_pb_t_kernel(tc, h, x, mask, w2, b2, g2, be2, out):
                 weigh_half(b, 0, 0)
             if step == 3 and 0 <= b < B - 1:
                 weigh_half(b, 1, 0)
+                if b == B - 2:
+                    weigh_half(b, 1, 1)
             if step == 2 and b == B - 1:
                 nc.vector.tensor_tensor(
                     out=sums[:, 0, 0 : B - 1], in0=half_sums[:, 0], in1=half_sums[:, 1], op=ALU.add
                 )
                 weigh_row(b, 0, 0)
+                nc.vector.reciprocal(out=recip[:], in_=sum_e[:])
                 weigh_row(b, 1, 0)
             if step == 3 and b == B - 1:
-                nc.vector.reciprocal(out=recip[:], in_=sum_e[:])
                 weigh_row(b, 0, 1)
                 nc.vector.tensor_tensor(out=v[:, 0], in0=sums[:, 0], in1=recip[:], op=ALU.mult)
+                nc.vector.tensor_tensor(
+                    out=sums[:, 1, 0 : B - 1], in0=sums[:, 1, 0 : B - 1], in1=recip[:, 0 : B - 1], op=ALU.mult
+                )
                 weigh_row(b, 1, 1)
 
         moments = const.tile([P, 2, 2 * B, C_TILES], F32)
@@ -415,17 +427,29 @@ def tile_attentivestatspool_pb_t_kernel(tc, h, x, mask, w2, b2, g2, be2, out):
                 turn_w2()
             if n + 1 >= HELPED_TILES:
                 regroup_on_vector(n + 1)
-            make_penalty(n)
-            if n in GPSIMD_EXTRA:
-                nc.vector.memset(zero[n][:], 0.0)
+            if n not in LATE:
+                make_penalty(n)
+                if n in ZERO_AT:
+                    nc.vector.memset(zero[n][:], 0.0)
             quantise_and_multiply(n)
-            regroup_on_gpsimd(n + REGROUP_LEAD)
+            if n in LATE:
+                make_penalty(n)
+                if n in ZERO_AT:
+                    nc.vector.memset(zero[n][:], 0.0)
+            if n % T_TILES != 2:
+                copy_x(n)
+            for i in GP:
+                if GP[i] == n:
+                    regroup_on_gpsimd(i)
             second_moment_elsewhere(n)
             if n + 1 < HELPED_TILES and n != 0:
                 regroup_on_vector(n + 1)
             mask_scores(n)
+            total_of_fold(n)
             pool_step(n - T_TILES)
-            copy_x(n)
+            if n % T_TILES == 2:
+                copy_x(n)
+            fold(n)
 
         nc.scalar.activation(out=warm[:], in_=sum_e[:, B - 1, C_TILES - 1 :], func=ACT.Sqrt)
 
@@ -439,8 +463,7 @@ def tile_attentivestatspool_pb_t_kernel(tc, h, x, mask, w2, b2, g2, be2, out):
 
         nc.vector.tensor_tensor(out=v_sq[:, 0], in0=v[:, 0], in1=v[:, 0], op=ALU.mult)
         variance = const.tile([P, B, C_TILES], F32)
-        nc.vector.tensor_tensor(out=variance[:], in0=sums[:, 1], in1=recip[:], op=ALU.mult)
-        nc.vector.tensor_tensor(out=variance[:], in0=variance[:], in1=v_sq[:, 0], op=ALU.subtract)
+        nc.vector.tensor_tensor(out=variance[:], in0=sums[:, 1], in1=v_sq[:, 0], op=ALU.subtract)
         nc.vector.tensor_scalar_max(out=v_sq[:, 1], in0=variance[:], scalar1=EPS_STD)
         nc.scalar.activation(out=v[:, 1], in_=v_sq[:, 1], func=ACT.Sqrt)
         nc.scalar.activation(out=warm[:], in_=warm[:], func=ACT.Abs_reciprocal_sqrt)

@@ -25,35 +25,39 @@ T_TILES = T // T_TILE
 C_TILES = C // P
 TILES = B * T_TILES
 RUN = 8
-PAD = 16
-MASKED = -1e30
+W2_SCALE = 2.0**-40
 
 LOAD_LEAD = 4
 REGROUP_LEAD = 2
 GP = {5: 4, 6: 5, 8: 6, 12: 10}
-ZERO_AT = (4,)
-LATE = (4,)
-PEN_AT = {1: 0, 5: 1, 6: 2, 10: 3}
+GSHARE = {5: 448, 6: 448, 8: 448, 12: 448}
+V_EXX = {0: (2560, 3072), 1: (2560, 3072), 2: (3584, 4096)}
+ZERO_AT = (4, 5, 6, 10)
+LATE = (4, 5)
 GPSIMD_STEP = 2
 VECTOR_AT = (6, 10, 14)
 VECTOR_SHARE = 512
-HEAD_SHARES = {0: (256, 256), 1: (0, 512), 2: (0, 512), 3: (0, 512), 11: (0, 512), 15: (0, 512)}
+HEAD_SHARES = {0: (256, 256), 1: (256, 512), 2: (0, 512), 3: (0, 512), 7: (0, 256), 11: (0, 512)}
 FIRST_PIECES = 2
 X_COLS = 1024
 X_PARTS = T // X_COLS
-EXX_PARTS = {3: (0, 900), 0: (900, 2750), 1: (2750, 4096)}
-LAST_PARTS = {3: (0, 2048), 1: (2048, 4096)}
+EXX_PARTS = {3: (0, 750), 0: (750, 2560), 1: (3072, 4096)}
+LAST_PARTS = {3: (0, 2048), 1: (2048, 3584)}
 FOLD_STEPS = (1, 2)
 MASK_AFTER = {1: 0, 5: 1, 7: 2, 11: 3}
 X_AFTER = {6: 0, 11: 1, 15: 2, 19: 3}
 X_COPIES = {
     5: ((0, 0, 1), (0, 0, 0), (0, 1, 0)),
-    6: ((0, 1, 1),),
-    8: ((1, 0, 1), (1, 0, 0)),
+    8: ((1, 0, 1),),
     9: ((1, 1, 0),),
-    10: ((1, 1, 1),),
-    12: ((2, 0, 1), (2, 0, 0)),
+    12: ((2, 0, 1),),
     13: ((2, 1, 0),),
+}
+X_COPIES_LATE = {
+    6: ((0, 1, 1),),
+    8: ((1, 0, 0),),
+    10: ((1, 1, 1),),
+    12: ((2, 0, 0),),
     14: ((2, 1, 1),),
 }
 HELPED_TILES = 4
@@ -133,9 +137,9 @@ def tile_attentivestatspool_pb_t_kernel(tc, h, x, mask, w2, b2, g2, be2, out):
         sum_e = const.tile([P, B, C_TILES], F32)
         sums = const.tile([P, 2, B, C_TILES], F32)
         half_sums = const.tile([P, X_PARTS, B - 1, C_TILES], F32)
+        last_sums = const.tile([P, B - 1], F32)
 
-        penalty = const.tile([P, B, T + PAD], BF16)
-        nc.vector.memset(penalty[:, :, T:], 1.0)
+        mask_rows = const.tile([P, B, T], BF16)
         x_rows = const.tile([P, B, C_TILES, T], BF16)
         grouped = {}
         codes = {}
@@ -144,7 +148,7 @@ def tile_attentivestatspool_pb_t_kernel(tc, h, x, mask, w2, b2, g2, be2, out):
         scores = {}
 
         def load_mask(b):
-            nc.sync.dma_start(out=penalty[:, b, 0:T], in_=mask[b, 0, :].partition_broadcast(P))
+            nc.sync.dma_start(out=mask_rows[:, b], in_=mask[b, 0, :].partition_broadcast(P))
 
         def load_tile(i):
             if i < 0:
@@ -187,7 +191,7 @@ def tile_attentivestatspool_pb_t_kernel(tc, h, x, mask, w2, b2, g2, be2, out):
                 if on_vector(i):
                     end = T_TILE - vector_frames(i, g)
                 if g == PASSES - 1 and on_gpsimd(i):
-                    end = 0
+                    end = T_TILE - GSHARE[i]
                 if end > 0:
                     dst, src = regroup_views(i, g, 0, end)
                     nc.scalar.copy(out=dst, in_=src)
@@ -219,14 +223,17 @@ def tile_attentivestatspool_pb_t_kernel(tc, h, x, mask, w2, b2, g2, be2, out):
                 ct = FOLD_STEPS.index(step)
                 if ct == 0:
                     folded[earlier] = misc_pool.tile([P, C_TILES, P], F32, name="folded", tag="misc")
-                for q in range(T // P):
+                chunks = [
+                    q for q in range(T // P) if not V_EXX[earlier][0] <= ct * T + q * P < V_EXX[earlier][1]
+                ]
+                for q in chunks:
                     nc.tensor.matmul(
                         out=folded[earlier][:, ct],
                         lhsT=prod[earlier][:, ct, q * P : (q + 1) * P],
                         rhs=ident_f32[:],
                         is_transpose=True,
-                        start=(q == 0),
-                        stop=(q == T // P - 1),
+                        start=(q == chunks[0]),
+                        stop=(q == chunks[-1]),
                     )
                 if ct == C_TILES - 1:
                     folded_sb[earlier] = fold_pool.tile([P, C_TILES, P], F32, name="folded_sb", tag="folded_sb")
@@ -256,8 +263,8 @@ def tile_attentivestatspool_pb_t_kernel(tc, h, x, mask, w2, b2, g2, be2, out):
                 )
             x_banks[b, ct, part] = bank
 
-        def copy_x(n):
-            for b, ct, part in X_COPIES.get(n, ()):
+        def copy_x(copies):
+            for b, ct, part in copies:
                 x_to_psum(b, ct, part)
 
         def weigh_half(b, ct, part):
@@ -276,10 +283,10 @@ def tile_attentivestatspool_pb_t_kernel(tc, h, x, mask, w2, b2, g2, be2, out):
 
         def regroup_on_gpsimd(i):
             nc.gpsimd.tensor_scalar(
-                out=grouped[i][:, PASSES - 1],
-                in0=raw[i][:, PASSES - 1].rearrange("p j t -> p t j"),
+                out=grouped[i][:, PASSES - 1, T_TILE - GSHARE[i] :],
+                in0=raw[i][:, PASSES - 1, :, T_TILE - GSHARE[i] :].rearrange("p j t -> p t j"),
                 scalar1=1.0,
-                scalar2=zero[GP[i]][:] if GP[i] in ZERO_AT else penalty[:, newest_penalty[0], T : T + 1],
+                scalar2=zero[GP[i]][:],
                 op0=ALU.mult,
                 op1=ALU.add,
             )
@@ -292,22 +299,7 @@ def tile_attentivestatspool_pb_t_kernel(tc, h, x, mask, w2, b2, g2, be2, out):
                     dst, src = regroup_views(i, g, T_TILE - vector_frames(i, g), T_TILE)
                     nc.vector.tensor_copy(out=dst, in_=src)
 
-        newest_penalty = [0]
         zero = {n: const.tile([P, 1], BF16, name="zero%d" % n) for n in ZERO_AT}
-
-        def make_penalty(i):
-            if i not in PEN_AT:
-                return
-            b = PEN_AT[i]
-            newest_penalty[0] = b
-            nc.vector.tensor_scalar(
-                out=penalty[:, b, :],
-                in0=penalty[:, b, :],
-                scalar1=0.0,
-                scalar2=MASKED,
-                op0=ALU.is_equal,
-                op1=ALU.mult,
-            )
 
         def quantise_and_multiply(i):
             if i < 0 or i >= TILES:
@@ -346,11 +338,26 @@ def tile_attentivestatspool_pb_t_kernel(tc, h, x, mask, w2, b2, g2, be2, out):
             frames = slice(tt * T_TILE, (tt + 1) * T_TILE)
             if tt == 0 and ct == 0:
                 scores[b] = score_pool.tile([P, C_TILES, T], F32, name="scores", tag="scores")
-            nc.vector.tensor_tensor(
+            nc.vector.scalar_tensor_tensor(
                 out=scores[b][:, ct, frames],
-                in0=banks[i, ct][:],
-                in1=penalty[:, b, frames],
-                op=ALU.add,
+                in0=mask_rows[:, b, frames],
+                scalar=0.0,
+                in1=banks[i, ct][:],
+                op0=ALU.is_equal,
+                op1=ALU.subtract,
+            )
+
+        def square_half(b):
+            start, end = (t - T for t in V_EXX[b])
+            part, first = divmod(start, X_COLS)
+            nc.vector.scalar_tensor_tensor(
+                out=prod[b][:, 1, start:end],
+                in0=prod[b][:, 1, start:end],
+                scalar=1.0,
+                in1=x_banks[b, 1, part][:, first : first + end - start],
+                op0=ALU.mult,
+                op1=ALU.mult,
+                accum_out=last_sums[:, b : b + 1],
             )
 
         def mask_scores(n):
@@ -360,14 +367,21 @@ def tile_attentivestatspool_pb_t_kernel(tc, h, x, mask, w2, b2, g2, be2, out):
 
         def maximum_and_exp(b, ct):
             row = scores[b][:, ct, :]
-            nc.vector.tensor_reduce(
-                out=neg_max[:, b, ct : ct + 1], in_=row, axis=AXIS.X, op=ALU.max, negate=True
+            nc.vector.tensor_scalar(
+                out=row,
+                in0=row,
+                scalar1=1.0 / W2_SCALE,
+                scalar2=None,
+                op0=ALU.mult,
+                op1=ALU.min,
+                accum_out=neg_max[:, b, ct : ct + 1],
             )
             nc.scalar.activation(
                 out=row,
                 in_=row,
                 func=ACT.Exp,
                 bias=neg_max[:, b, ct : ct + 1],
+                scale=-1.0,
                 accum_out=sum_e[:, b, ct : ct + 1],
             )
 
@@ -389,9 +403,12 @@ def tile_attentivestatspool_pb_t_kernel(tc, h, x, mask, w2, b2, g2, be2, out):
             if step == 0 and 0 <= b < B:
                 maximum_and_exp(b, 0)
             if step == 0 and 0 <= b - 1 < B - 2:
+                square_half(b - 1)
                 weigh_half(b - 1, 1, 1)
             if step == 1 and 0 <= b < B:
                 maximum_and_exp(b, 1)
+            if step == 1 and b == B - 1:
+                square_half(b - 1)
             if step == 2 and 0 <= b < B - 1:
                 weigh_half(b, 0, 1)
                 weigh_half(b, 0, 0)
@@ -410,6 +427,12 @@ def tile_attentivestatspool_pb_t_kernel(tc, h, x, mask, w2, b2, g2, be2, out):
                 weigh_row(b, 0, 1)
                 nc.vector.tensor_tensor(out=v[:, 0], in0=sums[:, 0], in1=recip[:], op=ALU.mult)
                 nc.vector.tensor_tensor(
+                    out=sums[:, 1, 0 : B - 1, C_TILES - 1],
+                    in0=sums[:, 1, 0 : B - 1, C_TILES - 1],
+                    in1=last_sums[:],
+                    op=ALU.add,
+                )
+                nc.vector.tensor_tensor(
                     out=sums[:, 1, 0 : B - 1], in0=sums[:, 1, 0 : B - 1], in1=recip[:, 0 : B - 1], op=ALU.mult
                 )
                 weigh_row(b, 1, 1)
@@ -422,33 +445,31 @@ def tile_attentivestatspool_pb_t_kernel(tc, h, x, mask, w2, b2, g2, be2, out):
         assert 2 * C_TILES == T_TILES
         for n in range(-REGROUP_LEAD - LOAD_LEAD, TILES + T_TILES):
             load_tile(n + REGROUP_LEAD + LOAD_LEAD)
-            regroup_on_scalar(n + REGROUP_LEAD)
-            if n + REGROUP_LEAD == 0:
+            if n + 1 == 0:
+                regroup_on_vector(0)
+                nc.vector.tensor_scalar(
+                    out=w2_rows[:], in0=w2_rows[:], scalar1=W2_SCALE, scalar2=None, op0=ALU.mult
+                )
                 turn_w2()
+            regroup_on_scalar(n + REGROUP_LEAD)
             if n + 1 >= HELPED_TILES:
                 regroup_on_vector(n + 1)
-            if n not in LATE:
-                make_penalty(n)
-                if n in ZERO_AT:
-                    nc.vector.memset(zero[n][:], 0.0)
+            if n in ZERO_AT and n not in LATE:
+                nc.vector.memset(zero[n][:], 0.0)
             quantise_and_multiply(n)
             if n in LATE:
-                make_penalty(n)
-                if n in ZERO_AT:
-                    nc.vector.memset(zero[n][:], 0.0)
-            if n % T_TILES != 2:
-                copy_x(n)
+                nc.vector.memset(zero[n][:], 0.0)
+            copy_x(X_COPIES.get(n, ()))
             for i in GP:
                 if GP[i] == n:
                     regroup_on_gpsimd(i)
             second_moment_elsewhere(n)
-            if n + 1 < HELPED_TILES and n != 0:
+            if n > 0 and n + 1 < HELPED_TILES:
                 regroup_on_vector(n + 1)
             mask_scores(n)
             total_of_fold(n)
             pool_step(n - T_TILES)
-            if n % T_TILES == 2:
-                copy_x(n)
+            copy_x(X_COPIES_LATE.get(n, ()))
             fold(n)
 
         nc.scalar.activation(out=warm[:], in_=sum_e[:, B - 1, C_TILES - 1 :], func=ACT.Sqrt)

@@ -25,7 +25,8 @@ T_TILES = T // T_TILE
 C_TILES = C // P
 TILES = B * T_TILES
 RUN = 8
-W2_SCALE = 2.0**-40
+MASKED = -1e30
+PEN_AT = {1: 0, 5: 1, 6: 2, 10: 3}
 
 LOAD_LEAD = 4
 REGROUP_LEAD = 2
@@ -301,6 +302,17 @@ def tile_attentivestatspool_pb_t_kernel(tc, h, x, mask, w2, b2, g2, be2, out):
 
         zero = {n: const.tile([P, 1], BF16, name="zero%d" % n) for n in ZERO_AT}
 
+        def make_penalty(n):
+            b = PEN_AT[n]
+            nc.vector.tensor_scalar(
+                out=mask_rows[:, b],
+                in0=mask_rows[:, b],
+                scalar1=0.0,
+                scalar2=MASKED,
+                op0=ALU.is_equal,
+                op1=ALU.mult,
+            )
+
         def quantise_and_multiply(i):
             if i < 0 or i >= TILES:
                 return
@@ -338,13 +350,11 @@ def tile_attentivestatspool_pb_t_kernel(tc, h, x, mask, w2, b2, g2, be2, out):
             frames = slice(tt * T_TILE, (tt + 1) * T_TILE)
             if tt == 0 and ct == 0:
                 scores[b] = score_pool.tile([P, C_TILES, T], F32, name="scores", tag="scores")
-            nc.vector.scalar_tensor_tensor(
+            nc.vector.tensor_tensor(
                 out=scores[b][:, ct, frames],
-                in0=mask_rows[:, b, frames],
-                scalar=0.0,
-                in1=banks[i, ct][:],
-                op0=ALU.is_equal,
-                op1=ALU.subtract,
+                in0=banks[i, ct][:],
+                in1=mask_rows[:, b, frames],
+                op=ALU.add,
             )
 
         def square_half(b):
@@ -367,21 +377,14 @@ def tile_attentivestatspool_pb_t_kernel(tc, h, x, mask, w2, b2, g2, be2, out):
 
         def maximum_and_exp(b, ct):
             row = scores[b][:, ct, :]
-            nc.vector.tensor_scalar(
-                out=row,
-                in0=row,
-                scalar1=1.0 / W2_SCALE,
-                scalar2=None,
-                op0=ALU.mult,
-                op1=ALU.min,
-                accum_out=neg_max[:, b, ct : ct + 1],
+            nc.vector.tensor_reduce(
+                out=neg_max[:, b, ct : ct + 1], in_=row, axis=AXIS.X, op=ALU.max, negate=True
             )
             nc.scalar.activation(
                 out=row,
                 in_=row,
                 func=ACT.Exp,
                 bias=neg_max[:, b, ct : ct + 1],
-                scale=-1.0,
                 accum_out=sum_e[:, b, ct : ct + 1],
             )
 
@@ -447,17 +450,18 @@ def tile_attentivestatspool_pb_t_kernel(tc, h, x, mask, w2, b2, g2, be2, out):
             load_tile(n + REGROUP_LEAD + LOAD_LEAD)
             if n + 1 == 0:
                 regroup_on_vector(0)
-                nc.vector.tensor_scalar(
-                    out=w2_rows[:], in0=w2_rows[:], scalar1=W2_SCALE, scalar2=None, op0=ALU.mult
-                )
                 turn_w2()
             regroup_on_scalar(n + REGROUP_LEAD)
             if n + 1 >= HELPED_TILES:
                 regroup_on_vector(n + 1)
+            if n in PEN_AT and n not in LATE:
+                make_penalty(n)
             if n in ZERO_AT and n not in LATE:
                 nc.vector.memset(zero[n][:], 0.0)
             quantise_and_multiply(n)
             if n in LATE:
+                if n in PEN_AT:
+                    make_penalty(n)
                 nc.vector.memset(zero[n][:], 0.0)
             copy_x(X_COPIES.get(n, ()))
             for i in GP:

@@ -26,27 +26,27 @@ C_TILES = C // P
 TILES = B * T_TILES
 RUN = 8
 MASKED = -1e30
-PEN_AT = {1: 0, 5: 1, 6: 2, 10: 3}
 
 LOAD_LEAD = 4
 REGROUP_LEAD = 2
 GP = {5: 4, 6: 5, 8: 6, 12: 10}
 GSHARE = {5: 448, 6: 448, 8: 448, 12: 448}
-V_EXX = {0: (2560, 3072), 1: (2560, 3072), 2: (3584, 4096)}
+V_EXX = {0: (2816, 3072), 1: (2816, 3072), 2: (0, 0)}
 ZERO_AT = (4, 5, 6, 10)
 LATE = (4, 5)
 GPSIMD_STEP = 2
 VECTOR_AT = (6, 10, 14)
 VECTOR_SHARE = 512
-HEAD_SHARES = {0: (256, 256), 1: (256, 512), 2: (0, 512), 3: (0, 512), 7: (0, 256), 11: (0, 512)}
+HEAD_SHARES = {0: (256, 256), 1: (256, 512), 2: (256, 512), 3: (256, 512), 7: (0, 256), 11: (0, 256)}
 FIRST_PIECES = 2
 X_COLS = 1024
 X_PARTS = T // X_COLS
-EXX_PARTS = {3: (0, 750), 0: (750, 2560), 1: (3072, 4096)}
-LAST_PARTS = {3: (0, 2048), 1: (2048, 3584)}
+EXX_PARTS = {3: (0, 896), 0: (896, 2816), 1: (3072, 4096)}
+LAST_PARTS = {3: (0, 2048), 1: (2048, 4096)}
+G_LAST = 1152
 FOLD_STEPS = (1, 2)
-MASK_AFTER = {1: 0, 5: 1, 7: 2, 11: 3}
-X_AFTER = {6: 0, 11: 1, 15: 2, 19: 3}
+X_AFTER = {6: 0, 11: 1, 13: 2, 15: 3}
+SPREAD = {0: ((1, 0), (1, 1)), 1: ((2, 0), (2, 1)), 2: ((3, 0), (3, 1))}
 X_COPIES = {
     5: ((0, 0, 1), (0, 0, 0), (0, 1, 0)),
     8: ((1, 0, 1),),
@@ -85,6 +85,8 @@ def tile_attentivestatspool_pb_t_kernel(tc, h, x, mask, w2, b2, g2, be2, out):
         nc.vector.memset(y_pad[:], 0.0)
         gb_rows = const.tile([P, P], BF16)
         nc.vector.memset(gb_rows[:], 0.0)
+        mask_rows = const.tile([P, P], BF16)
+        nc.vector.memset(mask_rows[:], 0.0)
         warm = const.tile([P, 1], F32)
         nc.vector.memset(warm[:], 0.0)
 
@@ -105,6 +107,7 @@ def tile_attentivestatspool_pb_t_kernel(tc, h, x, mask, w2, b2, g2, be2, out):
 
         w2_rows = const.tile([P, C_TILES, H], BF16)
         nc.sync.dma_start(out=w2_rows[:], in_=w2.rearrange("(ct c) k -> c ct k", c=P))
+        nc.scalar.dma_start(out=mask_rows[0 : B * T // P, :], in_=mask.rearrange("b o (q t) -> (b o q) t", t=P))
         nc.scalar.dma_start(out=gb_rows[0:4, :], in_=g2.rearrange("(r c) -> r c", c=P))
         nc.scalar.dma_start(out=gb_rows[4:8, :], in_=be2.rearrange("(r c) -> r c", c=P))
         nc.scalar.activation(out=warm[:], in_=warm[:], func=ACT.Exp)
@@ -137,19 +140,18 @@ def tile_attentivestatspool_pb_t_kernel(tc, h, x, mask, w2, b2, g2, be2, out):
         neg_max = const.tile([P, B, C_TILES], F32)
         sum_e = const.tile([P, B, C_TILES], F32)
         sums = const.tile([P, 2, B, C_TILES], F32)
-        half_sums = const.tile([P, X_PARTS, B - 1, C_TILES], F32)
-        last_sums = const.tile([P, B - 1], F32)
+        half_sums = const.tile([P, X_PARTS, B, C_TILES], F32)
+        last_sums = const.tile([P, B - 2], F32)
+        last_second = const.tile([P, 2, C_TILES], F32)
 
-        mask_rows = const.tile([P, B, T], BF16)
+        penalty = const.tile([P, B, T], BF16)
+        penalty_cols = const.tile([P, B * T // P], BF16)
         x_rows = const.tile([P, B, C_TILES, T], BF16)
         grouped = {}
         codes = {}
         scales = {}
         banks = {}
         scores = {}
-
-        def load_mask(b):
-            nc.sync.dma_start(out=mask_rows[:, b], in_=mask[b, 0, :].partition_broadcast(P))
 
         def load_tile(i):
             if i < 0:
@@ -160,8 +162,6 @@ def tile_attentivestatspool_pb_t_kernel(tc, h, x, mask, w2, b2, g2, be2, out):
                     raw[i] = raw_pool.tile([P, PASSES, PACK, T_TILE], BF16, name="raw", tag="raw")
                 for g in range(FIRST_PIECES if i == 0 else 0, PASSES):
                     load_piece(i, g)
-            if i in MASK_AFTER:
-                load_mask(MASK_AFTER[i])
             if i in X_AFTER:
                 nc.sync.dma_start(
                     out=x_rows[:, X_AFTER[i]], in_=x[X_AFTER[i]].rearrange("(ct c) t -> c ct t", c=P)
@@ -239,6 +239,25 @@ def tile_attentivestatspool_pb_t_kernel(tc, h, x, mask, w2, b2, g2, be2, out):
                 if ct == C_TILES - 1:
                     folded_sb[earlier] = fold_pool.tile([P, C_TILES, P], F32, name="folded_sb", tag="folded_sb")
                     nc.scalar.copy(out=folded_sb[earlier][:], in_=folded[earlier][:])
+        def fold_last():
+            tile_f = misc_pool.tile([P, P], F32, name="folded", tag="misc")
+            for q in range(G_LAST // P):
+                nc.tensor.matmul(
+                    out=tile_f[:],
+                    lhsT=prod[B - 1][:, 0, q * P : (q + 1) * P],
+                    rhs=ident_f32[:],
+                    is_transpose=True,
+                    start=(q == 0),
+                    stop=(q == G_LAST // P - 1),
+                )
+            tile_sb = fold_pool.tile([P, C_TILES, P], F32, name="folded_sb", tag="folded_sb")
+            nc.scalar.copy(out=tile_sb[:, 0], in_=tile_f[:])
+            total = misc_pool.tile([P, 1], F32, name="total", tag="misc")
+            nc.tensor.matmul(out=total[:], lhsT=tile_sb[:, 0], rhs=ones[:, 0:1], start=True, stop=True)
+            nc.scalar.activation(
+                out=last_second[:, 1, 0:1], in_=total[:], func=ACT.Copy, scale=recip[:, B - 1, 0:1]
+            )
+
         def total_of_fold(n):
             later, step = divmod(n - T_TILES, T_TILES)
             earlier = later - 1
@@ -263,6 +282,25 @@ def tile_attentivestatspool_pb_t_kernel(tc, h, x, mask, w2, b2, g2, be2, out):
                     stop=True,
                 )
             x_banks[b, ct, part] = bank
+
+        x_turned = const.tile([P, C_TILES, X_PARTS, X_COLS], BF16)
+
+        def turn_x(ct, part):
+            bank = x_pool.tile([P, X_COLS], BF16, name="x_bank", tag="x_bank")
+            for start in range(0, X_COLS, P):
+                first = part * X_COLS + start
+                nc.tensor.transpose(
+                    bank[:, start : start + P], x_rows[:, B - 1, ct, first : first + P], ident_bf[:]
+                )
+            nc.scalar.copy(out=x_turned[:, ct, part], in_=bank[:])
+
+        def turn_x_back(ct, part):
+            bank = bank_pool.tile([P, X_COLS], BF16, name="bank", tag="bank")
+            for start in range(0, X_COLS, P):
+                nc.tensor.transpose(
+                    bank[:, start : start + P], x_turned[:, ct, part, start : start + P], ident_bf[:]
+                )
+            x_banks[B - 1, ct, part] = bank
 
         def copy_x(copies):
             for b, ct, part in copies:
@@ -302,16 +340,29 @@ def tile_attentivestatspool_pb_t_kernel(tc, h, x, mask, w2, b2, g2, be2, out):
 
         zero = {n: const.tile([P, 1], BF16, name="zero%d" % n) for n in ZERO_AT}
 
-        def make_penalty(n):
-            b = PEN_AT[n]
+        def turn_mask():
+            mask_t = misc_pool.tile([P, P], BF16, name="mask_t", tag="misc")
+            nc.tensor.transpose(mask_t[:], mask_rows[:], ident_bf[:])
             nc.vector.tensor_scalar(
-                out=mask_rows[:, b],
-                in0=mask_rows[:, b],
+                out=penalty_cols[:],
+                in0=mask_t[:, 0 : B * T // P],
                 scalar1=0.0,
                 scalar2=MASKED,
                 op0=ALU.is_equal,
                 op1=ALU.mult,
             )
+
+        def spread_penalty(b, part):
+            if True:
+                bank = x_pool.tile([P, X_COLS], BF16, name="penalty_bank", tag="x_bank")
+                for q in range(X_COLS // P):
+                    col = (b * T + part * X_COLS) // P + q
+                    nc.tensor.transpose(
+                        bank[:, q * P : (q + 1) * P],
+                        penalty_cols[:, col : col + 1].to_broadcast([P, P]),
+                        ident_bf[:],
+                    )
+                nc.scalar.copy(out=penalty[:, b, part * X_COLS : (part + 1) * X_COLS], in_=bank[:])
 
         def quantise_and_multiply(i):
             if i < 0 or i >= TILES:
@@ -353,7 +404,7 @@ def tile_attentivestatspool_pb_t_kernel(tc, h, x, mask, w2, b2, g2, be2, out):
             nc.vector.tensor_tensor(
                 out=scores[b][:, ct, frames],
                 in0=banks[i, ct][:],
-                in1=mask_rows[:, b, frames],
+                in1=penalty[:, b, frames],
                 op=ALU.add,
             )
 
@@ -388,17 +439,18 @@ def tile_attentivestatspool_pb_t_kernel(tc, h, x, mask, w2, b2, g2, be2, out):
                 accum_out=sum_e[:, b, ct : ct + 1],
             )
 
-        def weigh_row(b, ct, power):
-            if b not in prod:
-                prod[b] = prod_pool.tile([P, C_TILES, T], F32, name="prod", tag="prod")
+        def square_last(ct, part, first, slot):
+            b = B - 1
+            start = part * X_COLS + first
+            end = (part + 1) * X_COLS
             nc.vector.scalar_tensor_tensor(
-                out=prod[b][:, ct],
-                in0=scores[b][:, ct, :] if power == 0 else prod[b][:, ct],
-                scalar=1.0 if power == 0 else recip[:, b, ct : ct + 1],
-                in1=x_rows[:, b, ct, :],
+                out=prod[b][:, ct, start:end],
+                in0=prod[b][:, ct, start:end],
+                scalar=recip[:, b, ct : ct + 1],
+                in1=x_banks[b, ct, part][:, first:],
                 op0=ALU.mult,
                 op1=ALU.mult,
-                accum_out=sums[:, power, b, ct : ct + 1],
+                accum_out=last_second[:, slot, ct : ct + 1],
             )
 
         def pool_step(k):
@@ -410,8 +462,6 @@ def tile_attentivestatspool_pb_t_kernel(tc, h, x, mask, w2, b2, g2, be2, out):
                 weigh_half(b - 1, 1, 1)
             if step == 1 and 0 <= b < B:
                 maximum_and_exp(b, 1)
-            if step == 1 and b == B - 1:
-                square_half(b - 1)
             if step == 2 and 0 <= b < B - 1:
                 weigh_half(b, 0, 1)
                 weigh_half(b, 0, 0)
@@ -420,25 +470,32 @@ def tile_attentivestatspool_pb_t_kernel(tc, h, x, mask, w2, b2, g2, be2, out):
                 if b == B - 2:
                     weigh_half(b, 1, 1)
             if step == 2 and b == B - 1:
-                nc.vector.tensor_tensor(
-                    out=sums[:, 0, 0 : B - 1], in0=half_sums[:, 0], in1=half_sums[:, 1], op=ALU.add
+                weigh_half(b, 0, 0)
+                weigh_half(b, 0, 1)
+                nc.gpsimd.tensor_tensor(
+                    out=prod[b][:, 0, 0:G_LAST],
+                    in0=prod[b][:, 0, 0:G_LAST],
+                    in1=x_rows[:, b, 0, 0:G_LAST],
+                    op=ALU.mult,
                 )
-                weigh_row(b, 0, 0)
                 nc.vector.reciprocal(out=recip[:], in_=sum_e[:])
-                weigh_row(b, 1, 0)
+                weigh_half(b, 1, 0)
+                weigh_half(b, 1, 1)
             if step == 3 and b == B - 1:
-                weigh_row(b, 0, 1)
-                nc.vector.tensor_tensor(out=v[:, 0], in0=sums[:, 0], in1=recip[:], op=ALU.mult)
+                square_last(0, G_LAST // X_COLS, G_LAST % X_COLS, 0)
+                nc.vector.tensor_tensor(out=sums[:, 0], in0=half_sums[:, 0], in1=half_sums[:, 1], op=ALU.add)
                 nc.vector.tensor_tensor(
-                    out=sums[:, 1, 0 : B - 1, C_TILES - 1],
-                    in0=sums[:, 1, 0 : B - 1, C_TILES - 1],
+                    out=sums[:, 1, 0 : B - 2, C_TILES - 1],
+                    in0=sums[:, 1, 0 : B - 2, C_TILES - 1],
                     in1=last_sums[:],
                     op=ALU.add,
                 )
+                square_last(1, 0, 0, 0)
+                nc.vector.tensor_tensor(out=v[:, 0], in0=sums[:, 0], in1=recip[:], op=ALU.mult)
                 nc.vector.tensor_tensor(
                     out=sums[:, 1, 0 : B - 1], in0=sums[:, 1, 0 : B - 1], in1=recip[:, 0 : B - 1], op=ALU.mult
                 )
-                weigh_row(b, 1, 1)
+                square_last(1, 1, 0, 1)
 
         moments = const.tile([P, 2, 2 * B, C_TILES], F32)
         v = moments[:, :, 0:B, :]
@@ -449,19 +506,20 @@ def tile_attentivestatspool_pb_t_kernel(tc, h, x, mask, w2, b2, g2, be2, out):
         for n in range(-REGROUP_LEAD - LOAD_LEAD, TILES + T_TILES):
             load_tile(n + REGROUP_LEAD + LOAD_LEAD)
             if n + 1 == 0:
+                turn_mask()
                 regroup_on_vector(0)
+                spread_penalty(0, 0)
                 turn_w2()
+                spread_penalty(0, 1)
+            for b, part in SPREAD.get(n, ()):
+                spread_penalty(b, part)
             regroup_on_scalar(n + REGROUP_LEAD)
             if n + 1 >= HELPED_TILES:
                 regroup_on_vector(n + 1)
-            if n in PEN_AT and n not in LATE:
-                make_penalty(n)
             if n in ZERO_AT and n not in LATE:
                 nc.vector.memset(zero[n][:], 0.0)
             quantise_and_multiply(n)
             if n in LATE:
-                if n in PEN_AT:
-                    make_penalty(n)
                 nc.vector.memset(zero[n][:], 0.0)
             copy_x(X_COPIES.get(n, ()))
             for i in GP:
@@ -474,7 +532,16 @@ def tile_attentivestatspool_pb_t_kernel(tc, h, x, mask, w2, b2, g2, be2, out):
             total_of_fold(n)
             pool_step(n - T_TILES)
             copy_x(X_COPIES_LATE.get(n, ()))
+            if n == TILES - 1:
+                for ct in range(C_TILES):
+                    for part in range(X_PARTS):
+                        turn_x(ct, part)
+            if n in (TILES, TILES + 1):
+                for part in range(X_PARTS):
+                    turn_x_back(n - TILES, part)
             fold(n)
+            if n == TILES + T_TILES - 1:
+                fold_last()
 
         nc.scalar.activation(out=warm[:], in_=sum_e[:, B - 1, C_TILES - 1 :], func=ACT.Sqrt)
 
@@ -488,7 +555,18 @@ def tile_attentivestatspool_pb_t_kernel(tc, h, x, mask, w2, b2, g2, be2, out):
 
         nc.vector.tensor_tensor(out=v_sq[:, 0], in0=v[:, 0], in1=v[:, 0], op=ALU.mult)
         variance = const.tile([P, B, C_TILES], F32)
-        nc.vector.tensor_tensor(out=variance[:], in0=sums[:, 1], in1=v_sq[:, 0], op=ALU.subtract)
+        for ct in range(C_TILES):
+            nc.vector.scalar_tensor_tensor(
+                out=variance[:, B - 1, ct : ct + 1],
+                in0=last_second[:, 1, ct : ct + 1],
+                scalar=last_second[:, 0, ct : ct + 1],
+                in1=v_sq[:, 0, B - 1, ct : ct + 1],
+                op0=ALU.add,
+                op1=ALU.subtract,
+            )
+        nc.vector.tensor_tensor(
+            out=variance[:, 0 : B - 1], in0=sums[:, 1, 0 : B - 1], in1=v_sq[:, 0, 0 : B - 1], op=ALU.subtract
+        )
         nc.vector.tensor_scalar_max(out=v_sq[:, 1], in0=variance[:], scalar1=EPS_STD)
         nc.scalar.activation(out=v[:, 1], in_=v_sq[:, 1], func=ACT.Sqrt)
         nc.scalar.activation(out=warm[:], in_=warm[:], func=ACT.Abs_reciprocal_sqrt)

@@ -26,27 +26,30 @@ C_TILES = C // P
 TILES = B * T_TILES
 RUN = 8
 MASKED = -1e30
+PEN_AT = {6: 2, 10: 3}
 
 LOAD_LEAD = 4
 REGROUP_LEAD = 2
 GP = {5: 4, 6: 5, 8: 6, 12: 10}
 GSHARE = {5: 448, 6: 448, 8: 448, 12: 448}
-V_EXX = {0: (2816, 3072), 1: (2816, 3072), 2: (0, 0)}
+V_EXX = {0: (2560, 3072), 1: (2560, 3072), 2: (0, 0)}
 ZERO_AT = (4, 5, 6, 10)
 LATE = (4, 5)
 GPSIMD_STEP = 2
 VECTOR_AT = (6, 10, 14)
 VECTOR_SHARE = 512
-HEAD_SHARES = {0: (256, 256), 1: (256, 512), 2: (256, 512), 3: (256, 512), 7: (0, 256), 11: (0, 256)}
+HEAD_SHARES = {0: (256, 256), 1: (256, 512), 2: (0, 512), 3: (256, 512), 7: (0, 256), 11: (0, 256)}
 FIRST_PIECES = 2
 X_COLS = 1024
 X_PARTS = T // X_COLS
-EXX_PARTS = {3: (0, 896), 0: (896, 2816), 1: (3072, 4096)}
+EXX_PARTS = {3: (0, 750), 0: (750, 2560), 1: (3072, 4096)}
 LAST_PARTS = {3: (0, 2048), 1: (2048, 4096)}
-G_LAST = 1152
+G_LAST = 1024
 FOLD_STEPS = (1, 2)
+MASK_AFTER = {7: 2, 11: 3}
+SPREAD_FIRST = 2
 X_AFTER = {6: 0, 11: 1, 13: 2, 15: 3}
-SPREAD = {0: ((1, 0), (1, 1)), 1: ((2, 0), (2, 1)), 2: ((3, 0), (3, 1))}
+SPREAD = {2: ((1, 0),), 3: ((1, 1),)}
 X_COPIES = {
     5: ((0, 0, 1), (0, 0, 0), (0, 1, 0)),
     8: ((1, 0, 1),),
@@ -107,7 +110,10 @@ def tile_attentivestatspool_pb_t_kernel(tc, h, x, mask, w2, b2, g2, be2, out):
 
         w2_rows = const.tile([P, C_TILES, H], BF16)
         nc.sync.dma_start(out=w2_rows[:], in_=w2.rearrange("(ct c) k -> c ct k", c=P))
-        nc.scalar.dma_start(out=mask_rows[0 : B * T // P, :], in_=mask.rearrange("b o (q t) -> (b o q) t", t=P))
+        nc.scalar.dma_start(
+            out=mask_rows[0 : SPREAD_FIRST * T // P, :],
+            in_=mask[0:SPREAD_FIRST].rearrange("b o (q t) -> (b o q) t", t=P),
+        )
         nc.scalar.dma_start(out=gb_rows[0:4, :], in_=g2.rearrange("(r c) -> r c", c=P))
         nc.scalar.dma_start(out=gb_rows[4:8, :], in_=be2.rearrange("(r c) -> r c", c=P))
         nc.scalar.activation(out=warm[:], in_=warm[:], func=ACT.Exp)
@@ -145,13 +151,16 @@ def tile_attentivestatspool_pb_t_kernel(tc, h, x, mask, w2, b2, g2, be2, out):
         last_second = const.tile([P, 2, C_TILES], F32)
 
         penalty = const.tile([P, B, T], BF16)
-        penalty_cols = const.tile([P, B * T // P], BF16)
+        penalty_cols = const.tile([P, SPREAD_FIRST * T // P], BF16)
         x_rows = const.tile([P, B, C_TILES, T], BF16)
         grouped = {}
         codes = {}
         scales = {}
         banks = {}
         scores = {}
+
+        def load_mask(b):
+            nc.sync.dma_start(out=penalty[:, b], in_=mask[b, 0, :].partition_broadcast(P))
 
         def load_tile(i):
             if i < 0:
@@ -162,6 +171,8 @@ def tile_attentivestatspool_pb_t_kernel(tc, h, x, mask, w2, b2, g2, be2, out):
                     raw[i] = raw_pool.tile([P, PASSES, PACK, T_TILE], BF16, name="raw", tag="raw")
                 for g in range(FIRST_PIECES if i == 0 else 0, PASSES):
                     load_piece(i, g)
+            if i in MASK_AFTER:
+                load_mask(MASK_AFTER[i])
             if i in X_AFTER:
                 nc.sync.dma_start(
                     out=x_rows[:, X_AFTER[i]], in_=x[X_AFTER[i]].rearrange("(ct c) t -> c ct t", c=P)
@@ -345,7 +356,7 @@ def tile_attentivestatspool_pb_t_kernel(tc, h, x, mask, w2, b2, g2, be2, out):
             nc.tensor.transpose(mask_t[:], mask_rows[:], ident_bf[:])
             nc.vector.tensor_scalar(
                 out=penalty_cols[:],
-                in0=mask_t[:, 0 : B * T // P],
+                in0=mask_t[:, 0 : SPREAD_FIRST * T // P],
                 scalar1=0.0,
                 scalar2=MASKED,
                 op0=ALU.is_equal,
@@ -353,16 +364,26 @@ def tile_attentivestatspool_pb_t_kernel(tc, h, x, mask, w2, b2, g2, be2, out):
             )
 
         def spread_penalty(b, part):
-            if True:
-                bank = x_pool.tile([P, X_COLS], BF16, name="penalty_bank", tag="x_bank")
-                for q in range(X_COLS // P):
-                    col = (b * T + part * X_COLS) // P + q
-                    nc.tensor.transpose(
-                        bank[:, q * P : (q + 1) * P],
-                        penalty_cols[:, col : col + 1].to_broadcast([P, P]),
-                        ident_bf[:],
-                    )
-                nc.scalar.copy(out=penalty[:, b, part * X_COLS : (part + 1) * X_COLS], in_=bank[:])
+            bank = x_pool.tile([P, X_COLS], BF16, name="penalty_bank", tag="x_bank")
+            for q in range(X_COLS // P):
+                col = (b * T + part * X_COLS) // P + q
+                nc.tensor.transpose(
+                    bank[:, q * P : (q + 1) * P],
+                    penalty_cols[:, col : col + 1].to_broadcast([P, P]),
+                    ident_bf[:],
+                )
+            nc.scalar.copy(out=penalty[:, b, part * X_COLS : (part + 1) * X_COLS], in_=bank[:])
+
+        def make_penalty(n):
+            b = PEN_AT[n]
+            nc.vector.tensor_scalar(
+                out=penalty[:, b],
+                in0=penalty[:, b],
+                scalar1=0.0,
+                scalar2=MASKED,
+                op0=ALU.is_equal,
+                op1=ALU.mult,
+            )
 
         def quantise_and_multiply(i):
             if i < 0 or i >= TILES:
@@ -478,8 +499,9 @@ def tile_attentivestatspool_pb_t_kernel(tc, h, x, mask, w2, b2, g2, be2, out):
                     in1=x_rows[:, b, 0, 0:G_LAST],
                     op=ALU.mult,
                 )
-                nc.vector.reciprocal(out=recip[:], in_=sum_e[:])
+                nc.scalar.activation(out=warm[:], in_=sum_e[:, b, C_TILES - 1 :], func=ACT.Sqrt)
                 weigh_half(b, 1, 0)
+                nc.vector.reciprocal(out=recip[:], in_=sum_e[:])
                 weigh_half(b, 1, 1)
             if step == 3 and b == B - 1:
                 square_last(0, G_LAST // X_COLS, G_LAST % X_COLS, 0)
@@ -491,15 +513,30 @@ def tile_attentivestatspool_pb_t_kernel(tc, h, x, mask, w2, b2, g2, be2, out):
                     op=ALU.add,
                 )
                 square_last(1, 0, 0, 0)
-                nc.vector.tensor_tensor(out=v[:, 0], in0=sums[:, 0], in1=recip[:], op=ALU.mult)
                 nc.vector.tensor_tensor(
-                    out=sums[:, 1, 0 : B - 1], in0=sums[:, 1, 0 : B - 1], in1=recip[:, 0 : B - 1], op=ALU.mult
+                    out=entries[:, 0:C_TILES, :, 0], in0=by_tile(sums[:, 0]), in1=by_tile(recip[:]), op=ALU.mult
+                )
+                nc.vector.tensor_tensor(
+                    out=second[:], in0=by_tile(sums[:, 1, 0:b]), in1=by_tile(recip[:, 0:b]), op=ALU.mult
+                )
+                nc.vector.scalar_tensor_tensor(
+                    out=neg_sq[:],
+                    in0=entries[:, 0:C_TILES, :, 0],
+                    scalar=-1.0,
+                    in1=entries[:, 0:C_TILES, :, 0],
+                    op0=ALU.mult,
+                    op1=ALU.mult,
                 )
                 square_last(1, 1, 0, 1)
 
-        moments = const.tile([P, 2, 2 * B, C_TILES], F32)
-        v = moments[:, :, 0:B, :]
-        v_sq = moments[:, :, B : 2 * B, :]
+        def by_tile(stat):
+            return stat.rearrange("p b ct -> p ct b")
+
+        entries = const.tile([P, 2 * C_TILES, B, 2], F32)
+        neg_sq = const.tile([P, C_TILES, B], F32)
+        floor = const.tile([P, C_TILES, B], F32)
+        second = const.tile([P, C_TILES, B - 1], F32)
+        top = const.tile([P, C_TILES, B], F32)
         recip = const.tile([P, B, C_TILES], F32)
 
         assert 2 * C_TILES == T_TILES
@@ -516,10 +553,14 @@ def tile_attentivestatspool_pb_t_kernel(tc, h, x, mask, w2, b2, g2, be2, out):
             regroup_on_scalar(n + REGROUP_LEAD)
             if n + 1 >= HELPED_TILES:
                 regroup_on_vector(n + 1)
+            if n in PEN_AT and n not in LATE:
+                make_penalty(n)
             if n in ZERO_AT and n not in LATE:
                 nc.vector.memset(zero[n][:], 0.0)
             quantise_and_multiply(n)
             if n in LATE:
+                if n in PEN_AT:
+                    make_penalty(n)
                 nc.vector.memset(zero[n][:], 0.0)
             copy_x(X_COPIES.get(n, ()))
             for i in GP:
@@ -543,77 +584,95 @@ def tile_attentivestatspool_pb_t_kernel(tc, h, x, mask, w2, b2, g2, be2, out):
             if n == TILES + T_TILES - 1:
                 fold_last()
 
-        nc.scalar.activation(out=warm[:], in_=sum_e[:, B - 1, C_TILES - 1 :], func=ACT.Sqrt)
+        first = slice(0, B - 1)
+        nc.vector.tensor_scalar(
+            out=floor[:], in0=neg_sq[:], scalar1=-1.0, scalar2=EPS_STD, op0=ALU.mult, op1=ALU.add
+        )
+        nc.vector.tensor_scalar(
+            out=entries[:, 0:C_TILES, :, 1], in0=neg_sq[:], scalar1=-1.0, scalar2=EPS_LN, op0=ALU.mult, op1=ALU.add
+        )
+        acc = x_pool.tile([P, B, 2], F32, name="acc", tag="x_bank")
 
-        full = [P, 2, B, C_TILES]
+        def add_to_sums(part):
+            nc.tensor.matmul(
+                out=acc[:].rearrange("p b k -> p (b k)"),
+                lhsT=averager[:],
+                rhs=entries[:, part].rearrange("p b k -> p (b k)"),
+                start=(part == 0),
+                stop=(part == 2 * C_TILES - 1),
+            )
 
-        def per_utterance(stat):
-            return stat.unsqueeze(1).unsqueeze(3).to_broadcast(full)
-
-        def per_entry(columns):
-            return columns.rearrange("p (s ct) -> p s ct", s=2).unsqueeze(2).to_broadcast(full)
-
-        nc.vector.tensor_tensor(out=v_sq[:, 0], in0=v[:, 0], in1=v[:, 0], op=ALU.mult)
-        variance = const.tile([P, B, C_TILES], F32)
+        for ct in range(C_TILES):
+            add_to_sums(ct)
         for ct in range(C_TILES):
             nc.vector.scalar_tensor_tensor(
-                out=variance[:, B - 1, ct : ct + 1],
+                out=top[:, ct, B - 1 :],
                 in0=last_second[:, 1, ct : ct + 1],
                 scalar=last_second[:, 0, ct : ct + 1],
-                in1=v_sq[:, 0, B - 1, ct : ct + 1],
+                in1=floor[:, ct, B - 1 :],
                 op0=ALU.add,
-                op1=ALU.subtract,
+                op1=ALU.max,
+            )
+        nc.vector.tensor_tensor(out=top[:, :, first], in0=second[:], in1=floor[:, :, first], op=ALU.max)
+        for ct in range(C_TILES):
+            nc.scalar.activation(
+                out=entries[:, C_TILES + ct, B - 1, 0:1],
+                in_=top[:, ct, B - 1 :],
+                func=ACT.Sqrt,
+                bias=neg_sq[:, ct, B - 1 :],
+            )
+        for ct in range(C_TILES):
+            nc.vector.tensor_scalar(
+                out=entries[:, C_TILES + ct, B - 1, 1:2],
+                in0=top[:, ct, B - 1 :],
+                scalar1=neg_sq[:, ct, B - 1 :],
+                scalar2=EPS_LN,
+                op0=ALU.add,
+                op1=ALU.add,
             )
         nc.vector.tensor_tensor(
-            out=variance[:, 0 : B - 1], in0=sums[:, 1, 0 : B - 1], in1=v_sq[:, 0, 0 : B - 1], op=ALU.subtract
+            out=second[:], in0=top[:, :, first], in1=neg_sq[:, :, first], op=ALU.add
         )
-        nc.vector.tensor_scalar_max(out=v_sq[:, 1], in0=variance[:], scalar1=EPS_STD)
-        nc.scalar.activation(out=v[:, 1], in_=v_sq[:, 1], func=ACT.Sqrt)
-        nc.scalar.activation(out=warm[:], in_=warm[:], func=ACT.Abs_reciprocal_sqrt)
-
-        share = misc_pool.tile([P, 2, 2 * B, C_TILES], F32, tag="misc")
-        nc.tensor.matmul(
-            out=share[:].rearrange("p s m ct -> p (s m ct)"),
-            lhsT=averager[:],
-            rhs=moments[:].rearrange("p s m ct -> p (s m ct)"),
-            start=True,
-            stop=True,
-        )
-        averages = const.tile([P, 2 * B], F32)
-        nc.vector.tensor_reduce(
-            out=averages[:], in_=share[:].rearrange("p s m ct -> p m s ct"), axis=AXIS.XY, op=ALU.add
-        )
-        mu = averages[:, 0:B]
-        mu_sq = const.tile([P, B], F32)
-        nc.vector.tensor_tensor(out=mu_sq[:], in0=mu, in1=mu, op=ALU.mult)
-        var_ln = const.tile([P, B], F32)
-        nc.vector.scalar_tensor_tensor(
-            out=var_ln[:],
-            in0=averages[:, B : 2 * B],
-            scalar=EPS_LN,
-            in1=mu_sq[:],
-            op0=ALU.add,
-            op1=ALU.subtract,
-        )
-        rstd_ln = const.tile([P, B], F32)
-        nc.scalar.activation(out=rstd_ln[:], in_=var_ln[:], func=ACT.Abs_reciprocal_sqrt)
-        gained = const.tile(full, F32)
-        nc.vector.tensor_tensor(out=gained[:], in0=v, in1=per_utterance(mu), op=ALU.subtract)
-        nc.vector.tensor_tensor(
-            out=gained[:], in0=gained[:], in1=per_entry(gb[:, 0:4]), op=ALU.mult
-        )
-        nc.vector.tensor_tensor(
-            out=gained[:], in0=gained[:], in1=per_utterance(rstd_ln[:]), op=ALU.mult
-        )
-        rows = 2 * B * C_TILES
-        nc.vector.tensor_tensor(
-            out=y_pad[:, 0:rows].rearrange("p (b s ct) -> p s b ct", s=2, ct=C_TILES),
-            in0=gained[:],
-            in1=per_entry(gb[:, 4:8]),
-            op=ALU.add,
-        )
+        nc.scalar.activation(out=entries[:, C_TILES:, first, 0], in_=second[:], func=ACT.Sqrt)
+        nc.vector.tensor_scalar_add(out=entries[:, C_TILES:, first, 1], in0=second[:], scalar1=EPS_LN)
+        for ct in range(C_TILES):
+            add_to_sums(C_TILES + ct)
+        neg_var = const.tile([P, B], F32)
+        for b in range(B):
+            nc.vector.tensor_scalar(
+                out=neg_var[:, b : b + 1],
+                in0=acc[:, b, 0:1],
+                scalar1=acc[:, b, 0:1],
+                scalar2=acc[:, b, 1:2],
+                op0=ALU.mult,
+                op1=ALU.subtract,
+            )
+        root = const.tile([P, B], F32)
+        nc.scalar.activation(out=root[:], in_=neg_var[:], func=ACT.Sqrt, scale=-1.0)
+        gained = const.tile([P, B, 2 * C_TILES], F32)
+        for b in range(B):
+            nc.vector.scalar_tensor_tensor(
+                out=gained[:, b],
+                in0=entries[:, :, b, 0],
+                scalar=acc[:, b, 0:1],
+                in1=gb[:, 0 : 2 * C_TILES],
+                op0=ALU.subtract,
+                op1=ALU.mult,
+            )
+        rstd = const.tile([P, B], F32)
+        nc.vector.reciprocal(out=rstd[:], in_=root[:])
+        for b in range(B):
+            nc.vector.scalar_tensor_tensor(
+                out=y_pad[:, 2 * C_TILES * b : 2 * C_TILES * (b + 1)],
+                in0=gained[:, b],
+                scalar=rstd[:, b : b + 1],
+                in1=gb[:, 2 * C_TILES :],
+                op0=ALU.mult,
+                op1=ALU.add,
+            )
         y_t = misc_pool.tile([P, P], F32, tag="misc")
         nc.tensor.transpose(y_t[:], y_pad[:], ident_f32[:])
+        rows = 2 * B * C_TILES
         y_rows = const.tile([rows, P], F32)
         nc.scalar.copy(out=y_rows[:], in_=y_t[0:rows, :])
         nc.sync.dma_start(out=out.rearrange("b (e c) o -> (b e) (c o)", c=P), in_=y_rows[:])

@@ -34,7 +34,7 @@ GP = {5: 4, 6: 5, 8: 6, 12: 10}
 GSHARE = {5: 448, 6: 448, 8: 448, 12: 448}
 V_EXX = {0: (2560, 3072), 1: (2560, 3072), 2: (0, 0)}
 ZERO_AT = (4, 5, 6, 10)
-LATE = (4, 5)
+LATE = (4, 5, 6, 10)
 GPSIMD_STEP = 2
 VECTOR_AT = (6, 10, 14)
 VECTOR_SHARE = 512
@@ -82,17 +82,21 @@ def tile_attentivestatspool_pb_t_kernel(tc, h, x, mask, w2, b2, g2, be2, out):
         make_identity(nc, ident_bf[:])
         ident_f32 = const.tile([P, P], F32)
         make_identity(nc, ident_f32[:])
+        mask_rows = const.tile([P, P], BF16)
+        nc.vector.memset(mask_rows[:], 0.0)
         averager = const.tile([P, P], F32)
         nc.vector.memset(averager[:], 1.0 / (2 * C))
         y_pad = const.tile([P, P], F32)
         nc.vector.memset(y_pad[:], 0.0)
         gb_rows = const.tile([P, P], BF16)
         nc.vector.memset(gb_rows[:], 0.0)
-        mask_rows = const.tile([P, P], BF16)
-        nc.vector.memset(mask_rows[:], 0.0)
         warm = const.tile([P, 1], F32)
         nc.vector.memset(warm[:], 0.0)
 
+        nc.sync.dma_start(
+            out=mask_rows[0 : SPREAD_FIRST * T // P, :],
+            in_=mask[0:SPREAD_FIRST].rearrange("b o (q t) -> (b o q) t", t=P),
+        )
         raw = {}
 
         def load_piece(i, g):
@@ -110,10 +114,6 @@ def tile_attentivestatspool_pb_t_kernel(tc, h, x, mask, w2, b2, g2, be2, out):
 
         w2_rows = const.tile([P, C_TILES, H], BF16)
         nc.sync.dma_start(out=w2_rows[:], in_=w2.rearrange("(ct c) k -> c ct k", c=P))
-        nc.scalar.dma_start(
-            out=mask_rows[0 : SPREAD_FIRST * T // P, :],
-            in_=mask[0:SPREAD_FIRST].rearrange("b o (q t) -> (b o q) t", t=P),
-        )
         nc.scalar.dma_start(out=gb_rows[0:4, :], in_=g2.rearrange("(r c) -> r c", c=P))
         nc.scalar.dma_start(out=gb_rows[4:8, :], in_=be2.rearrange("(r c) -> r c", c=P))
         nc.scalar.activation(out=warm[:], in_=warm[:], func=ACT.Exp)
@@ -146,6 +146,7 @@ def tile_attentivestatspool_pb_t_kernel(tc, h, x, mask, w2, b2, g2, be2, out):
         neg_max = const.tile([P, B, C_TILES], F32)
         sum_e = const.tile([P, B, C_TILES], F32)
         sums = const.tile([P, 2, B, C_TILES], F32)
+        half_e = const.tile([P, X_PARTS, C_TILES], F32)
         half_sums = const.tile([P, X_PARTS, B, C_TILES], F32)
         last_sums = const.tile([P, B - 2], F32)
         last_second = const.tile([P, 2, C_TILES], F32)
@@ -447,18 +448,22 @@ def tile_attentivestatspool_pb_t_kernel(tc, h, x, mask, w2, b2, g2, be2, out):
                 for ct in range(C_TILES):
                     mask_bank(n - 1, ct)
 
+        def exp(b, ct, part, total):
+            row = scores[b][:, ct, part]
+            nc.scalar.activation(
+                out=row, in_=row, func=ACT.Exp, bias=neg_max[:, b, ct : ct + 1], accum_out=total
+            )
+
         def maximum_and_exp(b, ct):
             row = scores[b][:, ct, :]
             nc.vector.tensor_reduce(
                 out=neg_max[:, b, ct : ct + 1], in_=row, axis=AXIS.X, op=ALU.max, negate=True
             )
-            nc.scalar.activation(
-                out=row,
-                in_=row,
-                func=ACT.Exp,
-                bias=neg_max[:, b, ct : ct + 1],
-                accum_out=sum_e[:, b, ct : ct + 1],
-            )
+            if b == B - 1:
+                for part in range(X_PARTS):
+                    exp(b, ct, slice(part * X_COLS, (part + 1) * X_COLS), half_e[:, part, ct : ct + 1])
+            else:
+                exp(b, ct, slice(0, T), sum_e[:, b, ct : ct + 1])
 
         def square_last(ct, part, first, slot):
             b = B - 1
@@ -499,19 +504,20 @@ def tile_attentivestatspool_pb_t_kernel(tc, h, x, mask, w2, b2, g2, be2, out):
                     in1=x_rows[:, b, 0, 0:G_LAST],
                     op=ALU.mult,
                 )
-                nc.scalar.activation(out=warm[:], in_=sum_e[:, b, C_TILES - 1 :], func=ACT.Sqrt)
                 weigh_half(b, 1, 0)
-                nc.vector.reciprocal(out=recip[:], in_=sum_e[:])
+                nc.vector.tensor_tensor(out=sum_e[:, b], in0=half_e[:, 0], in1=half_e[:, 1], op=ALU.add)
                 weigh_half(b, 1, 1)
+                nc.vector.reciprocal(out=recip[:], in_=sum_e[:])
             if step == 3 and b == B - 1:
-                square_last(0, G_LAST // X_COLS, G_LAST % X_COLS, 0)
-                nc.vector.tensor_tensor(out=sums[:, 0], in0=half_sums[:, 0], in1=half_sums[:, 1], op=ALU.add)
+                nc.scalar.activation(out=warm[:], in_=half_e[:, 1, C_TILES - 1 :], func=ACT.Sqrt)
                 nc.vector.tensor_tensor(
                     out=sums[:, 1, 0 : B - 2, C_TILES - 1],
                     in0=sums[:, 1, 0 : B - 2, C_TILES - 1],
                     in1=last_sums[:],
                     op=ALU.add,
                 )
+                square_last(0, G_LAST // X_COLS, G_LAST % X_COLS, 0)
+                nc.vector.tensor_tensor(out=sums[:, 0], in0=half_sums[:, 0], in1=half_sums[:, 1], op=ALU.add)
                 square_last(1, 0, 0, 0)
                 nc.vector.tensor_tensor(
                     out=entries[:, 0:C_TILES, :, 0], in0=by_tile(sums[:, 0]), in1=by_tile(recip[:]), op=ALU.mult

@@ -30,19 +30,19 @@ PEN_AT = {6: 2, 10: 3}
 
 LOAD_LEAD = 4
 REGROUP_LEAD = 2
-GP = {5: 4, 6: 5, 8: 6, 12: 10}
-GSHARE = {5: 448, 6: 448, 8: 448, 12: 448}
-V_EXX = {0: (2560, 3072), 1: (2560, 3072), 2: (0, 0)}
-ZERO_AT = (4, 5, 6, 10)
-LATE = (4, 5, 6, 10)
+GP = {5: 4, 6: 5, 8: 6, 12: 10, 15: 14}
+GSHARE = {5: 448, 6: 448, 8: 448, 12: 448, 15: 448}
+V_EXX = {0: (2816, 3072), 1: (2816, 3072), 2: (0, 0)}
+ZERO_AT = (4, 5, 6, 10, 14)
+LATE = (4, 5, 6, 10, 14)
 GPSIMD_STEP = 2
 VECTOR_AT = (6, 10, 14)
 VECTOR_SHARE = 512
-HEAD_SHARES = {0: (256, 256), 1: (256, 512), 2: (0, 512), 3: (256, 512), 7: (0, 256), 11: (0, 256)}
+HEAD_SHARES = {0: (256, 256), 1: (256, 512), 2: (0, 512), 3: (256, 512), 7: (0, 256)}
 FIRST_PIECES = 2
 X_COLS = 1024
 X_PARTS = T // X_COLS
-EXX_PARTS = {3: (0, 750), 0: (750, 2560), 1: (3072, 4096)}
+EXX_PARTS = {3: (0, 896), 0: (896, 2816), 1: (3072, 4096)}
 LAST_PARTS = {3: (0, 2048), 1: (2048, 4096)}
 G_LAST = 1024
 FOLD_STEPS = (1, 2)
@@ -93,10 +93,6 @@ def tile_attentivestatspool_pb_t_kernel(tc, h, x, mask, w2, b2, g2, be2, out):
         warm = const.tile([P, 1], F32)
         nc.vector.memset(warm[:], 0.0)
 
-        nc.sync.dma_start(
-            out=mask_rows[0 : SPREAD_FIRST * T // P, :],
-            in_=mask[0:SPREAD_FIRST].rearrange("b o (q t) -> (b o q) t", t=P),
-        )
         raw = {}
 
         def load_piece(i, g):
@@ -111,11 +107,14 @@ def tile_attentivestatspool_pb_t_kernel(tc, h, x, mask, w2, b2, g2, be2, out):
         raw[0] = raw_pool.tile([P, PASSES, PACK, T_TILE], BF16, name="raw", tag="raw")
         for g in range(FIRST_PIECES):
             load_piece(0, g)
+            if g == 0:
+                nc.sync.dma_start(
+                    out=mask_rows[0 : SPREAD_FIRST * T // P, :],
+                    in_=mask[0:SPREAD_FIRST].rearrange("b o (q t) -> (b o q) t", t=P),
+                )
 
         w2_rows = const.tile([P, C_TILES, H], BF16)
         nc.sync.dma_start(out=w2_rows[:], in_=w2.rearrange("(ct c) k -> c ct k", c=P))
-        nc.scalar.dma_start(out=gb_rows[0:4, :], in_=g2.rearrange("(r c) -> r c", c=P))
-        nc.scalar.dma_start(out=gb_rows[4:8, :], in_=be2.rearrange("(r c) -> r c", c=P))
         nc.scalar.activation(out=warm[:], in_=warm[:], func=ACT.Exp)
         w2_pairs = w2_rows[:].bitcast(F32).rearrange("c ct (g p u) -> c ct g u p", p=P, u=PAIRS)
         w2_grouped = const.tile([P, PASSES, C_TILES, P, PACK], BF16, align_bytes=64)
@@ -132,6 +131,11 @@ def tile_attentivestatspool_pb_t_kernel(tc, h, x, mask, w2, b2, g2, be2, out):
                 nc.scalar.copy(
                     out=w2_grouped[:, g].bitcast(F32), in_=w2_t[:].rearrange("p ct u c -> p ct c u")
                 )
+        def load_gains():
+            nc.sync.dma_start(out=gb_rows[0:4, :], in_=g2.rearrange("(r c) -> r c", c=P))
+            nc.sync.dma_start(out=gb_rows[4:8, :], in_=be2.rearrange("(r c) -> r c", c=P))
+
+        def turn_gains():
             gb_t = misc_pool.tile([P, P], BF16, name="gb_t", tag="misc")
             nc.tensor.transpose(gb_t[:], gb_rows[:], ident_bf[:])
             nc.scalar.copy(out=gb[:], in_=gb_t[:, 0:8])
@@ -342,10 +346,10 @@ def tile_attentivestatspool_pb_t_kernel(tc, h, x, mask, w2, b2, g2, be2, out):
                 op1=ALU.add,
             )
 
-        def regroup_on_vector(i):
+        def regroup_on_vector(i, pieces=range(PASSES)):
             if i < 0 or i >= TILES or not on_vector(i):
                 return
-            for g in range(PASSES):
+            for g in pieces:
                 if vector_frames(i, g) > 0:
                     dst, src = regroup_views(i, g, T_TILE - vector_frames(i, g), T_TILE)
                     nc.vector.tensor_copy(out=dst, in_=src)
@@ -548,9 +552,14 @@ def tile_attentivestatspool_pb_t_kernel(tc, h, x, mask, w2, b2, g2, be2, out):
         assert 2 * C_TILES == T_TILES
         for n in range(-REGROUP_LEAD - LOAD_LEAD, TILES + T_TILES):
             load_tile(n + REGROUP_LEAD + LOAD_LEAD)
+            if n + REGROUP_LEAD + LOAD_LEAD == TILES:
+                load_gains()
+            if n == TILES + 1:
+                turn_gains()
             if n + 1 == 0:
+                regroup_on_vector(0, (0,))
                 turn_mask()
-                regroup_on_vector(0)
+                regroup_on_vector(0, (1,))
                 spread_penalty(0, 0)
                 turn_w2()
                 spread_penalty(0, 1)

import concourse.mybir as mybir
from concourse.masks import make_identity

F32 = mybir.dt.float32
BF16 = mybir.dt.bfloat16
U32 = mybir.dt.uint32
U8 = mybir.dt.uint8
FP8X4 = mybir.dt.float8_e4m3fn_x4
ALU = mybir.AluOpType
ACT = mybir.ActivationFunctionType
AXIS = mybir.AxisListType

B, C, T, H = 4, 256, 2048, 1024
EPS_LN = 1e-5
EPS_STD = 1e-5
FLOPS = 2 * B * C * H * T

P = 128
PACK = 4
K_PASS = P * PACK
PAIRS = PACK // 2
PASSES = H // K_PASS
T_TILE = 512
T_TILES = T // T_TILE
C_TILES = C // P
TILES = B * T_TILES
RUN = 8
MASKED = -1e30
PEN_AT = {6: 2, 10: 3}

LOAD_LEAD = 4
REGROUP_LEAD = 2
GP = {5: 4, 6: 5, 8: 6, 12: 10, 15: 14}
GSHARE = {5: 448, 6: 448, 8: 448, 12: 448, 15: 448}
V_EXX = {0: (2816, 3072), 1: (2816, 3072), 2: (0, 0)}
ZERO_AT = (4, 5, 6, 10, 14)
LATE = (4, 5, 6, 10, 14)
GPSIMD_STEP = 2
VECTOR_AT = (6, 10, 14)
VECTOR_SHARE = 512
HEAD_SHARES = {0: (256, 256), 1: (256, 512), 2: (0, 512), 3: (256, 512), 7: (0, 256)}
FIRST_PIECES = 2
X_COLS = 1024
X_PARTS = T // X_COLS
EXX_PARTS = {3: (0, 896), 0: (896, 2816), 1: (3072, 4096)}
LAST_PARTS = {3: (0, 2048), 1: (2048, 4096)}
G_LAST = 1024
FOLD_STEPS = (1, 2)
MASK_AFTER = {7: 2, 11: 3}
SPREAD_FIRST = 2
X_AFTER = {6: 0, 11: 1, 13: 2, 15: 3}
SPREAD = {2: ((1, 0),), 3: ((1, 1),)}
X_COPIES = {
    5: ((0, 0, 1), (0, 0, 0), (0, 1, 0)),
    8: ((1, 0, 1),),
    9: ((1, 1, 0),),
    12: ((2, 0, 1),),
    13: ((2, 1, 0),),
}
X_COPIES_LATE = {
    6: ((0, 1, 1),),
    8: ((1, 0, 0),),
    10: ((1, 1, 1),),
    12: ((2, 0, 0),),
    14: ((2, 1, 1),),
}
HELPED_TILES = 4


def tile_attentivestatspool_pb_t_kernel(tc, h, x, mask, w2, b2, g2, be2, out):
    nc = tc.nc
    with tc.tile_pool(name="const", bufs=1) as const, tc.tile_pool(
        name="raw", bufs=LOAD_LEAD + 2
    ) as raw_pool, tc.tile_pool(name="grouped", bufs=REGROUP_LEAD + 2) as grouped_pool, tc.tile_pool(
        name="codes", bufs=3
    ) as codes_pool, tc.tile_pool(name="scores", bufs=2) as score_pool, tc.tile_pool(
        name="prod", bufs=2
    ) as prod_pool, tc.tile_pool(name="fold", bufs=2) as fold_pool, tc.psum_pool(name="banks", bufs=4) as bank_pool, tc.psum_pool(
        name="xbanks", bufs=3
    ) as x_pool, tc.psum_pool(name="misc", bufs=1) as misc_pool, tc.manual_schedule():
        ident_bf = const.tile([P, P], BF16)
        make_identity(nc, ident_bf[:])
        ident_f32 = const.tile([P, P], F32)
        make_identity(nc, ident_f32[:])
        mask_rows = const.tile([P, P], BF16)
        nc.vector.memset(mask_rows[:], 0.0)
        averager = const.tile([P, P], F32)
        nc.vector.memset(averager[:], 1.0 / (2 * C))
        y_pad = const.tile([P, P], F32)
        nc.vector.memset(y_pad[:], 0.0)
        gb_rows = const.tile([P, P], BF16)
        nc.vector.memset(gb_rows[:], 0.0)
        warm = const.tile([P, 1], F32)
        nc.vector.memset(warm[:], 0.0)

        raw = {}

        def load_piece(i, g):
            b, tt = divmod(i, T_TILES)
            nc.sync.dma_start(
                out=raw[i][:, g],
                in_=h[b, g * K_PASS : (g + 1) * K_PASS, tt * T_TILE : (tt + 1) * T_TILE].rearrange(
                    "(p j) t -> p j t", j=PACK
                ),
            )

        raw[0] = raw_pool.tile([P, PASSES, PACK, T_TILE], BF16, name="raw", tag="raw")
        for g in range(FIRST_PIECES):
            load_piece(0, g)
            if g == 0:
                nc.sync.dma_start(
                    out=mask_rows[0 : SPREAD_FIRST * T // P, :],
                    in_=mask[0:SPREAD_FIRST].rearrange("b o (q t) -> (b o q) t", t=P),
                )

        w2_rows = const.tile([P, C_TILES, H], BF16)
        nc.sync.dma_start(out=w2_rows[:], in_=w2.rearrange("(ct c) k -> c ct k", c=P))
        nc.scalar.activation(out=warm[:], in_=warm[:], func=ACT.Exp)
        w2_pairs = w2_rows[:].bitcast(F32).rearrange("c ct (g p u) -> c ct g u p", p=P, u=PAIRS)
        w2_grouped = const.tile([P, PASSES, C_TILES, P, PACK], BF16, align_bytes=64)
        w2_codes = const.tile([P, PASSES, C], U32, align_bytes=64)
        w2_scales = const.tile([P, PASSES, C], U8, align_bytes=64)
        gb = const.tile([P, 8], F32)

        def turn_w2():
            for g in range(PASSES):
                w2_t = x_pool.tile([P, C_TILES, PAIRS, P], F32, name="w2_t", tag="x_bank")
                for ct in range(C_TILES):
                    for u in range(PAIRS):
                        nc.tensor.transpose(w2_t[:, ct, u, :], w2_pairs[:, ct, g, u, :], ident_f32[:])
                nc.scalar.copy(
                    out=w2_grouped[:, g].bitcast(F32), in_=w2_t[:].rearrange("p ct u c -> p ct c u")
                )
        def load_gains():
            nc.sync.dma_start(out=gb_rows[0:4, :], in_=g2.rearrange("(r c) -> r c", c=P))
            nc.sync.dma_start(out=gb_rows[4:8, :], in_=be2.rearrange("(r c) -> r c", c=P))

        def turn_gains():
            gb_t = misc_pool.tile([P, P], BF16, name="gb_t", tag="misc")
            nc.tensor.transpose(gb_t[:], gb_rows[:], ident_bf[:])
            nc.scalar.copy(out=gb[:], in_=gb_t[:, 0:8])

        def quantise_w2():
            nc.vector.quantize_mx(
                out=w2_codes[:].rearrange("p g c -> p (g c)").bitcast(FP8X4),
                scales=w2_scales[:].rearrange("p g c -> p (g c)"),
                in_=w2_grouped[:].rearrange("p g ct c j -> p (g ct c j)"),
            )

        neg_max = const.tile([P, B, C_TILES], F32)
        sum_e = const.tile([P, B, C_TILES], F32)
        sums = const.tile([P, 2, B, C_TILES], F32)
        half_e = const.tile([P, X_PARTS, C_TILES], F32)
        half_sums = const.tile([P, X_PARTS, B, C_TILES], F32)
        last_sums = const.tile([P, B - 2], F32)
        last_second = const.tile([P, 2, C_TILES], F32)

        penalty = const.tile([P, B, T], BF16)
        penalty_cols = const.tile([P, SPREAD_FIRST * T // P], BF16)
        x_rows = const.tile([P, B, C_TILES, T], BF16)
        grouped = {}
        codes = {}
        scales = {}
        banks = {}
        scores = {}

        def load_mask(b):
            nc.sync.dma_start(out=penalty[:, b], in_=mask[b, 0, :].partition_broadcast(P))

        def load_tile(i):
            if i < 0:
                return
            b, tt = divmod(i, T_TILES)
            if b < B:
                if i > 0:
                    raw[i] = raw_pool.tile([P, PASSES, PACK, T_TILE], BF16, name="raw", tag="raw")
                for g in range(FIRST_PIECES if i == 0 else 0, PASSES):
                    load_piece(i, g)
            if i in MASK_AFTER:
                load_mask(MASK_AFTER[i])
            if i in X_AFTER:
                nc.sync.dma_start(
                    out=x_rows[:, X_AFTER[i]], in_=x[X_AFTER[i]].rearrange("(ct c) t -> c ct t", c=P)
                )

        def regroup_views(i, g, start=0, end=T_TILE):
            dst = grouped[i][:, g, start:end].rearrange("p (c r) j -> p c j r", r=RUN)
            src = raw[i][:, g, :, start:end].rearrange("p j (c r) -> p c j r", r=RUN)
            return dst, src

        def vector_frames(i, g):
            return HEAD_SHARES[i][g]

        def on_gpsimd(i):
            return i in GP

        def on_vector(i):
            return i in HEAD_SHARES

        def regroup_on_scalar(i):
            if i < 0 or i >= TILES:
                return
            grouped[i] = grouped_pool.tile(
                [P, PASSES, T_TILE, PACK], BF16, name="grouped", tag="grouped", align_bytes=64
            )
            for g in range(PASSES):
                end = T_TILE
                if on_vector(i):
                    end = T_TILE - vector_frames(i, g)
                if g == PASSES - 1 and on_gpsimd(i):
                    end = T_TILE - GSHARE[i]
                if end > 0:
                    dst, src = regroup_views(i, g, 0, end)
                    nc.scalar.copy(out=dst, in_=src)

        ones = const.tile([P, 1], F32)
        nc.vector.memset(ones[:], 1.0)
        folded = {}
        folded_sb = {}
        prod = {}

        def second_moment_elsewhere(n):
            later, step = divmod(n - T_TILES, T_TILES)
            earlier = later - 1
            b = later if step == 3 else earlier
            parts = LAST_PARTS if b == B - 2 else EXX_PARTS
            if step in parts and 0 <= b < B - 1:
                cut = slice(*parts[step])
                row = prod[b][:].rearrange("p ct t -> p (ct t)")
                nc.gpsimd.tensor_tensor(
                    out=row[:, cut],
                    in0=row[:, cut],
                    in1=x_rows[:, b].rearrange("p ct t -> p (ct t)")[:, cut],
                    op=ALU.mult,
                )
        def fold(n):
            later, step = divmod(n - T_TILES, T_TILES)
            earlier = later - 1
            if step in FOLD_STEPS and 0 <= earlier < B - 1:
                ct = FOLD_STEPS.index(step)
                if ct == 0:
                    folded[earlier] = misc_pool.tile([P, C_TILES, P], F32, name="folded", tag="misc")
                chunks = [
                    q for q in range(T // P) if not V_EXX[earlier][0] <= ct * T + q * P < V_EXX[earlier][1]
                ]
                for q in chunks:
                    nc.tensor.matmul(
                        out=folded[earlier][:, ct],
                        lhsT=prod[earlier][:, ct, q * P : (q + 1) * P],
                        rhs=ident_f32[:],
                        is_transpose=True,
                        start=(q == chunks[0]),
                        stop=(q == chunks[-1]),
                    )
                if ct == C_TILES - 1:
                    folded_sb[earlier] = fold_pool.tile([P, C_TILES, P], F32, name="folded_sb", tag="folded_sb")
                    nc.scalar.copy(out=folded_sb[earlier][:], in_=folded[earlier][:])
        def fold_last():
            tile_f = misc_pool.tile([P, P], F32, name="folded", tag="misc")
            for q in range(G_LAST // P):
                nc.tensor.matmul(
                    out=tile_f[:],
                    lhsT=prod[B - 1][:, 0, q * P : (q + 1) * P],
                    rhs=ident_f32[:],
                    is_transpose=True,
                    start=(q == 0),
                    stop=(q == G_LAST // P - 1),
                )
            tile_sb = fold_pool.tile([P, C_TILES, P], F32, name="folded_sb", tag="folded_sb")
            nc.scalar.copy(out=tile_sb[:, 0], in_=tile_f[:])
            total = misc_pool.tile([P, 1], F32, name="total", tag="misc")
            nc.tensor.matmul(out=total[:], lhsT=tile_sb[:, 0], rhs=ones[:, 0:1], start=True, stop=True)
            nc.scalar.activation(
                out=last_second[:, 1, 0:1], in_=total[:], func=ACT.Copy, scale=recip[:, B - 1, 0:1]
            )

        def total_of_fold(n):
            later, step = divmod(n - T_TILES, T_TILES)
            earlier = later - 1
            if step == FOLD_STEPS[-1] + 1 and 0 <= earlier < B - 1:
                total = misc_pool.tile([P, C_TILES], F32, name="total", tag="misc")
                for ct in range(C_TILES):
                    nc.tensor.matmul(
                        out=total[:, ct : ct + 1], lhsT=folded_sb[earlier][:, ct], rhs=ones[:, 0:1], start=True, stop=True
                    )
                nc.scalar.copy(out=sums[:, 1, earlier], in_=total[:])

        x_banks = {}

        def x_to_psum(b, ct, part):
            bank = x_pool.tile([P, X_COLS], BF16, name="x_bank", tag="x_bank")
            for start in range(0, X_COLS, T_TILE):
                nc.tensor.matmul(
                    out=bank[:, start : start + T_TILE],
                    lhsT=ident_bf[:],
                    rhs=x_rows[:, b, ct, part * X_COLS + start : part * X_COLS + start + T_TILE],
                    start=True,
                    stop=True,
                )
            x_banks[b, ct, part] = bank

        x_turned = const.tile([P, C_TILES, X_PARTS, X_COLS], BF16)

        def turn_x(ct, part):
            bank = x_pool.tile([P, X_COLS], BF16, name="x_bank", tag="x_bank")
            for start in range(0, X_COLS, P):
                first = part * X_COLS + start
                nc.tensor.transpose(
                    bank[:, start : start + P], x_rows[:, B - 1, ct, first : first + P], ident_bf[:]
                )
            nc.scalar.copy(out=x_turned[:, ct, part], in_=bank[:])

        def turn_x_back(ct, part):
            bank = bank_pool.tile([P, X_COLS], BF16, name="bank", tag="bank")
            for start in range(0, X_COLS, P):
                nc.tensor.transpose(
                    bank[:, start : start + P], x_turned[:, ct, part, start : start + P], ident_bf[:]
                )
            x_banks[B - 1, ct, part] = bank

        def copy_x(copies):
            for b, ct, part in copies:
                x_to_psum(b, ct, part)

        def weigh_half(b, ct, part):
            if b not in prod:
                prod[b] = prod_pool.tile([P, C_TILES, T], F32, name="prod", tag="prod")
            cols = slice(part * X_COLS, (part + 1) * X_COLS)
            nc.vector.scalar_tensor_tensor(
                out=prod[b][:, ct, cols],
                in0=scores[b][:, ct, cols],
                scalar=1.0,
                in1=x_banks[b, ct, part][:],
                op0=ALU.mult,
                op1=ALU.mult,
                accum_out=half_sums[:, part, b, ct : ct + 1],
            )

        def regroup_on_gpsimd(i):
            nc.gpsimd.tensor_scalar(
                out=grouped[i][:, PASSES - 1, T_TILE - GSHARE[i] :],
                in0=raw[i][:, PASSES - 1, :, T_TILE - GSHARE[i] :].rearrange("p j t -> p t j"),
                scalar1=1.0,
                scalar2=zero[GP[i]][:],
                op0=ALU.mult,
                op1=ALU.add,
            )

        def regroup_on_vector(i, pieces=range(PASSES)):
            if i < 0 or i >= TILES or not on_vector(i):
                return
            for g in pieces:
                if vector_frames(i, g) > 0:
                    dst, src = regroup_views(i, g, T_TILE - vector_frames(i, g), T_TILE)
                    nc.vector.tensor_copy(out=dst, in_=src)

        zero = {n: const.tile([P, 1], BF16, name="zero%d" % n) for n in ZERO_AT}

        def turn_mask():
            mask_t = misc_pool.tile([P, P], BF16, name="mask_t", tag="misc")
            nc.tensor.transpose(mask_t[:], mask_rows[:], ident_bf[:])
            nc.vector.tensor_scalar(
                out=penalty_cols[:],
                in0=mask_t[:, 0 : SPREAD_FIRST * T // P],
                scalar1=0.0,
                scalar2=MASKED,
                op0=ALU.is_equal,
                op1=ALU.mult,
            )

        def spread_penalty(b, part):
            bank = x_pool.tile([P, X_COLS], BF16, name="penalty_bank", tag="x_bank")
            for q in range(X_COLS // P):
                col = (b * T + part * X_COLS) // P + q
                nc.tensor.transpose(
                    bank[:, q * P : (q + 1) * P],
                    penalty_cols[:, col : col + 1].to_broadcast([P, P]),
                    ident_bf[:],
                )
            nc.scalar.copy(out=penalty[:, b, part * X_COLS : (part + 1) * X_COLS], in_=bank[:])

        def make_penalty(n):
            b = PEN_AT[n]
            nc.vector.tensor_scalar(
                out=penalty[:, b],
                in0=penalty[:, b],
                scalar1=0.0,
                scalar2=MASKED,
                op0=ALU.is_equal,
                op1=ALU.mult,
            )

        def quantise_and_multiply(i):
            if i < 0 or i >= TILES:
                return
            b, tt = divmod(i, T_TILES)
            codes[i] = codes_pool.tile(
                [P, PASSES, T_TILE], U32, name="codes", tag="codes", align_bytes=64
            )
            scales[i] = codes_pool.tile(
                [P, PASSES, T_TILE], U8, name="scales", tag="scales", align_bytes=64
            )
            nc.vector.quantize_mx(
                out=codes[i][:].rearrange("p g t -> p (g t)").bitcast(FP8X4),
                scales=scales[i][:].rearrange("p g t -> p (g t)"),
                in_=grouped[i][:].rearrange("p g t j -> p (g t j)"),
            )
            if i == 0:
                regroup_on_vector(1)
                quantise_w2()
            for ct in range(C_TILES):
                channels = slice(ct * P, (ct + 1) * P)
                banks[i, ct] = bank_pool.tile([P, T_TILE], F32, name="bank", tag="bank")
                for g in range(PASSES):
                    nc.tensor.matmul_mx(
                        out=banks[i, ct][:],
                        lhsT=w2_codes[:, g, channels].bitcast(FP8X4),
                        lhsT_scale=w2_scales[:, g, channels],
                        rhs=codes[i][:, g, :].bitcast(FP8X4),
                        rhs_scale=scales[i][:, g, :],
                        start=(g == 0),
                        stop=(g == PASSES - 1),
                    )

        def mask_bank(i, ct):
            b, tt = divmod(i, T_TILES)
            frames = slice(tt * T_TILE, (tt + 1) * T_TILE)
            if tt == 0 and ct == 0:
                scores[b] = score_pool.tile([P, C_TILES, T], F32, name="scores", tag="scores")
            nc.vector.tensor_tensor(
                out=scores[b][:, ct, frames],
                in0=banks[i, ct][:],
                in1=penalty[:, b, frames],
                op=ALU.add,
            )

        def square_half(b):
            start, end = (t - T for t in V_EXX[b])
            part, first = divmod(start, X_COLS)
            nc.vector.scalar_tensor_tensor(
                out=prod[b][:, 1, start:end],
                in0=prod[b][:, 1, start:end],
                scalar=1.0,
                in1=x_banks[b, 1, part][:, first : first + end - start],
                op0=ALU.mult,
                op1=ALU.mult,
                accum_out=last_sums[:, b : b + 1],
            )

        def mask_scores(n):
            if 0 <= n - 1 < TILES:
                for ct in range(C_TILES):
                    mask_bank(n - 1, ct)

        def exp(b, ct, part, total):
            row = scores[b][:, ct, part]
            nc.scalar.activation(
                out=row, in_=row, func=ACT.Exp, bias=neg_max[:, b, ct : ct + 1], accum_out=total
            )

        def maximum_and_exp(b, ct):
            row = scores[b][:, ct, :]
            nc.vector.tensor_reduce(
                out=neg_max[:, b, ct : ct + 1], in_=row, axis=AXIS.X, op=ALU.max, negate=True
            )
            if b == B - 1:
                for part in range(X_PARTS):
                    exp(b, ct, slice(part * X_COLS, (part + 1) * X_COLS), half_e[:, part, ct : ct + 1])
            else:
                exp(b, ct, slice(0, T), sum_e[:, b, ct : ct + 1])

        def square_last(ct, part, first, slot):
            b = B - 1
            start = part * X_COLS + first
            end = (part + 1) * X_COLS
            nc.vector.scalar_tensor_tensor(
                out=prod[b][:, ct, start:end],
                in0=prod[b][:, ct, start:end],
                scalar=recip[:, b, ct : ct + 1],
                in1=x_banks[b, ct, part][:, first:],
                op0=ALU.mult,
                op1=ALU.mult,
                accum_out=last_second[:, slot, ct : ct + 1],
            )

        def pool_step(k):
            b, step = divmod(k, T_TILES)
            if step == 0 and 0 <= b < B:
                maximum_and_exp(b, 0)
            if step == 0 and 0 <= b - 1 < B - 2:
                square_half(b - 1)
                weigh_half(b - 1, 1, 1)
            if step == 1 and 0 <= b < B:
                maximum_and_exp(b, 1)
            if step == 2 and 0 <= b < B - 1:
                weigh_half(b, 0, 1)
                weigh_half(b, 0, 0)
            if step == 3 and 0 <= b < B - 1:
                weigh_half(b, 1, 0)
                if b == B - 2:
                    weigh_half(b, 1, 1)
            if step == 2 and b == B - 1:
                weigh_half(b, 0, 0)
                weigh_half(b, 0, 1)
                nc.gpsimd.tensor_tensor(
                    out=prod[b][:, 0, 0:G_LAST],
                    in0=prod[b][:, 0, 0:G_LAST],
                    in1=x_rows[:, b, 0, 0:G_LAST],
                    op=ALU.mult,
                )
                weigh_half(b, 1, 0)
                nc.vector.tensor_tensor(out=sum_e[:, b], in0=half_e[:, 0], in1=half_e[:, 1], op=ALU.add)
                weigh_half(b, 1, 1)
                nc.vector.reciprocal(out=recip[:], in_=sum_e[:])
            if step == 3 and b == B - 1:
                nc.scalar.activation(out=warm[:], in_=half_e[:, 1, C_TILES - 1 :], func=ACT.Sqrt)
                nc.vector.tensor_tensor(
                    out=sums[:, 1, 0 : B - 2, C_TILES - 1],
                    in0=sums[:, 1, 0 : B - 2, C_TILES - 1],
                    in1=last_sums[:],
                    op=ALU.add,
                )
                square_last(0, G_LAST // X_COLS, G_LAST % X_COLS, 0)
                nc.vector.tensor_tensor(out=sums[:, 0], in0=half_sums[:, 0], in1=half_sums[:, 1], op=ALU.add)
                square_last(1, 0, 0, 0)
                nc.vector.tensor_tensor(
                    out=entries[:, 0:C_TILES, :, 0], in0=by_tile(sums[:, 0]), in1=by_tile(recip[:]), op=ALU.mult
                )
                nc.vector.tensor_tensor(
                    out=second[:], in0=by_tile(sums[:, 1, 0:b]), in1=by_tile(recip[:, 0:b]), op=ALU.mult
                )
                nc.vector.scalar_tensor_tensor(
                    out=neg_sq[:],
                    in0=entries[:, 0:C_TILES, :, 0],
                    scalar=-1.0,
                    in1=entries[:, 0:C_TILES, :, 0],
                    op0=ALU.mult,
                    op1=ALU.mult,
                )
                square_last(1, 1, 0, 1)

        def by_tile(stat):
            return stat.rearrange("p b ct -> p ct b")

        entries = const.tile([P, 2 * C_TILES, B, 2], F32)
        neg_sq = const.tile([P, C_TILES, B], F32)
        floor = const.tile([P, C_TILES, B], F32)
        second = const.tile([P, C_TILES, B - 1], F32)
        top = const.tile([P, C_TILES, B], F32)
        recip = const.tile([P, B, C_TILES], F32)

        assert 2 * C_TILES == T_TILES
        for n in range(-REGROUP_LEAD - LOAD_LEAD, TILES + T_TILES):
            load_tile(n + REGROUP_LEAD + LOAD_LEAD)
            if n + REGROUP_LEAD + LOAD_LEAD == TILES:
                load_gains()
            if n == TILES + 1:
                turn_gains()
            if n + 1 == 0:
                regroup_on_vector(0, (0,))
                turn_mask()
                regroup_on_vector(0, (1,))
                spread_penalty(0, 0)
                turn_w2()
                spread_penalty(0, 1)
            for b, part in SPREAD.get(n, ()):
                spread_penalty(b, part)
            regroup_on_scalar(n + REGROUP_LEAD)
            if n + 1 >= HELPED_TILES:
                regroup_on_vector(n + 1)
            if n in PEN_AT and n not in LATE:
                make_penalty(n)
            if n in ZERO_AT and n not in LATE:
                nc.vector.memset(zero[n][:], 0.0)
            quantise_and_multiply(n)
            if n in LATE:
                if n in PEN_AT:
                    make_penalty(n)
                nc.vector.memset(zero[n][:], 0.0)
            copy_x(X_COPIES.get(n, ()))
            for i in GP:
                if GP[i] == n:
                    regroup_on_gpsimd(i)
            second_moment_elsewhere(n)
            if n > 0 and n + 1 < HELPED_TILES:
                regroup_on_vector(n + 1)
            mask_scores(n)
            total_of_fold(n)
            pool_step(n - T_TILES)
            copy_x(X_COPIES_LATE.get(n, ()))
            if n == TILES - 1:
                for ct in range(C_TILES):
                    for part in range(X_PARTS):
                        turn_x(ct, part)
            if n in (TILES, TILES + 1):
                for part in range(X_PARTS):
                    turn_x_back(n - TILES, part)
            fold(n)
            if n == TILES + T_TILES - 1:
                fold_last()

        first = slice(0, B - 1)
        nc.vector.tensor_scalar(
            out=floor[:], in0=neg_sq[:], scalar1=-1.0, scalar2=EPS_STD, op0=ALU.mult, op1=ALU.add
        )
        nc.vector.tensor_scalar(
            out=entries[:, 0:C_TILES, :, 1], in0=neg_sq[:], scalar1=-1.0, scalar2=EPS_LN, op0=ALU.mult, op1=ALU.add
        )
        acc = x_pool.tile([P, B, 2], F32, name="acc", tag="x_bank")

        def add_to_sums(part):
            nc.tensor.matmul(
                out=acc[:].rearrange("p b k -> p (b k)"),
                lhsT=averager[:],
                rhs=entries[:, part].rearrange("p b k -> p (b k)"),
                start=(part == 0),
                stop=(part == 2 * C_TILES - 1),
            )

        for ct in range(C_TILES):
            add_to_sums(ct)
        for ct in range(C_TILES):
            nc.vector.scalar_tensor_tensor(
                out=top[:, ct, B - 1 :],
                in0=last_second[:, 1, ct : ct + 1],
                scalar=last_second[:, 0, ct : ct + 1],
                in1=floor[:, ct, B - 1 :],
                op0=ALU.add,
                op1=ALU.max,
            )
        nc.vector.tensor_tensor(out=top[:, :, first], in0=second[:], in1=floor[:, :, first], op=ALU.max)
        for ct in range(C_TILES):
            nc.scalar.activation(
                out=entries[:, C_TILES + ct, B - 1, 0:1],
                in_=top[:, ct, B - 1 :],
                func=ACT.Sqrt,
                bias=neg_sq[:, ct, B - 1 :],
            )
        for ct in range(C_TILES):
            nc.vector.tensor_scalar(
                out=entries[:, C_TILES + ct, B - 1, 1:2],
                in0=top[:, ct, B - 1 :],
                scalar1=neg_sq[:, ct, B - 1 :],
                scalar2=EPS_LN,
                op0=ALU.add,
                op1=ALU.add,
            )
        nc.vector.tensor_tensor(
            out=second[:], in0=top[:, :, first], in1=neg_sq[:, :, first], op=ALU.add
        )
        nc.scalar.activation(out=entries[:, C_TILES:, first, 0], in_=second[:], func=ACT.Sqrt)
        nc.vector.tensor_scalar_add(out=entries[:, C_TILES:, first, 1], in0=second[:], scalar1=EPS_LN)
        for ct in range(C_TILES):
            add_to_sums(C_TILES + ct)
        neg_var = const.tile([P, B], F32)
        for b in range(B):
            nc.vector.tensor_scalar(
                out=neg_var[:, b : b + 1],
                in0=acc[:, b, 0:1],
                scalar1=acc[:, b, 0:1],
                scalar2=acc[:, b, 1:2],
                op0=ALU.mult,
                op1=ALU.subtract,
            )
        root = const.tile([P, B], F32)
        nc.scalar.activation(out=root[:], in_=neg_var[:], func=ACT.Sqrt, scale=-1.0)
        gained = const.tile([P, B, 2 * C_TILES], F32)
        for b in range(B):
            nc.vector.scalar_tensor_tensor(
                out=gained[:, b],
                in0=entries[:, :, b, 0],
                scalar=acc[:, b, 0:1],
                in1=gb[:, 0 : 2 * C_TILES],
                op0=ALU.subtract,
                op1=ALU.mult,
            )
        rstd = const.tile([P, B], F32)
        nc.vector.reciprocal(out=rstd[:], in_=root[:])
        for b in range(B):
            nc.vector.scalar_tensor_tensor(
                out=y_pad[:, 2 * C_TILES * b : 2 * C_TILES * (b + 1)],
                in0=gained[:, b],
                scalar=rstd[:, b : b + 1],
                in1=gb[:, 2 * C_TILES :],
                op0=ALU.mult,
                op1=ALU.add,
            )
        y_t = misc_pool.tile([P, P], F32, tag="misc")
        nc.tensor.transpose(y_t[:], y_pad[:], ident_f32[:])
        rows = 2 * B * C_TILES
        y_rows = const.tile([rows, P], F32)
        nc.scalar.copy(out=y_rows[:], in_=y_t[0:rows, :])
        nc.sync.dma_start(out=out.rearrange("b (e c) o -> (b e) (c o)", c=P), in_=y_rows[:])
